import numpy as np
import ml_dtypes


def mxq(x, axis, fmt="e4m3"):
    dtype, down = {"e4m3": (ml_dtypes.float8_e4m3fn, 7), "e5m2": (ml_dtypes.float8_e5m2, 14)}[fmt]
    v = np.moveaxis(np.asarray(x, np.float32).astype(ml_dtypes.bfloat16).astype(np.float64), axis, -1)
    blocks = v.reshape(v.shape[:-1] + (-1, 32))
    amax = np.abs(blocks).max(-1, keepdims=True)
    byte = np.maximum(np.where(amax > 0, np.frexp(amax)[1] - 1 + 127, 0) - down, 1)
    scale = np.exp2(byte - 127.0)
    codes = (blocks / scale).astype(np.float32).astype(dtype).astype(np.float64)
    return np.moveaxis((codes * scale).reshape(v.shape), -1, axis)


WIDE = False


def mx_kscale(k):
    if not WIDE:
        return np.ones(k)
    levels = np.array([10, -10, 5, -5, 0])
    if k % 512:
        return np.exp2(np.random.permutation(np.resize(levels, k // 32))).repeat(32)
    a = np.empty((k // 512, 16))
    for p in range(k // 512):
        a[p, :8] = np.random.permutation(np.resize(levels, 8))
        for g in range(8):
            far = levels[np.abs(levels - a[p, g]) >= 10]
            a[p, g + 8] = far[np.random.randint(len(far))]
    return np.exp2(a.ravel()).repeat(32)


BF16 = ml_dtypes.bfloat16


def bf(x):
    return np.asarray(x, np.float32).astype(BF16)


def f64(x):
    return np.asarray(x).astype(np.float64)


B, I, H = 4096, 256, 512


def sigmoid(v):
    return 1.0 / (1.0 + np.exp(-v))


def setup_inputs():
    s = mx_kscale(H)
    return {"x_t": bf(np.random.standard_normal((B, I))),
            "h": bf(np.random.standard_normal((B, H)) * s),
            "c": bf(np.random.standard_normal((B, H))),
            "W_ih": bf(np.random.standard_normal((4 * H, I)) * 0.7 / np.sqrt(I)),
            "W_hh": bf(np.random.standard_normal((4 * H, H)) * 0.7 / np.sqrt(H) / s),
            "b_ih": bf(np.random.standard_normal(4 * H) * 0.3),
            "b_hh": bf(np.random.standard_normal(4 * H) * 0.3)}


def reference(x_t, h, c, W_ih, W_hh, b_ih, b_hh):
    gates = f64(x_t) @ f64(W_ih).T + f64(b_ih) + (mxq(f64(h), 1, "e4m3") @ mxq(f64(W_hh), 1, "e4m3").T) + f64(b_hh)
    i, f, g, o = np.split(gates, 4, axis=1)
    c_next = sigmoid(f) * f64(c) + sigmoid(i) * np.tanh(g)
    h_next = sigmoid(o) * np.tanh(c_next)
    return h_next, c_next

@@ -1,0 +1,354 @@
+from contextlib import ExitStack
+
+import concourse.mybir as mybir
+from concourse.masks import make_identity
+
+F32 = mybir.dt.float32
+BF16 = mybir.dt.bfloat16
+U32 = mybir.dt.uint32
+U8 = mybir.dt.uint8
+FP8X4 = mybir.dt.float8_e4m3fn_x4
+ACT = mybir.ActivationFunctionType
+ALU = mybir.AluOpType
+
+P = 128
+BATCH, IN_DIM, HID = 4096, 256, 512
+GATES = 4
+GATE_I, GATE_F, GATE_G, GATE_O = 0, 1, 2, 3
+TILES = 4
+GROUP_ROWS = TILES * P
+N_GROUPS = BATCH // GROUP_ROWS
+N_TILES = N_GROUPS * TILES
+N_STEPS = N_TILES * GATES
+BLOCKS_PER_GATE = HID // P
+BLOCKS = GATES * BLOCKS_PER_GATE
+REC_GATES = (GATE_F, GATE_G, GATE_O)
+REC_BLOCKS = len(REC_GATES) * BLOCKS_PER_GATE
+REC_BLOCKS_PER_TILE = REC_BLOCKS // TILES
+PAIR = 2
+H_WORDS = HID // PAIR
+X_WORDS = IN_DIM // PAIR
+H_HALVES = H_WORDS // P
+PACK = 4
+ROWS_AHEAD = 2 * TILES
+
+FLOPS = 2 * BATCH * GATES * HID * (IN_DIM + HID)
+
+
+def tile_nodelstmcell_pa_t_kernel(tc, x_t, h, c, W_ih, W_hh, b_ih, b_hh, out_0, out_1):
+    nc = tc.nc
+
+    x_rows = x_t.rearrange("(s p j) k -> s p (j k)", p=P, j=TILES)
+    h_rows = h.rearrange("(s p j) k -> s p (j k)", p=P, j=TILES)
+    c_rows = c.rearrange("(s p j) n -> s p (j n)", p=P, j=TILES)
+    h_next_rows = out_0.rearrange("(s p j) n -> s j p n", p=P, j=TILES)
+    c_next_rows = out_1.rearrange("(s p j) n -> s j p n", p=P, j=TILES)
+
+    with ExitStack() as stack:
+        const = stack.enter_context(tc.tile_pool(name="const", bufs=1))
+        setup = stack.enter_context(tc.tile_pool(name="setup", bufs=4))
+        rows = stack.enter_context(tc.tile_pool(name="rows", bufs=3))
+        operands = stack.enter_context(tc.tile_pool(name="operands", bufs=3))
+        work = stack.enter_context(tc.tile_pool(name="work", bufs=3))
+        psum = stack.enter_context(tc.psum_pool(name="psum", bufs=4))
+        stack.enter_context(tc.manual_schedule())
+
+        x_in, h_in, c_in = {}, {}, {}
+        x_T, h_codes, h_scales = {}, {}, {}
+        h_grouped = {}
+        rec_T = {}
+        gate_ps = {}
+        rec_ps = {}
+        acts = {}
+        c_new, tanh_c = {}, {}
+
+        def place(step):
+            tile_index, gate = divmod(step, GATES)
+            s, j = divmod(tile_index, TILES)
+            return tile_index, gate, s, j
+
+        def load_rows(s):
+            h_in[s] = rows.tile([P, TILES * HID], BF16, name="h_in", tag="h_in")
+            nc.sync.dma_start(out=h_in[s][:], in_=h_rows[s])
+            x_in[s] = rows.tile([P, TILES * IN_DIM], BF16, name="x_in", tag="x_in")
+            nc.sync.dma_start(out=x_in[s][:], in_=x_rows[s])
+
+        def load_cell(s):
+            c_in[s] = rows.tile([P, TILES * HID], BF16, name="c_in", tag="c_in")
+            nc.sync.dma_start(out=c_in[s][:], in_=c_rows[s])
+
+        def transpose_rows(tile_index):
+            s, j = divmod(tile_index, TILES)
+            if j == 0:
+                h_codes[s] = operands.tile([P, GROUP_ROWS], U32, name="h_codes", tag="h_codes", align_bytes=64)
+                h_scales[s] = operands.tile([P, GROUP_ROWS], U8, name="h_scales", tag="h_scales", align_bytes=64)
+                x_T[s] = operands.tile([P, TILES, PAIR, P], BF16, name="x_T", tag="x_T")
+            words_ps = psum.tile([P, H_WORDS + X_WORDS], F32, tag="copied_out")
+            h_words = h_in[s][:].bitcast(F32)
+            for u in range(H_HALVES):
+                first = j * H_WORDS + u
+                nc.tensor.transpose(
+                    words_ps[:, u * P : (u + 1) * P],
+                    h_words[:, first : (j + 1) * H_WORDS : H_HALVES],
+                    ident_f32[:],
+                )
+            x_words = x_in[s][:].bitcast(F32)
+            nc.tensor.transpose(words_ps[:, H_WORDS:], x_words[:, j * X_WORDS : (j + 1) * X_WORDS], ident_f32[:])
+            h_grouped[tile_index] = work.tile([P, P * PACK], BF16, name="h_grouped", tag="h_grouped", align_bytes=64)
+            nc.scalar.copy(
+                out=h_grouped[tile_index][:].bitcast(F32).rearrange("p (r u) -> p r u", u=H_HALVES),
+                in_=words_ps[:, 0:H_WORDS].rearrange("p (u r) -> p r u", u=H_HALVES),
+            )
+            nc.scalar.copy(
+                out=x_T[s][:, j, :, :],
+                in_=words_ps[:, H_WORDS:].bitcast(BF16).rearrange("p (r e) -> p e r", e=PAIR),
+            )
+
+        def quantise_rows(tile_index):
+            s, j = divmod(tile_index, TILES)
+            cols = slice(j * P, (j + 1) * P)
+            nc.vector.quantize_mx(
+                out=h_codes[s][:, cols].bitcast(FP8X4), scales=h_scales[s][:, cols], in_=h_grouped[tile_index][:]
+            )
+
+        def recurrent_block(s, local, on_scalar):
+            if local == 0:
+                rec_T[s] = operands.tile([P, REC_BLOCKS, GROUP_ROWS], F32, name="rec_T", tag="rec_T", bufs=2)
+            blk = REC_GATES[0] * BLOCKS_PER_GATE + local
+            cols = slice(blk * P, (blk + 1) * P)
+            recT_ps = psum.tile([P, GROUP_ROWS], F32, tag="copied_out")
+            nc.tensor.matmul_mx(
+                out=recT_ps[:],
+                lhsT=w_codes[:, cols].bitcast(FP8X4),
+                lhsT_scale=w_scales[:, cols],
+                rhs=h_codes[s][:].bitcast(FP8X4),
+                rhs_scale=h_scales[s][:],
+                start=True,
+                stop=True,
+            )
+            if on_scalar:
+                nc.scalar.activation(
+                    out=rec_T[s][:, local, :], in_=recT_ps[:], func=ACT.Identity, bias=bias[:, blk : blk + 1]
+                )
+            else:
+                nc.vector.tensor_scalar(
+                    out=rec_T[s][:, local, :], in0=recT_ps[:], scalar1=bias[:, blk : blk + 1], scalar2=None, op0=ALU.add
+                )
+
+        def recurrent_rows(tile_index):
+            s, j = divmod(tile_index, TILES)
+            rec_ps[tile_index] = psum.tile([P, HID], F32, name="rec_ps", tag="copied_out")
+            nc.tensor.matmul_mx(
+                out=rec_ps[tile_index][:],
+                lhsT=h_codes[s][:, j * P : (j + 1) * P].bitcast(FP8X4),
+                lhsT_scale=h_scales[s][:, j * P : (j + 1) * P],
+                rhs=w_codes[:, GATE_I * HID : (GATE_I + 1) * HID].bitcast(FP8X4),
+                rhs_scale=w_scales[:, GATE_I * HID : (GATE_I + 1) * HID],
+                start=True,
+                stop=True,
+            )
+
+        def add_bias(tile_index):
+            acts[tile_index, GATE_I] = work.tile([P, HID], F32, name="act%d" % GATE_I, tag="act%d" % GATE_I)
+            nc.vector.tensor_tensor(
+                out=acts[tile_index, GATE_I][:], in0=gate_ps[tile_index * GATES + GATE_I][:], in1=bias_spread[:], op=ALU.add
+            )
+
+        def add_recurrent_rows(tile_index):
+            total = acts[tile_index, GATE_I]
+            nc.vector.tensor_tensor(out=total[:], in0=rec_ps[tile_index][:], in1=total[:], op=ALU.add)
+
+        def input_pass(step, e):
+            tile_index, gate, s, j = place(step)
+            if e == 0:
+                gate_ps[step] = psum.tile([P, HID], F32, name="gate_ps", tag="gate")
+            nc.tensor.matmul(
+                out=gate_ps[step][:],
+                lhsT=x_T[s][:, j, e, :],
+                rhs=w_ih_T[:, e, gate * HID : (gate + 1) * HID],
+                start=(e == 0),
+                stop=(e == PAIR - 1 and gate == GATE_I),
+            )
+
+        def add_recurrent(step, half):
+            tile_index, gate, s, j = place(step)
+            for a in range(PAIR * half, PAIR * half + PAIR):
+                nc.tensor.matmul(
+                    out=gate_ps[step][:, a * P : (a + 1) * P],
+                    lhsT=rec_T[s][:, REC_GATES.index(gate) * BLOCKS_PER_GATE + a, j * P : (j + 1) * P],
+                    rhs=ident_f32[:],
+                    is_transpose=True,
+                    start=False,
+                    stop=(a == BLOCKS_PER_GATE - 1),
+                )
+
+        def activate(step):
+            tile_index, gate, s, j = place(step)
+            if gate == GATE_I:
+                total = acts[tile_index, gate]
+                nc.scalar.activation(out=total[:], in_=total[:], func=ACT.Sigmoid)
+            else:
+                acts[tile_index, gate] = work.tile([P, HID], F32, name="act%d" % gate, tag="act%d" % gate)
+                nc.scalar.activation(
+                    out=acts[tile_index, gate][:],
+                    in_=gate_ps[step][:],
+                    func=(ACT.Tanh if gate == GATE_G else ACT.Sigmoid),
+                )
+
+        def keep_old_cell(tile_index):
+            s, j = divmod(tile_index, TILES)
+            keep = acts[tile_index, GATE_F]
+            nc.gpsimd.tensor_tensor(out=keep[:], in0=keep[:], in1=c_in[s][:, j * HID : (j + 1) * HID], op=ALU.mult)
+
+        def write_candidate(tile_index):
+            write = acts[tile_index, GATE_I]
+            nc.gpsimd.tensor_tensor(out=write[:], in0=write[:], in1=acts[tile_index, GATE_G][:], op=ALU.mult)
+
+        def new_cell(tile_index):
+            s, j = divmod(tile_index, TILES)
+            c_new[tile_index] = work.tile([P, HID], F32, name="c_new", tag="c_new")
+            nc.vector.tensor_tensor(
+                out=c_new[tile_index][:], in0=acts[tile_index, GATE_F][:], in1=acts[tile_index, GATE_I][:], op=ALU.add
+            )
+            nc.sync.dma_start(out=c_next_rows[s, j], in_=c_new[tile_index][:])
+
+        def tanh_of_new_cell(tile_index):
+            tanh_c[tile_index] = work.tile([P, HID], F32, name="tanh_c", tag="tanh_c")
+            nc.scalar.activation(out=tanh_c[tile_index][:], in_=c_new[tile_index][:], func=ACT.Tanh)
+
+        def new_hidden(tile_index):
+            s, j = divmod(tile_index, TILES)
+            h_new = work.tile([P, HID], F32, tag="h_new")
+            nc.vector.tensor_tensor(
+                out=h_new[:], in0=acts[tile_index, GATE_O][:], in1=tanh_c[tile_index][:], op=ALU.mult
+            )
+            nc.sync.dma_start(out=h_next_rows[s, j], in_=h_new[:])
+
+        bias_rows = const.tile([P, P], BF16)
+        nc.vector.memset(bias_rows[:], 0.0)
+        nc.sync.dma_start(out=bias_rows[0:BLOCKS, :], in_=b_ih.rearrange("(b n) -> b n", n=P))
+        nc.sync.dma_start(out=bias_rows[BLOCKS : 2 * BLOCKS, :], in_=b_hh.rearrange("(b n) -> b n", n=P))
+        load_rows(0)
+        w_hh_raw, w_ih_raw = [], []
+        for gate in range(GATES):
+            w_hh_raw.append(setup.tile([P, BLOCKS_PER_GATE, HID], BF16, name="w_hh_raw", tag="w_hh_raw"))
+            nc.sync.dma_start(
+                out=w_hh_raw[gate][:], in_=W_hh[gate * HID : (gate + 1) * HID, :].rearrange("(a p) k -> p a k", p=P)
+            )
+            w_ih_raw.append(setup.tile([P, BLOCKS_PER_GATE, IN_DIM], BF16, name="w_ih_raw", tag="w_ih_raw"))
+            nc.sync.dma_start(
+                out=w_ih_raw[gate][:], in_=W_ih[gate * HID : (gate + 1) * HID, :].rearrange("(a p) k -> p a k", p=P)
+            )
+        load_rows(1)
+        load_cell(0)
+        load_rows(2)
+
+        ident_f32 = const.tile([P, P], F32)
+        make_identity(nc, ident_f32[:])
+        ident_bf16 = const.tile([P, P], BF16)
+        make_identity(nc, ident_bf16[:])
+
+        biasT_ps = psum.tile([P, P], BF16, tag="copied_out")
+        nc.tensor.transpose(biasT_ps[:], bias_rows[:], ident_bf16[:])
+        bias_pair = const.tile([P, 2 * BLOCKS], F32)
+        nc.vector.tensor_copy(out=bias_pair[:], in_=biasT_ps[:, 0 : 2 * BLOCKS])
+        bias = const.tile([P, BLOCKS], F32)
+        nc.vector.tensor_tensor(out=bias[:], in0=bias_pair[:, 0:BLOCKS], in1=bias_pair[:, BLOCKS : 2 * BLOCKS], op=ALU.add)
+        bias_spread = const.tile([P, HID], F32)
+        spread_ps = psum.tile([P, HID], F32, tag="gate")
+        for a in range(BLOCKS_PER_GATE):
+            blk = GATE_I * BLOCKS_PER_GATE + a
+            nc.tensor.transpose(
+                spread_ps[:, a * P : (a + 1) * P], bias[:, blk : blk + 1].to_broadcast([P, P]), ident_f32[:]
+            )
+        nc.scalar.copy(out=bias_spread[:], in_=spread_ps[:])
+
+        for tile_index in range(TILES):
+            transpose_rows(tile_index)
+            quantise_rows(tile_index)
+
+        w_codes = const.tile([P, GATES * HID], U32, align_bytes=64)
+        w_scales = const.tile([P, GATES * HID], U8, align_bytes=64)
+        w_ih_T = const.tile([P, PAIR, GATES * HID], BF16)
+
+        def first_group_blocks(gate):
+            if gate in REC_GATES:
+                for a in range(BLOCKS_PER_GATE):
+                    recurrent_block(0, REC_GATES.index(gate) * BLOCKS_PER_GATE + a, on_scalar=(a % 2 == 1))
+
+        for gate in range(GATES):
+            cols = slice(gate * HID, (gate + 1) * HID)
+            w_grouped = setup.tile([P, HID * PACK], BF16, tag="w_grouped", bufs=2, align_bytes=64)
+            grouped_words = w_grouped[:].bitcast(F32).rearrange(
+                "p (a n u) -> p a n u", a=BLOCKS_PER_GATE, u=H_HALVES
+            )
+            for half in range(2):
+                wT_ps = psum.tile([P, 2, H_HALVES, P], F32, tag="gate")
+                for a in range(2):
+                    raw_words = w_hh_raw[gate][:, 2 * half + a, :].bitcast(F32)
+                    for u in range(H_HALVES):
+                        nc.tensor.transpose(wT_ps[:, a, u, :], raw_words[:, u:H_WORDS:H_HALVES], ident_f32[:])
+                copy_out = nc.vector.tensor_copy if half == 0 else nc.scalar.copy
+                copy_out(
+                    out=grouped_words[:, 2 * half : 2 * half + 2, :, :], in_=wT_ps[:].rearrange("p a u n -> p a n u")
+                )
+            nc.vector.quantize_mx(out=w_codes[:, cols].bitcast(FP8X4), scales=w_scales[:, cols], in_=w_grouped[:])
+            wT_ps = psum.tile([P, HID], F32, tag="gate")
+            for a in range(BLOCKS_PER_GATE):
+                nc.tensor.transpose(wT_ps[:, a * P : (a + 1) * P], w_ih_raw[gate][:, a, :].bitcast(F32), ident_f32[:])
+            nc.scalar.copy(out=w_ih_T[:, :, cols], in_=wT_ps[:].bitcast(BF16).rearrange("p (n e) -> p e n", e=PAIR))
+            if gate > 0:
+                first_group_blocks(gate - 1)
+        for tile_index in range(TILES, ROWS_AHEAD):
+            transpose_rows(tile_index)
+            quantise_rows(tile_index)
+        first_group_blocks(GATES - 1)
+
+        for turn in range(N_TILES + 2):
+            s, j = divmod(turn, TILES)
+            running = turn < N_TILES
+            if running and j == 0:
+                if s + 3 < N_GROUPS:
+                    load_rows(s + 3)
+                if s + 1 < N_GROUPS:
+                    load_cell(s + 1)
+
+            for gate in range(GATES):
+                step = turn * GATES + gate
+                before = step - 1
+                finish = 0 <= before < N_STEPS
+                finish_by_transposes = finish and before % GATES in REC_GATES
+
+                if running:
+                    input_pass(step, 0)
+                if finish_by_transposes:
+                    add_recurrent(before, 0)
+                if gate == GATE_F:
+                    if running:
+                        recurrent_rows(turn)
+                        add_recurrent_rows(turn)
+                    if running and s + 1 < N_GROUPS:
+                        for b in range(REC_BLOCKS_PER_TILE):
+                            recurrent_block(s + 1, j * REC_BLOCKS_PER_TILE + b, on_scalar=(b == 0))
+                    if 0 <= turn - 1 < N_TILES:
+                        keep_old_cell(turn - 1)
+                        write_candidate(turn - 1)
+                    if 0 <= turn - 2 < N_TILES:
+                        tanh_of_new_cell(turn - 2)
+                if running:
+                    input_pass(step, 1)
+                if finish_by_transposes:
+                    add_recurrent(before, 1)
+                if gate == GATE_F and turn + ROWS_AHEAD < N_TILES:
+                    transpose_rows(turn + ROWS_AHEAD)
+                if finish:
+                    activate(before)
+                if gate == GATE_I and running:
+                    add_bias(turn)
+
+            if 0 <= turn - 1 < N_TILES:
+                new_cell(turn - 1)
+            if 0 <= turn - 2 < N_TILES:
+                new_hidden(turn - 2)
+            if turn + ROWS_AHEAD < N_TILES:
+                quantise_rows(turn + ROWS_AHEAD)

@@ -15,23 +15,55 @@ P = 128
 BATCH, IN_DIM, HID = 4096, 256, 512
 GATES = 4
 GATE_I, GATE_F, GATE_G, GATE_O = 0, 1, 2, 3
+GATE_ORDER = (GATE_F, GATE_I, GATE_G, GATE_O)
+HEAD_ORDER = (GATE_F, GATE_I, GATE_G, GATE_O)
 TILES = 4
 GROUP_ROWS = TILES * P
 N_GROUPS = BATCH // GROUP_ROWS
 N_TILES = N_GROUPS * TILES
-N_STEPS = N_TILES * GATES
 BLOCKS_PER_GATE = HID // P
 BLOCKS = GATES * BLOCKS_PER_GATE
-REC_GATES = (GATE_F, GATE_G, GATE_O)
-REC_BLOCKS = len(REC_GATES) * BLOCKS_PER_GATE
-REC_BLOCKS_PER_TILE = REC_BLOCKS // TILES
+TURNED_GATES = (GATE_G,)
 PAIR = 2
 H_WORDS = HID // PAIR
 X_WORDS = IN_DIM // PAIR
 H_HALVES = H_WORDS // P
 PACK = 4
-ROWS_AHEAD = 2 * TILES
+ROWS_AHEAD = 2
+N_HEAD = 4
+TCOPY = "S"
+KW = {}
 
+C_ENG, H_ENG = "V", "G"
+MV, ACT_LAG = 1.55, 2.5
+ROW_GATE, ROW_POS, ROW_COPY, ROW_QUANT = GATE_G, 0.15, 1.45, 3.53
+T_HEAD, T_LAG, T_COPY = 1, 2, 0.8
+W_LEAD, W_STEP, W_V = 4, 1, True
+K_LAG, B_LAG, C_LAG, TANH_LAG, H_LAG = 2.9, 2.9, 4.52, 5.55, 6.9
+C_ENG = "V"
+H_ENG = "G"
+MV = 1.55
+ACT_LAG = 2.55
+ROW_GATE = GATE_I
+ROW_POS = 0.45
+ROW_COPY = 1.45
+ROW_QUANT = 4.52
+T_HEAD = 1
+T_LAG = 2
+T_COPY = 1.45
+W_LEAD = 3
+W_STEP = 0
+W_V = True
+K_LAG = 2.9
+B_LAG = 2.9
+C_LAG = 4.6
+TANH_LAG = 5.58
+H_LAG = 6.9
+N_HEAD = 2
+TCOPY = "S"
+ROWS_AHEAD = 2
+GATE_ORDER = (GATE_F, GATE_G, GATE_I, GATE_O)
+HEAD_ORDER = (GATE_F, GATE_I, GATE_G, GATE_O)
 FLOPS = 2 * BATCH * GATES * HID * (IN_DIM + HID)
 
 
@@ -44,32 +76,37 @@ def tile_nodelstmcell_pa_t_kernel(tc, x_t, h, c, W_ih, W_hh, b_ih, b_hh, out_0, 
     h_next_rows = out_0.rearrange("(s p j) n -> s j p n", p=P, j=TILES)
     c_next_rows = out_1.rearrange("(s p j) n -> s j p n", p=P, j=TILES)
 
+    steps = [(t, gate) for gate in HEAD_ORDER for t in range(N_HEAD)]
+    steps += [(t, gate) for t in range(N_HEAD, N_TILES) for gate in GATE_ORDER]
+    at = {step: n for n, step in enumerate(steps)}
+    n_steps = len(steps)
+
     with ExitStack() as stack:
         const = stack.enter_context(tc.tile_pool(name="const", bufs=1))
         setup = stack.enter_context(tc.tile_pool(name="setup", bufs=4))
         rows = stack.enter_context(tc.tile_pool(name="rows", bufs=3))
         operands = stack.enter_context(tc.tile_pool(name="operands", bufs=3))
-        work = stack.enter_context(tc.tile_pool(name="work", bufs=3))
+        work = stack.enter_context(tc.tile_pool(name="work", bufs=4))
         psum = stack.enter_context(tc.psum_pool(name="psum", bufs=4))
         stack.enter_context(tc.manual_schedule())
 
         x_in, h_in, c_in = {}, {}, {}
-        x_T, h_codes, h_scales = {}, {}, {}
+        h_codes, h_scales = {}, {}
+        x_T = {}
+        words_ps = {}
         h_grouped = {}
         rec_T = {}
+        recT_ps = {}
         gate_ps = {}
         rec_ps = {}
         acts = {}
         c_new, tanh_c = {}, {}
 
-        def place(step):
-            tile_index, gate = divmod(step, GATES)
-            s, j = divmod(tile_index, TILES)
-            return tile_index, gate, s, j
-
-        def load_rows(s):
+        def load_h(s):
             h_in[s] = rows.tile([P, TILES * HID], BF16, name="h_in", tag="h_in")
             nc.sync.dma_start(out=h_in[s][:], in_=h_rows[s])
+
+        def load_x(s):
             x_in[s] = rows.tile([P, TILES * IN_DIM], BF16, name="x_in", tag="x_in")
             nc.sync.dma_start(out=x_in[s][:], in_=x_rows[s])
 
@@ -77,171 +114,313 @@ def tile_nodelstmcell_pa_t_kernel(tc, x_t, h, c, W_ih, W_hh, b_ih, b_hh, out_0, 
             c_in[s] = rows.tile([P, TILES * HID], BF16, name="c_in", tag="c_in")
             nc.sync.dma_start(out=c_in[s][:], in_=c_rows[s])
 
-        def transpose_rows(tile_index):
-            s, j = divmod(tile_index, TILES)
-            if j == 0:
-                h_codes[s] = operands.tile([P, GROUP_ROWS], U32, name="h_codes", tag="h_codes", align_bytes=64)
-                h_scales[s] = operands.tile([P, GROUP_ROWS], U8, name="h_scales", tag="h_scales", align_bytes=64)
-                x_T[s] = operands.tile([P, TILES, PAIR, P], BF16, name="x_T", tag="x_T")
-            words_ps = psum.tile([P, H_WORDS + X_WORDS], F32, tag="copied_out")
+        w_hh_raw, w_ih_raw = {}, {}
+
+        def load_w_hh(gate):
+            w_hh_raw[gate] = setup.tile([P, BLOCKS_PER_GATE, HID], BF16, name="w_hh_raw", tag="w_hh_raw")
+            nc.sync.dma_start(
+                out=w_hh_raw[gate][:], in_=W_hh[gate * HID : (gate + 1) * HID, :].rearrange("(a p) k -> p a k", p=P)
+            )
+
+        def load_w_ih(gate):
+            w_ih_raw[gate] = setup.tile([P, BLOCKS_PER_GATE, IN_DIM], BF16, name="w_ih_raw", tag="w_ih_raw")
+            nc.sync.dma_start(
+                out=w_ih_raw[gate][:], in_=W_ih[gate * HID : (gate + 1) * HID, :].rearrange("(a p) k -> p a k", p=P)
+            )
+
+        w_grouped, weights_ps = {}, {}
+
+        def weights_hh_half(gate, half):
+            if half == 0:
+                w_grouped[gate] = setup.tile(
+                    [P, HID * PACK], BF16, name="w_grouped", tag="w_grouped", bufs=2, align_bytes=64
+                )
+            wT_ps = psum.tile([P, 2, H_HALVES, P], F32, name="wT_ps", tag="copied_out")
+            for a in range(2):
+                raw_words = w_hh_raw[gate][:, 2 * half + a, :].bitcast(F32)
+                for u in range(H_HALVES):
+                    nc.tensor.transpose(wT_ps[:, a, u, :], raw_words[:, u:H_WORDS:H_HALVES], ident_f32[:])
+            weights_ps[gate, half] = wT_ps
+
+        def copy_weights_hh_half(gate, half, copy_out):
+            grouped_words = w_grouped[gate][:].bitcast(F32).rearrange(
+                "p (a n u) -> p a n u", a=BLOCKS_PER_GATE, u=H_HALVES
+            )
+            copy_out(
+                out=grouped_words[:, 2 * half : 2 * half + 2, :, :],
+                in_=weights_ps[gate, half][:].rearrange("p a u n -> p a n u"),
+            )
+
+        def weights_quantise(gate):
+            cols = slice(gate * HID, (gate + 1) * HID)
+            nc.vector.quantize_mx(out=w_codes[:, cols].bitcast(FP8X4), scales=w_scales[:, cols], in_=w_grouped[gate][:])
+
+        def weights_ih(gate):
+            wT_ps = psum.tile([P, HID], F32, name="wihT_ps", tag="copied_out")
+            for a in range(BLOCKS_PER_GATE):
+                nc.tensor.transpose(wT_ps[:, a * P : (a + 1) * P], w_ih_raw[gate][:, a, :].bitcast(F32), ident_f32[:])
+            weights_ps[gate, 2] = wT_ps
+
+        def copy_weights_ih(gate):
+            cols = slice(gate * HID, (gate + 1) * HID)
+            nc.scalar.copy(
+                out=w_ih_T[:, :, cols],
+                in_=weights_ps[gate, 2][:].bitcast(BF16).rearrange("p (n e) -> p e n", e=PAIR),
+            )
+
+        def transpose_rows(t):
+            s, j = divmod(t, TILES)
+            words_ps[t] = psum.tile([P, H_WORDS + X_WORDS], F32, name="words_ps", tag="copied_out")
             h_words = h_in[s][:].bitcast(F32)
             for u in range(H_HALVES):
-                first = j * H_WORDS + u
                 nc.tensor.transpose(
-                    words_ps[:, u * P : (u + 1) * P],
-                    h_words[:, first : (j + 1) * H_WORDS : H_HALVES],
+                    words_ps[t][:, u * P : (u + 1) * P],
+                    h_words[:, j * H_WORDS + u : (j + 1) * H_WORDS : H_HALVES],
                     ident_f32[:],
                 )
             x_words = x_in[s][:].bitcast(F32)
-            nc.tensor.transpose(words_ps[:, H_WORDS:], x_words[:, j * X_WORDS : (j + 1) * X_WORDS], ident_f32[:])
-            h_grouped[tile_index] = work.tile([P, P * PACK], BF16, name="h_grouped", tag="h_grouped", align_bytes=64)
-            nc.scalar.copy(
-                out=h_grouped[tile_index][:].bitcast(F32).rearrange("p (r u) -> p r u", u=H_HALVES),
-                in_=words_ps[:, 0:H_WORDS].rearrange("p (u r) -> p r u", u=H_HALVES),
-            )
-            nc.scalar.copy(
-                out=x_T[s][:, j, :, :],
-                in_=words_ps[:, H_WORDS:].bitcast(BF16).rearrange("p (r e) -> p e r", e=PAIR),
-            )
+            nc.tensor.transpose(words_ps[t][:, H_WORDS:], x_words[:, j * X_WORDS : (j + 1) * X_WORDS], ident_f32[:])
 
-        def quantise_rows(tile_index):
-            s, j = divmod(tile_index, TILES)
+        def copy_rows(t):
+            h_grouped[t] = work.tile([P, P * PACK], BF16, name="h_grouped", tag="h_grouped", align_bytes=64)
+            nc.scalar.copy(
+                out=h_grouped[t][:].bitcast(F32).rearrange("p (r u) -> p r u", u=H_HALVES),
+                in_=words_ps[t][:, 0:H_WORDS].rearrange("p (u r) -> p r u", u=H_HALVES),
+            )
+            x_T[t] = operands.tile([P, X_WORDS], F32, name="x_T", tag="x_T", bufs=ROWS_AHEAD + 4)
+            nc.scalar.copy(out=x_T[t][:], in_=words_ps[t][:, H_WORDS:])
+
+        def quantise_rows(t):
+            s, j = divmod(t, TILES)
+            if j == 0:
+                h_codes[s] = operands.tile([P, GROUP_ROWS], U32, name="h_codes", tag="h_codes", align_bytes=64)
+                h_scales[s] = operands.tile([P, GROUP_ROWS], U8, name="h_scales", tag="h_scales", align_bytes=64)
             cols = slice(j * P, (j + 1) * P)
             nc.vector.quantize_mx(
-                out=h_codes[s][:, cols].bitcast(FP8X4), scales=h_scales[s][:, cols], in_=h_grouped[tile_index][:]
+                out=h_codes[s][:, cols].bitcast(FP8X4), scales=h_scales[s][:, cols], in_=h_grouped[t][:]
             )
 
-        def recurrent_block(s, local, on_scalar):
-            if local == 0:
-                rec_T[s] = operands.tile([P, REC_BLOCKS, GROUP_ROWS], F32, name="rec_T", tag="rec_T", bufs=2)
-            blk = REC_GATES[0] * BLOCKS_PER_GATE + local
-            cols = slice(blk * P, (blk + 1) * P)
-            recT_ps = psum.tile([P, GROUP_ROWS], F32, tag="copied_out")
-            nc.tensor.matmul_mx(
-                out=recT_ps[:],
-                lhsT=w_codes[:, cols].bitcast(FP8X4),
-                lhsT_scale=w_scales[:, cols],
-                rhs=h_codes[s][:].bitcast(FP8X4),
-                rhs_scale=h_scales[s][:],
-                start=True,
-                stop=True,
-            )
-            if on_scalar:
-                nc.scalar.activation(
-                    out=rec_T[s][:, local, :], in_=recT_ps[:], func=ACT.Identity, bias=bias[:, blk : blk + 1]
+        def turned_blocks(t, gate):
+            s, j = divmod(t, TILES)
+            recT_ps[t, gate] = psum.tile([P, BLOCKS_PER_GATE, P], F32, name="recT_ps", tag="copied_out")
+            for a in range(BLOCKS_PER_GATE):
+                blk = gate * BLOCKS_PER_GATE + a
+                cols = slice(blk * P, (blk + 1) * P)
+                nc.tensor.matmul_mx(
+                    out=recT_ps[t, gate][:, a, :],
+                    lhsT=w_codes[:, cols].bitcast(FP8X4),
+                    lhsT_scale=w_scales[:, cols],
+                    rhs=h_codes[s][:, j * P : (j + 1) * P].bitcast(FP8X4),
+                    rhs_scale=h_scales[s][:, j * P : (j + 1) * P],
+                    start=True,
+                    stop=True,
                 )
+
+        def copy_turned_blocks(t, gate):
+            rec_T[t, gate] = operands.tile([P, BLOCKS_PER_GATE, P], F32, name="rec_T", tag="rec_T%d" % gate, bufs=6)
+            blk0 = gate * BLOCKS_PER_GATE
+            if TCOPY == "S" or (TCOPY == "A" and t % 2):
+                for a in range(BLOCKS_PER_GATE):
+                    nc.scalar.activation(
+                        out=rec_T[t, gate][:, a, :],
+                        in_=recT_ps[t, gate][:, a, :],
+                        func=ACT.Identity,
+                        bias=bias[:, blk0 + a : blk0 + a + 1],
+                    )
             else:
-                nc.vector.tensor_scalar(
-                    out=rec_T[s][:, local, :], in0=recT_ps[:], scalar1=bias[:, blk : blk + 1], scalar2=None, op0=ALU.add
+                nc.vector.tensor_tensor(
+                    out=rec_T[t, gate][:],
+                    in0=recT_ps[t, gate][:],
+                    in1=bias[:, blk0 : blk0 + BLOCKS_PER_GATE].unsqueeze(2).to_broadcast([P, BLOCKS_PER_GATE, P]),
+                    op=ALU.add,
                 )
 
-        def recurrent_rows(tile_index):
-            s, j = divmod(tile_index, TILES)
-            rec_ps[tile_index] = psum.tile([P, HID], F32, name="rec_ps", tag="copied_out")
-            nc.tensor.matmul_mx(
-                out=rec_ps[tile_index][:],
-                lhsT=h_codes[s][:, j * P : (j + 1) * P].bitcast(FP8X4),
-                lhsT_scale=h_scales[s][:, j * P : (j + 1) * P],
-                rhs=w_codes[:, GATE_I * HID : (GATE_I + 1) * HID].bitcast(FP8X4),
-                rhs_scale=w_scales[:, GATE_I * HID : (GATE_I + 1) * HID],
-                start=True,
-                stop=True,
-            )
-
-        def add_bias(tile_index):
-            acts[tile_index, GATE_I] = work.tile([P, HID], F32, name="act%d" % GATE_I, tag="act%d" % GATE_I)
-            nc.vector.tensor_tensor(
-                out=acts[tile_index, GATE_I][:], in0=gate_ps[tile_index * GATES + GATE_I][:], in1=bias_spread[:], op=ALU.add
-            )
-
-        def add_recurrent_rows(tile_index):
-            total = acts[tile_index, GATE_I]
-            nc.vector.tensor_tensor(out=total[:], in0=rec_ps[tile_index][:], in1=total[:], op=ALU.add)
-
-        def input_pass(step, e):
-            tile_index, gate, s, j = place(step)
+        def input_pass(n, e):
+            t, gate = steps[n]
             if e == 0:
-                gate_ps[step] = psum.tile([P, HID], F32, name="gate_ps", tag="gate")
+                gate_ps[n] = psum.tile([P, HID], F32, name="gate_ps", tag="gate")
             nc.tensor.matmul(
-                out=gate_ps[step][:],
-                lhsT=x_T[s][:, j, e, :],
+                out=gate_ps[n][:],
+                lhsT=x_T[t][:].bitcast(BF16)[:, e:IN_DIM:PAIR],
                 rhs=w_ih_T[:, e, gate * HID : (gate + 1) * HID],
                 start=(e == 0),
-                stop=(e == PAIR - 1 and gate == GATE_I),
+                stop=(e == PAIR - 1 and gate not in TURNED_GATES),
             )
 
-        def add_recurrent(step, half):
-            tile_index, gate, s, j = place(step)
-            for a in range(PAIR * half, PAIR * half + PAIR):
+        def recurrent_rows(n):
+            t, gate = steps[n]
+            s, j = divmod(t, TILES)
+            rec_ps[n] = psum.tile([P, HID], F32, name="rec_ps", tag="copied_out")
+            nc.tensor.matmul_mx(
+                out=rec_ps[n][:],
+                lhsT=h_codes[s][:, j * P : (j + 1) * P].bitcast(FP8X4),
+                lhsT_scale=h_scales[s][:, j * P : (j + 1) * P],
+                rhs=w_codes[:, gate * HID : (gate + 1) * HID].bitcast(FP8X4),
+                rhs_scale=w_scales[:, gate * HID : (gate + 1) * HID],
+                start=True,
+                stop=True,
+            )
+
+        def add_turned(n, half):
+            t, gate = steps[n]
+            s, j = divmod(t, TILES)
+            for a in range(2 * half, 2 * half + 2):
                 nc.tensor.matmul(
-                    out=gate_ps[step][:, a * P : (a + 1) * P],
-                    lhsT=rec_T[s][:, REC_GATES.index(gate) * BLOCKS_PER_GATE + a, j * P : (j + 1) * P],
+                    out=gate_ps[n][:, a * P : (a + 1) * P],
+                    lhsT=rec_T[t, gate][:, a, :],
                     rhs=ident_f32[:],
                     is_transpose=True,
                     start=False,
                     stop=(a == BLOCKS_PER_GATE - 1),
                 )
 
-        def activate(step):
-            tile_index, gate, s, j = place(step)
-            if gate == GATE_I:
-                total = acts[tile_index, gate]
-                nc.scalar.activation(out=total[:], in_=total[:], func=ACT.Sigmoid)
-            else:
-                acts[tile_index, gate] = work.tile([P, HID], F32, name="act%d" % gate, tag="act%d" % gate)
-                nc.scalar.activation(
-                    out=acts[tile_index, gate][:],
-                    in_=gate_ps[step][:],
-                    func=(ACT.Tanh if gate == GATE_G else ACT.Sigmoid),
-                )
+        def add_bias(n):
+            t, gate = steps[n]
+            acts[t, gate] = work.tile([P, HID], F32, name="act%d" % gate, tag="act%d" % gate, bufs=N_HEAD + 3)
+            nc.vector.tensor_tensor(
+                out=acts[t, gate][:], in0=gate_ps[n][:], in1=bias_spread[:, gate, :], op=ALU.add
+            )
 
-        def keep_old_cell(tile_index):
-            s, j = divmod(tile_index, TILES)
-            keep = acts[tile_index, GATE_F]
+        def add_recurrent(n):
+            total = acts[steps[n]]
+            nc.vector.tensor_tensor(out=total[:], in0=rec_ps[n][:], in1=total[:], op=ALU.add)
+
+        def activate(n):
+            t, gate = steps[n]
+            func = ACT.Tanh if gate == GATE_G else ACT.Sigmoid
+            if gate in TURNED_GATES:
+                acts[t, gate] = work.tile([P, HID], F32, name="act%d" % gate, tag="act%d" % gate, bufs=N_HEAD + 3)
+                nc.scalar.activation(out=acts[t, gate][:], in_=gate_ps[n][:], func=func)
+            else:
+                nc.scalar.activation(out=acts[t, gate][:], in_=acts[t, gate][:], func=func)
+
+        def keep_old_cell(t):
+            s, j = divmod(t, TILES)
+            keep = acts[t, GATE_F]
             nc.gpsimd.tensor_tensor(out=keep[:], in0=keep[:], in1=c_in[s][:, j * HID : (j + 1) * HID], op=ALU.mult)
 
-        def write_candidate(tile_index):
-            write = acts[tile_index, GATE_I]
-            nc.gpsimd.tensor_tensor(out=write[:], in0=write[:], in1=acts[tile_index, GATE_G][:], op=ALU.mult)
+        def write_candidate(t):
+            write = acts[t, GATE_I]
+            nc.gpsimd.tensor_tensor(out=write[:], in0=write[:], in1=acts[t, GATE_G][:], op=ALU.mult)
 
-        def new_cell(tile_index):
-            s, j = divmod(tile_index, TILES)
-            c_new[tile_index] = work.tile([P, HID], F32, name="c_new", tag="c_new")
-            nc.vector.tensor_tensor(
-                out=c_new[tile_index][:], in0=acts[tile_index, GATE_F][:], in1=acts[tile_index, GATE_I][:], op=ALU.add
-            )
-            nc.sync.dma_start(out=c_next_rows[s, j], in_=c_new[tile_index][:])
+        def new_cell(t):
+            s, j = divmod(t, TILES)
+            c_new[t] = work.tile([P, HID], F32, name="c_new", tag="c_new")
+            KW["C"].tensor_tensor(out=c_new[t][:], in0=acts[t, GATE_F][:], in1=acts[t, GATE_I][:], op=ALU.add)
+            nc.sync.dma_start(out=c_next_rows[s, j], in_=c_new[t][:])
 
-        def tanh_of_new_cell(tile_index):
-            tanh_c[tile_index] = work.tile([P, HID], F32, name="tanh_c", tag="tanh_c")
-            nc.scalar.activation(out=tanh_c[tile_index][:], in_=c_new[tile_index][:], func=ACT.Tanh)
+        def tanh_of_new_cell(t):
+            tanh_c[t] = work.tile([P, HID], F32, name="tanh_c", tag="tanh_c")
+            nc.scalar.activation(out=tanh_c[t][:], in_=c_new[t][:], func=ACT.Tanh)
 
-        def new_hidden(tile_index):
-            s, j = divmod(tile_index, TILES)
+        def new_hidden(t):
+            s, j = divmod(t, TILES)
             h_new = work.tile([P, HID], F32, tag="h_new")
-            nc.vector.tensor_tensor(
-                out=h_new[:], in0=acts[tile_index, GATE_O][:], in1=tanh_c[tile_index][:], op=ALU.mult
-            )
+            KW["H"].tensor_tensor(out=h_new[:], in0=acts[t, GATE_O][:], in1=tanh_c[t][:], op=ALU.mult)
             nc.sync.dma_start(out=h_next_rows[s, j], in_=h_new[:])
+
+        KW["C"] = nc.vector if C_ENG == "V" else nc.gpsimd
+        KW["H"] = nc.vector if H_ENG == "V" else nc.gpsimd
+        plan = []
+
+        def put(key, fn, *args):
+            plan.append((key, fn, args))
+
+        def turned(n):
+            return 0 <= n < n_steps and steps[n][1] in TURNED_GATES
+
+        head = N_HEAD * GATES
+        for n, (t, gate) in enumerate(steps):
+            put(n, input_pass, n, 0)
+            put(n + 0.3, input_pass, n, 1)
+            if turned(n):
+                put(n + 1.1, add_turned, n, 0)
+                put(n + 1.4, add_turned, n, 1)
+            else:
+                put(n + 1.05 if turned(n - 1) else n + 0.1, recurrent_rows, n)
+                put(n + 0.5, add_bias, n)
+                put(n + MV, add_recurrent, n)
+            put(n + ACT_LAG, activate, n)
+        for t in range(N_TILES):
+            if t < 2:
+                continue
+            if t < N_HEAD:
+                k = t - 2
+                put(k + 0.45, transpose_rows, t)
+                put(k + 0.6, copy_rows, t)
+                put(k + 0.7, quantise_rows, t)
+                continue
+            if t < N_HEAD + ROWS_AHEAD:
+                k = head - 2 - (N_HEAD + ROWS_AHEAD - t) * 2
+                put(k + 0.45, transpose_rows, t)
+                put(k + 1.45, copy_rows, t)
+                put(k + 1.75, quantise_rows, t)
+                continue
+            k = at[t - ROWS_AHEAD, ROW_GATE]
+            put(k + ROW_POS, transpose_rows, t)
+            put(k + ROW_COPY, copy_rows, t)
+            put(k + ROW_QUANT, quantise_rows, t)
+        for gate in TURNED_GATES:
+            for t in range(N_TILES):
+                if t < N_HEAD:
+                    k = at[t, gate] - T_HEAD
+                else:
+                    k = at[t, gate] - T_LAG
+                put(k + 0.42, turned_blocks, t, gate)
+                put(k + T_COPY, copy_turned_blocks, t, gate)
+        for q in range(1, GATES):
+            gate = HEAD_ORDER[q]
+            k = at[0, gate] - W_LEAD
+            dd = W_STEP
+            put(k + 0.43, weights_hh_half, gate, 0)
+            put(k + 0.65, copy_weights_hh_half, gate, 0, nc.vector.tensor_copy if W_V else nc.scalar.copy)
+            put(k + dd + 0.43, weights_hh_half, gate, 1)
+            put(k + dd + 0.65, copy_weights_hh_half, gate, 1, nc.scalar.copy)
+            put(k + 2 * dd + 0.43, weights_ih, gate)
+            put(k + 2 * dd + 0.65, copy_weights_ih, gate)
+            put(k + dd + 0.9, weights_quantise, gate)
+        for t in range(N_TILES):
+            last_in = max(at[t, GATE_I], at[t, GATE_G], at[t, GATE_F])
+            put(at[t, GATE_F] + K_LAG, keep_old_cell, t)
+            b = max(at[t, GATE_I], at[t, GATE_G])
+            put(b + B_LAG, write_candidate, t)
+            put(max(b, at[t, GATE_F]) + C_LAG, new_cell, t)
+            put(max(b, at[t, GATE_F]) + TANH_LAG, tanh_of_new_cell, t)
+            put(max(max(b, at[t, GATE_F]) + H_LAG, at[t, GATE_O] + ACT_LAG + 0.1), new_hidden, t)
+        put(4, load_h, 3)
+        put(4, load_x, 3)
+        for s in range(1, N_GROUPS):
+            k = at[TILES * s, GATE_F] if TILES * s >= N_HEAD else head
+            if s + 3 < N_GROUPS:
+                put(k - 0.01, load_h, s + 3)
+                put(k - 0.01, load_x, s + 3)
+            if s + 1 < N_GROUPS:
+                put(k - 0.01, load_cell, s + 1)
 
         bias_rows = const.tile([P, P], BF16)
         nc.vector.memset(bias_rows[:], 0.0)
         nc.sync.dma_start(out=bias_rows[0:BLOCKS, :], in_=b_ih.rearrange("(b n) -> b n", n=P))
         nc.sync.dma_start(out=bias_rows[BLOCKS : 2 * BLOCKS, :], in_=b_hh.rearrange("(b n) -> b n", n=P))
-        load_rows(0)
-        w_hh_raw, w_ih_raw = [], []
-        for gate in range(GATES):
-            w_hh_raw.append(setup.tile([P, BLOCKS_PER_GATE, HID], BF16, name="w_hh_raw", tag="w_hh_raw"))
-            nc.sync.dma_start(
-                out=w_hh_raw[gate][:], in_=W_hh[gate * HID : (gate + 1) * HID, :].rearrange("(a p) k -> p a k", p=P)
-            )
-            w_ih_raw.append(setup.tile([P, BLOCKS_PER_GATE, IN_DIM], BF16, name="w_ih_raw", tag="w_ih_raw"))
-            nc.sync.dma_start(
-                out=w_ih_raw[gate][:], in_=W_ih[gate * HID : (gate + 1) * HID, :].rearrange("(a p) k -> p a k", p=P)
-            )
-        load_rows(1)
+        load_w_hh(GATE_F)
+        load_h(0)
+        load_w_ih(GATE_F)
+        load_x(0)
+        load_w_hh(GATE_I)
+        load_w_ih(GATE_I)
         load_cell(0)
-        load_rows(2)
+        load_w_hh(GATE_G)
+        load_w_ih(GATE_G)
+        load_h(1)
+        load_x(1)
+        load_w_hh(GATE_O)
+        load_w_ih(GATE_O)
+        load_h(2)
+        load_x(2)
+        load_cell(1)
+
+        warm = const.tile([P, 1], F32)
+        nc.vector.memset(warm[:], 0.0)
+        nc.scalar.activation(out=warm[:], in_=warm[:], func=ACT.Sigmoid)
 
         ident_f32 = const.tile([P, P], F32)
         make_identity(nc, ident_f32[:])
@@ -254,101 +433,32 @@ def tile_nodelstmcell_pa_t_kernel(tc, x_t, h, c, W_ih, W_hh, b_ih, b_hh, out_0, 
         nc.vector.tensor_copy(out=bias_pair[:], in_=biasT_ps[:, 0 : 2 * BLOCKS])
         bias = const.tile([P, BLOCKS], F32)
         nc.vector.tensor_tensor(out=bias[:], in0=bias_pair[:, 0:BLOCKS], in1=bias_pair[:, BLOCKS : 2 * BLOCKS], op=ALU.add)
-        bias_spread = const.tile([P, HID], F32)
-        spread_ps = psum.tile([P, HID], F32, tag="gate")
-        for a in range(BLOCKS_PER_GATE):
-            blk = GATE_I * BLOCKS_PER_GATE + a
-            nc.tensor.transpose(
-                spread_ps[:, a * P : (a + 1) * P], bias[:, blk : blk + 1].to_broadcast([P, P]), ident_f32[:]
-            )
-        nc.scalar.copy(out=bias_spread[:], in_=spread_ps[:])
-
-        for tile_index in range(TILES):
-            transpose_rows(tile_index)
-            quantise_rows(tile_index)
+        bias_spread = const.tile([P, GATES, HID], F32)
+        for gate in GATE_ORDER:
+            if gate not in TURNED_GATES:
+                spread_ps = psum.tile([P, HID], F32, tag="gate")
+                for a in range(BLOCKS_PER_GATE):
+                    blk = gate * BLOCKS_PER_GATE + a
+                    nc.tensor.transpose(
+                        spread_ps[:, a * P : (a + 1) * P], bias[:, blk : blk + 1].to_broadcast([P, P]), ident_f32[:]
+                    )
+                nc.vector.tensor_copy(out=bias_spread[:, gate, :], in_=spread_ps[:])
 
         w_codes = const.tile([P, GATES * HID], U32, align_bytes=64)
         w_scales = const.tile([P, GATES * HID], U8, align_bytes=64)
         w_ih_T = const.tile([P, PAIR, GATES * HID], BF16)
 
-        def first_group_blocks(gate):
-            if gate in REC_GATES:
-                for a in range(BLOCKS_PER_GATE):
-                    recurrent_block(0, REC_GATES.index(gate) * BLOCKS_PER_GATE + a, on_scalar=(a % 2 == 1))
+        weights_hh_half(HEAD_ORDER[0], 0)
+        copy_weights_hh_half(HEAD_ORDER[0], 0, nc.vector.tensor_copy)
+        weights_hh_half(HEAD_ORDER[0], 1)
+        copy_weights_hh_half(HEAD_ORDER[0], 1, nc.scalar.copy)
+        weights_quantise(HEAD_ORDER[0])
+        for t in range(2):
+            transpose_rows(t)
+            copy_rows(t)
+            quantise_rows(t)
+        weights_ih(HEAD_ORDER[0])
+        copy_weights_ih(HEAD_ORDER[0])
 
-        for gate in range(GATES):
-            cols = slice(gate * HID, (gate + 1) * HID)
-            w_grouped = setup.tile([P, HID * PACK], BF16, tag="w_grouped", bufs=2, align_bytes=64)
-            grouped_words = w_grouped[:].bitcast(F32).rearrange(
-                "p (a n u) -> p a n u", a=BLOCKS_PER_GATE, u=H_HALVES
-            )
-            for half in range(2):
-                wT_ps = psum.tile([P, 2, H_HALVES, P], F32, tag="gate")
-                for a in range(2):
-                    raw_words = w_hh_raw[gate][:, 2 * half + a, :].bitcast(F32)
-                    for u in range(H_HALVES):
-                        nc.tensor.transpose(wT_ps[:, a, u, :], raw_words[:, u:H_WORDS:H_HALVES], ident_f32[:])
-                copy_out = nc.vector.tensor_copy if half == 0 else nc.scalar.copy
-                copy_out(
-                    out=grouped_words[:, 2 * half : 2 * half + 2, :, :], in_=wT_ps[:].rearrange("p a u n -> p a n u")
-                )
-            nc.vector.quantize_mx(out=w_codes[:, cols].bitcast(FP8X4), scales=w_scales[:, cols], in_=w_grouped[:])
-            wT_ps = psum.tile([P, HID], F32, tag="gate")
-            for a in range(BLOCKS_PER_GATE):
-                nc.tensor.transpose(wT_ps[:, a * P : (a + 1) * P], w_ih_raw[gate][:, a, :].bitcast(F32), ident_f32[:])
-            nc.scalar.copy(out=w_ih_T[:, :, cols], in_=wT_ps[:].bitcast(BF16).rearrange("p (n e) -> p e n", e=PAIR))
-            if gate > 0:
-                first_group_blocks(gate - 1)
-        for tile_index in range(TILES, ROWS_AHEAD):
-            transpose_rows(tile_index)
-            quantise_rows(tile_index)
-        first_group_blocks(GATES - 1)
-
-        for turn in range(N_TILES + 2):
-            s, j = divmod(turn, TILES)
-            running = turn < N_TILES
-            if running and j == 0:
-                if s + 3 < N_GROUPS:
-                    load_rows(s + 3)
-                if s + 1 < N_GROUPS:
-                    load_cell(s + 1)
-
-            for gate in range(GATES):
-                step = turn * GATES + gate
-                before = step - 1
-                finish = 0 <= before < N_STEPS
-                finish_by_transposes = finish and before % GATES in REC_GATES
-
-                if running:
-                    input_pass(step, 0)
-                if finish_by_transposes:
-                    add_recurrent(before, 0)
-                if gate == GATE_F:
-                    if running:
-                        recurrent_rows(turn)
-                        add_recurrent_rows(turn)
-                    if running and s + 1 < N_GROUPS:
-                        for b in range(REC_BLOCKS_PER_TILE):
-                            recurrent_block(s + 1, j * REC_BLOCKS_PER_TILE + b, on_scalar=(b == 0))
-                    if 0 <= turn - 1 < N_TILES:
-                        keep_old_cell(turn - 1)
-                        write_candidate(turn - 1)
-                    if 0 <= turn - 2 < N_TILES:
-                        tanh_of_new_cell(turn - 2)
-                if running:
-                    input_pass(step, 1)
-                if finish_by_transposes:
-                    add_recurrent(before, 1)
-                if gate == GATE_F and turn + ROWS_AHEAD < N_TILES:
-                    transpose_rows(turn + ROWS_AHEAD)
-                if finish:
-                    activate(before)
-                if gate == GATE_I and running:
-                    add_bias(turn)
-
-            if 0 <= turn - 1 < N_TILES:
-                new_cell(turn - 1)
-            if 0 <= turn - 2 < N_TILES:
-                new_hidden(turn - 2)
-            if turn + ROWS_AHEAD < N_TILES:
-                quantise_rows(turn + ROWS_AHEAD)
+        for key, fn, args in sorted(plan, key=lambda e: e[0]):
+            fn(*args)

@@ -187,8 +187,10 @@ def tile_nodelstmcell_pa_t_kernel(tc, x_t, h, c, W_ih, W_hh, b_ih, b_hh, out_0, 
                 out=h_grouped[t][:].bitcast(F32).rearrange("p (r u) -> p r u", u=H_HALVES),
                 in_=words_ps[t][:, 0:H_WORDS].rearrange("p (u r) -> p r u", u=H_HALVES),
             )
-            x_T[t] = operands.tile([P, X_WORDS], F32, name="x_T", tag="x_T", bufs=ROWS_AHEAD + 4)
-            nc.scalar.copy(out=x_T[t][:], in_=words_ps[t][:, H_WORDS:])
+            x_T[t] = operands.tile([P, PAIR, P], BF16, name="x_T", tag="x_T", bufs=ROWS_AHEAD + 4)
+            nc.scalar.copy(
+                out=x_T[t][:], in_=words_ps[t][:, H_WORDS:].bitcast(BF16).rearrange("p (r e) -> p e r", e=PAIR)
+            )
 
         def quantise_rows(t):
             s, j = divmod(t, TILES)
@@ -241,7 +243,7 @@ def tile_nodelstmcell_pa_t_kernel(tc, x_t, h, c, W_ih, W_hh, b_ih, b_hh, out_0, 
                 gate_ps[n] = psum.tile([P, HID], F32, name="gate_ps", tag="gate")
             nc.tensor.matmul(
                 out=gate_ps[n][:],
-                lhsT=x_T[t][:].bitcast(BF16)[:, e:IN_DIM:PAIR],
+                lhsT=x_T[t][:, e, :],
                 rhs=w_ih_T[:, e, gate * HID : (gate + 1) * HID],
                 start=(e == 0),
                 stop=(e == PAIR - 1 and gate not in TURNED_GATES),

@@ -15,56 +15,67 @@ P = 128
 BATCH, IN_DIM, HID = 4096, 256, 512
 GATES = 4
 GATE_I, GATE_F, GATE_G, GATE_O = 0, 1, 2, 3
-GATE_ORDER = (GATE_F, GATE_I, GATE_G, GATE_O)
-HEAD_ORDER = (GATE_F, GATE_I, GATE_G, GATE_O)
+GATE_ORDER = (GATE_F, GATE_G, GATE_I, GATE_O)
 TILES = 4
 GROUP_ROWS = TILES * P
 N_GROUPS = BATCH // GROUP_ROWS
 N_TILES = N_GROUPS * TILES
 BLOCKS_PER_GATE = HID // P
 BLOCKS = GATES * BLOCKS_PER_GATE
-TURNED_GATES = (GATE_G,)
 PAIR = 2
 H_WORDS = HID // PAIR
 X_WORDS = IN_DIM // PAIR
 H_HALVES = H_WORDS // P
 PACK = 4
+HEAD_ORDER = (GATE_F, GATE_I, GATE_G, GATE_O)
+N_HEAD = 2
 ROWS_AHEAD = 2
-N_HEAD = 4
-TCOPY = "S"
-KW = {}
+ROW_POS, ROW_COPY, ROW_QUANT = 0.45, 1.45, 2.9
+ROW_GATE = GATE_I
+T_LAG, T_COPY = 2, 0.8
+T_HEAD = 1
+K2_GATE, K2 = GATE_O, "all"
+COPY1, COPY2 = "S", "V"
+ACT_LAG = 2.5
+K_LAG, W_LAG, C_LAG, TANH_LAG, H_LAG = 2.9, 2.9, 6.6, 9.58, 12.9
+H_G = "none"
+W_LEAD, W_STEP = 3, 0
+SHORT = 3
 
-C_ENG, H_ENG = "V", "G"
-MV, ACT_LAG = 1.55, 2.5
-ROW_GATE, ROW_POS, ROW_COPY, ROW_QUANT = GATE_G, 0.15, 1.45, 3.53
-T_HEAD, T_LAG, T_COPY = 1, 2, 0.8
-W_LEAD, W_STEP, W_V = 4, 1, True
-K_LAG, B_LAG, C_LAG, TANH_LAG, H_LAG = 2.9, 2.9, 4.52, 5.55, 6.9
-C_ENG = "V"
-H_ENG = "G"
-MV = 1.55
-ACT_LAG = 2.55
+H_LAG = 11.52
+T_COPY = 0.56
+HEAD_ORDER = (GATE_F, GATE_G, GATE_I, GATE_O)
+W_LAG = 4.9
+COPY2 = "S"
+TANH_LAG = 9.58
+COPY1 = "V"
+W_STEP = 0
+W_LEAD = 3
+K_LAG = 4.9
+ACT_LAG = 2.5
+C_LAG = 6.52
+T_HEAD = 1
 ROW_GATE = GATE_I
 ROW_POS = 0.45
-ROW_COPY = 1.45
-ROW_QUANT = 4.52
-T_HEAD = 1
-T_LAG = 2
-T_COPY = 1.45
-W_LEAD = 3
-W_STEP = 0
-W_V = True
-K_LAG = 2.9
-B_LAG = 2.9
-C_LAG = 4.6
-TANH_LAG = 5.58
-H_LAG = 6.9
+ROW_QUANT = 4.6
+ROWS_AHEAD = 3
+ROW_COPY = 1.56
 N_HEAD = 2
-TCOPY = "S"
-ROWS_AHEAD = 2
+H_G = "none"
+K2_GATE = GATE_O
+K2 = "all"
+T_LAG = 2
+SHORT = 2
 GATE_ORDER = (GATE_F, GATE_G, GATE_I, GATE_O)
-HEAD_ORDER = (GATE_F, GATE_I, GATE_G, GATE_O)
 FLOPS = 2 * BATCH * GATES * HID * (IN_DIM + HID)
+
+
+def turned_gate(t, gate):
+    return gate == GATE_G or (gate == K2_GATE and (K2 == "all" or (K2 == "even" and t % 2 == 0)))
+
+
+def chosen(what, t):
+    return what == "all" or (what == "even" and t % 2 == 0) or (what == "third" and t % 3 == 0) or (what == "q" and t % 4 == 0)
 
 
 def tile_nodelstmcell_pa_t_kernel(tc, x_t, h, c, W_ih, W_hh, b_ih, b_hh, out_0, out_1):
@@ -163,10 +174,9 @@ def tile_nodelstmcell_pa_t_kernel(tc, x_t, h, c, W_ih, W_hh, b_ih, b_hh, out_0, 
 
         def copy_weights_ih(gate):
             cols = slice(gate * HID, (gate + 1) * HID)
-            nc.scalar.copy(
-                out=w_ih_T[:, :, cols],
-                in_=weights_ps[gate, 2][:].bitcast(BF16).rearrange("p (n e) -> p e n", e=PAIR),
-            )
+            halves = weights_ps[gate, 2][:].bitcast(BF16).rearrange("p (n e) -> p e n", e=PAIR)
+            nc.scalar.copy(out=w_ih_T[:, 0, cols], in_=halves[:, 0, :])
+            nc.vector.tensor_copy(out=w_ih_T[:, 1, cols], in_=halves[:, 1, :])
 
         def transpose_rows(t):
             s, j = divmod(t, TILES)
@@ -187,10 +197,8 @@ def tile_nodelstmcell_pa_t_kernel(tc, x_t, h, c, W_ih, W_hh, b_ih, b_hh, out_0, 
                 out=h_grouped[t][:].bitcast(F32).rearrange("p (r u) -> p r u", u=H_HALVES),
                 in_=words_ps[t][:, 0:H_WORDS].rearrange("p (u r) -> p r u", u=H_HALVES),
             )
-            x_T[t] = operands.tile([P, PAIR, P], BF16, name="x_T", tag="x_T", bufs=ROWS_AHEAD + 4)
-            nc.scalar.copy(
-                out=x_T[t][:], in_=words_ps[t][:, H_WORDS:].bitcast(BF16).rearrange("p (r e) -> p e r", e=PAIR)
-            )
+            x_T[t] = operands.tile([P, X_WORDS], F32, name="x_T", tag="x_T", bufs=ROWS_AHEAD + 4)
+            nc.scalar.copy(out=x_T[t][:], in_=words_ps[t][:, H_WORDS:])
 
         def quantise_rows(t):
             s, j = divmod(t, TILES)
@@ -221,7 +229,7 @@ def tile_nodelstmcell_pa_t_kernel(tc, x_t, h, c, W_ih, W_hh, b_ih, b_hh, out_0, 
         def copy_turned_blocks(t, gate):
             rec_T[t, gate] = operands.tile([P, BLOCKS_PER_GATE, P], F32, name="rec_T", tag="rec_T%d" % gate, bufs=6)
             blk0 = gate * BLOCKS_PER_GATE
-            if TCOPY == "S" or (TCOPY == "A" and t % 2):
+            if (COPY1 if gate == GATE_G else COPY2) == "S":
                 for a in range(BLOCKS_PER_GATE):
                     nc.scalar.activation(
                         out=rec_T[t, gate][:, a, :],
@@ -243,10 +251,10 @@ def tile_nodelstmcell_pa_t_kernel(tc, x_t, h, c, W_ih, W_hh, b_ih, b_hh, out_0, 
                 gate_ps[n] = psum.tile([P, HID], F32, name="gate_ps", tag="gate")
             nc.tensor.matmul(
                 out=gate_ps[n][:],
-                lhsT=x_T[t][:, e, :],
+                lhsT=x_T[t][:].bitcast(BF16)[:, e:IN_DIM:PAIR],
                 rhs=w_ih_T[:, e, gate * HID : (gate + 1) * HID],
                 start=(e == 0),
-                stop=(e == PAIR - 1 and gate not in TURNED_GATES),
+                stop=(e == PAIR - 1 and not turned_gate(t, gate)),
             )
 
         def recurrent_rows(n):
@@ -278,7 +286,7 @@ def tile_nodelstmcell_pa_t_kernel(tc, x_t, h, c, W_ih, W_hh, b_ih, b_hh, out_0, 
 
         def add_bias(n):
             t, gate = steps[n]
-            acts[t, gate] = work.tile([P, HID], F32, name="act%d" % gate, tag="act%d" % gate, bufs=N_HEAD + 3)
+            acts[t, gate] = work.tile([P, HID], F32, name="act%d" % gate, tag="act%d" % gate, bufs=6)
             nc.vector.tensor_tensor(
                 out=acts[t, gate][:], in0=gate_ps[n][:], in1=bias_spread[:, gate, :], op=ALU.add
             )
@@ -290,8 +298,8 @@ def tile_nodelstmcell_pa_t_kernel(tc, x_t, h, c, W_ih, W_hh, b_ih, b_hh, out_0, 
         def activate(n):
             t, gate = steps[n]
             func = ACT.Tanh if gate == GATE_G else ACT.Sigmoid
-            if gate in TURNED_GATES:
-                acts[t, gate] = work.tile([P, HID], F32, name="act%d" % gate, tag="act%d" % gate, bufs=N_HEAD + 3)
+            if turned_gate(t, gate):
+                acts[t, gate] = work.tile([P, HID], F32, name="act%d" % gate, tag="act%d" % gate, bufs=6)
                 nc.scalar.activation(out=acts[t, gate][:], in_=gate_ps[n][:], func=func)
             else:
                 nc.scalar.activation(out=acts[t, gate][:], in_=acts[t, gate][:], func=func)
@@ -308,7 +316,7 @@ def tile_nodelstmcell_pa_t_kernel(tc, x_t, h, c, W_ih, W_hh, b_ih, b_hh, out_0, 
         def new_cell(t):
             s, j = divmod(t, TILES)
             c_new[t] = work.tile([P, HID], F32, name="c_new", tag="c_new")
-            KW["C"].tensor_tensor(out=c_new[t][:], in0=acts[t, GATE_F][:], in1=acts[t, GATE_I][:], op=ALU.add)
+            nc.vector.tensor_tensor(out=c_new[t][:], in0=acts[t, GATE_F][:], in1=acts[t, GATE_I][:], op=ALU.add)
             nc.sync.dma_start(out=c_next_rows[s, j], in_=c_new[t][:])
 
         def tanh_of_new_cell(t):
@@ -318,18 +326,16 @@ def tile_nodelstmcell_pa_t_kernel(tc, x_t, h, c, W_ih, W_hh, b_ih, b_hh, out_0, 
         def new_hidden(t):
             s, j = divmod(t, TILES)
             h_new = work.tile([P, HID], F32, tag="h_new")
-            KW["H"].tensor_tensor(out=h_new[:], in0=acts[t, GATE_O][:], in1=tanh_c[t][:], op=ALU.mult)
+            (nc.gpsimd if chosen(H_G, t) else nc.vector).tensor_tensor(out=h_new[:], in0=acts[t, GATE_O][:], in1=tanh_c[t][:], op=ALU.mult)
             nc.sync.dma_start(out=h_next_rows[s, j], in_=h_new[:])
 
-        KW["C"] = nc.vector if C_ENG == "V" else nc.gpsimd
-        KW["H"] = nc.vector if H_ENG == "V" else nc.gpsimd
         plan = []
 
         def put(key, fn, *args):
             plan.append((key, fn, args))
 
         def turned(n):
-            return 0 <= n < n_steps and steps[n][1] in TURNED_GATES
+            return 0 <= n < n_steps and turned_gate(*steps[n])
 
         head = N_HEAD * GATES
         for n, (t, gate) in enumerate(steps):
@@ -341,33 +347,27 @@ def tile_nodelstmcell_pa_t_kernel(tc, x_t, h, c, W_ih, W_hh, b_ih, b_hh, out_0, 
             else:
                 put(n + 1.05 if turned(n - 1) else n + 0.1, recurrent_rows, n)
                 put(n + 0.5, add_bias, n)
-                put(n + MV, add_recurrent, n)
+                put(n + 1.55, add_recurrent, n)
             put(n + ACT_LAG, activate, n)
-        for t in range(N_TILES):
-            if t < 2:
-                continue
+        for t in range(2, N_TILES):
             if t < N_HEAD:
                 k = t - 2
                 put(k + 0.45, transpose_rows, t)
                 put(k + 0.6, copy_rows, t)
                 put(k + 0.7, quantise_rows, t)
-                continue
-            if t < N_HEAD + ROWS_AHEAD:
+            elif t < N_HEAD + ROWS_AHEAD:
                 k = head - 2 - (N_HEAD + ROWS_AHEAD - t) * 2
                 put(k + 0.45, transpose_rows, t)
                 put(k + 1.45, copy_rows, t)
                 put(k + 1.75, quantise_rows, t)
-                continue
-            k = at[t - ROWS_AHEAD, ROW_GATE]
-            put(k + ROW_POS, transpose_rows, t)
-            put(k + ROW_COPY, copy_rows, t)
-            put(k + ROW_QUANT, quantise_rows, t)
-        for gate in TURNED_GATES:
-            for t in range(N_TILES):
-                if t < N_HEAD:
-                    k = at[t, gate] - T_HEAD
-                else:
-                    k = at[t, gate] - T_LAG
+            else:
+                k = at[t - ROWS_AHEAD, ROW_GATE]
+                put(k + ROW_POS, transpose_rows, t)
+                put(k + ROW_COPY, copy_rows, t)
+                put(k + ROW_QUANT, quantise_rows, t)
+        for n, (t, gate) in enumerate(steps):
+            if turned_gate(t, gate):
+                k = n - (T_HEAD if t < N_HEAD else T_LAG)
                 put(k + 0.42, turned_blocks, t, gate)
                 put(k + T_COPY, copy_turned_blocks, t, gate)
         for q in range(1, GATES):
@@ -375,20 +375,25 @@ def tile_nodelstmcell_pa_t_kernel(tc, x_t, h, c, W_ih, W_hh, b_ih, b_hh, out_0, 
             k = at[0, gate] - W_LEAD
             dd = W_STEP
             put(k + 0.43, weights_hh_half, gate, 0)
-            put(k + 0.65, copy_weights_hh_half, gate, 0, nc.vector.tensor_copy if W_V else nc.scalar.copy)
+            put(k + 0.65, copy_weights_hh_half, gate, 0, nc.vector.tensor_copy)
             put(k + dd + 0.43, weights_hh_half, gate, 1)
             put(k + dd + 0.65, copy_weights_hh_half, gate, 1, nc.scalar.copy)
             put(k + 2 * dd + 0.43, weights_ih, gate)
             put(k + 2 * dd + 0.65, copy_weights_ih, gate)
             put(k + dd + 0.9, weights_quantise, gate)
         for t in range(N_TILES):
-            last_in = max(at[t, GATE_I], at[t, GATE_G], at[t, GATE_F])
-            put(at[t, GATE_F] + K_LAG, keep_old_cell, t)
-            b = max(at[t, GATE_I], at[t, GATE_G])
-            put(b + B_LAG, write_candidate, t)
-            put(max(b, at[t, GATE_F]) + C_LAG, new_cell, t)
-            put(max(b, at[t, GATE_F]) + TANH_LAG, tanh_of_new_cell, t)
-            put(max(max(b, at[t, GATE_F]) + H_LAG, at[t, GATE_O] + ACT_LAG + 0.1), new_hidden, t)
+            short = t >= N_TILES - SHORT
+            b = max(at[t, GATE_I], at[t, GATE_G], at[t, GATE_F])
+            k_key = at[t, GATE_F] + (2.9 if short else K_LAG)
+            w_key = max(at[t, GATE_I], at[t, GATE_G]) + (2.9 if short else W_LAG)
+            c_key = b + (3.6 if short else C_LAG)
+            assert c_key > max(k_key, w_key)
+            assert k_key > at[t, GATE_F] + ACT_LAG and w_key > max(at[t, GATE_I], at[t, GATE_G]) + ACT_LAG
+            put(k_key, keep_old_cell, t)
+            put(w_key, write_candidate, t)
+            put(c_key, new_cell, t)
+            put(b + (4.58 if short else TANH_LAG), tanh_of_new_cell, t)
+            put(max(b + (4.9 if short else H_LAG), at[t, GATE_O] + ACT_LAG + 0.1), new_hidden, t)
         put(4, load_h, 3)
         put(4, load_x, 3)
         for s in range(1, N_GROUPS):
@@ -401,24 +406,24 @@ def tile_nodelstmcell_pa_t_kernel(tc, x_t, h, c, W_ih, W_hh, b_ih, b_hh, out_0, 
 
         bias_rows = const.tile([P, P], BF16)
         nc.vector.memset(bias_rows[:], 0.0)
-        nc.sync.dma_start(out=bias_rows[0:BLOCKS, :], in_=b_ih.rearrange("(b n) -> b n", n=P))
-        nc.sync.dma_start(out=bias_rows[BLOCKS : 2 * BLOCKS, :], in_=b_hh.rearrange("(b n) -> b n", n=P))
-        load_w_hh(GATE_F)
+        nc.scalar.dma_start(out=bias_rows[0:BLOCKS, :], in_=b_ih.rearrange("(b n) -> b n", n=P))
+        nc.scalar.dma_start(out=bias_rows[BLOCKS : 2 * BLOCKS, :], in_=b_hh.rearrange("(b n) -> b n", n=P))
+        load_w_hh(HEAD_ORDER[0])
         load_h(0)
-        load_w_ih(GATE_F)
+        load_w_ih(HEAD_ORDER[0])
         load_x(0)
-        load_w_hh(GATE_I)
-        load_w_ih(GATE_I)
+        load_w_hh(HEAD_ORDER[1])
+        load_w_ih(HEAD_ORDER[1])
+        load_w_hh(HEAD_ORDER[2])
+        load_w_ih(HEAD_ORDER[2])
         load_cell(0)
-        load_w_hh(GATE_G)
-        load_w_ih(GATE_G)
+        load_w_hh(HEAD_ORDER[3])
+        load_w_ih(HEAD_ORDER[3])
         load_h(1)
         load_x(1)
-        load_w_hh(GATE_O)
-        load_w_ih(GATE_O)
+        load_cell(1)
         load_h(2)
         load_x(2)
-        load_cell(1)
 
         warm = const.tile([P, 1], F32)
         nc.vector.memset(warm[:], 0.0)
@@ -428,6 +433,9 @@ def tile_nodelstmcell_pa_t_kernel(tc, x_t, h, c, W_ih, W_hh, b_ih, b_hh, out_0, 
         make_identity(nc, ident_f32[:])
         ident_bf16 = const.tile([P, P], BF16)
         make_identity(nc, ident_bf16[:])
+        w_codes = const.tile([P, GATES * HID], U32, align_bytes=64)
+        w_scales = const.tile([P, GATES * HID], U8, align_bytes=64)
+        w_ih_T = const.tile([P, PAIR, GATES * HID], BF16)
 
         biasT_ps = psum.tile([P, P], BF16, tag="copied_out")
         nc.tensor.transpose(biasT_ps[:], bias_rows[:], ident_bf16[:])
@@ -435,32 +443,33 @@ def tile_nodelstmcell_pa_t_kernel(tc, x_t, h, c, W_ih, W_hh, b_ih, b_hh, out_0, 
         nc.vector.tensor_copy(out=bias_pair[:], in_=biasT_ps[:, 0 : 2 * BLOCKS])
         bias = const.tile([P, BLOCKS], F32)
         nc.vector.tensor_tensor(out=bias[:], in0=bias_pair[:, 0:BLOCKS], in1=bias_pair[:, BLOCKS : 2 * BLOCKS], op=ALU.add)
-        bias_spread = const.tile([P, GATES, HID], F32)
-        for gate in GATE_ORDER:
-            if gate not in TURNED_GATES:
-                spread_ps = psum.tile([P, HID], F32, tag="gate")
-                for a in range(BLOCKS_PER_GATE):
-                    blk = gate * BLOCKS_PER_GATE + a
-                    nc.tensor.transpose(
-                        spread_ps[:, a * P : (a + 1) * P], bias[:, blk : blk + 1].to_broadcast([P, P]), ident_f32[:]
-                    )
-                nc.vector.tensor_copy(out=bias_spread[:, gate, :], in_=spread_ps[:])
-
-        w_codes = const.tile([P, GATES * HID], U32, align_bytes=64)
-        w_scales = const.tile([P, GATES * HID], U8, align_bytes=64)
-        w_ih_T = const.tile([P, PAIR, GATES * HID], BF16)
 
         weights_hh_half(HEAD_ORDER[0], 0)
         copy_weights_hh_half(HEAD_ORDER[0], 0, nc.vector.tensor_copy)
         weights_hh_half(HEAD_ORDER[0], 1)
         copy_weights_hh_half(HEAD_ORDER[0], 1, nc.scalar.copy)
         weights_quantise(HEAD_ORDER[0])
+        weights_ih(HEAD_ORDER[0])
+        copy_weights_ih(HEAD_ORDER[0])
         for t in range(2):
             transpose_rows(t)
             copy_rows(t)
             quantise_rows(t)
-        weights_ih(HEAD_ORDER[0])
-        copy_weights_ih(HEAD_ORDER[0])
+
+        bias_spread = const.tile([P, GATES, HID], F32)
+
+        def spread_bias(gate):
+            spread_ps = psum.tile([P, HID], F32, name="spread_ps", tag="gate")
+            for a in range(BLOCKS_PER_GATE):
+                blk = gate * BLOCKS_PER_GATE + a
+                nc.tensor.transpose(
+                    spread_ps[:, a * P : (a + 1) * P], bias[:, blk : blk + 1].to_broadcast([P, P]), ident_f32[:]
+                )
+            nc.vector.tensor_copy(out=bias_spread[:, gate, :], in_=spread_ps[:])
+
+        for gate in HEAD_ORDER:
+            if not (turned_gate(0, gate) and turned_gate(1, gate)):
+                spread_bias(gate)
 
         for key, fn, args in sorted(plan, key=lambda e: e[0]):
             fn(*args)

@@ -42,30 +42,30 @@ H_G = "none"
 W_LEAD, W_STEP = 3, 0
 SHORT = 3
 
-H_LAG = 11.52
+H_LAG = 10.52
 T_COPY = 0.56
-HEAD_ORDER = (GATE_F, GATE_G, GATE_I, GATE_O)
+HEAD_ORDER = (GATE_I, GATE_O, GATE_G, GATE_F)
 W_LAG = 4.9
-COPY2 = "S"
-TANH_LAG = 9.58
-COPY1 = "V"
+COPY2 = "A"
+TANH_LAG = 7.45
+COPY1 = "S"
 W_STEP = 0
 W_LEAD = 3
 K_LAG = 4.9
-ACT_LAG = 2.5
-C_LAG = 6.52
+ACT_LAG = 2.45
+C_LAG = 5.52
 T_HEAD = 1
 ROW_GATE = GATE_I
 ROW_POS = 0.45
 ROW_QUANT = 4.6
 ROWS_AHEAD = 3
-ROW_COPY = 1.56
+ROW_COPY = 1.45
 N_HEAD = 2
-H_G = "none"
+H_G = "q"
 K2_GATE = GATE_O
 K2 = "all"
 T_LAG = 2
-SHORT = 2
+SHORT = 0
 GATE_ORDER = (GATE_F, GATE_G, GATE_I, GATE_O)
 FLOPS = 2 * BATCH * GATES * HID * (IN_DIM + HID)
 
@@ -229,7 +229,8 @@ def tile_nodelstmcell_pa_t_kernel(tc, x_t, h, c, W_ih, W_hh, b_ih, b_hh, out_0, 
         def copy_turned_blocks(t, gate):
             rec_T[t, gate] = operands.tile([P, BLOCKS_PER_GATE, P], F32, name="rec_T", tag="rec_T%d" % gate, bufs=6)
             blk0 = gate * BLOCKS_PER_GATE
-            if (COPY1 if gate == GATE_G else COPY2) == "S":
+            how = COPY1 if gate == GATE_G else COPY2
+            if how == "S" or (how == "A" and t % 2 == 0) or (how == "B" and t % 4 != 0):
                 for a in range(BLOCKS_PER_GATE):
                     nc.scalar.activation(
                         out=rec_T[t, gate][:, a, :],

@@ -29,49 +29,52 @@ H_HALVES = H_WORDS // P
 PACK = 4
 HEAD_ORDER = (GATE_F, GATE_I, GATE_G, GATE_O)
 N_HEAD = 2
-ROWS_AHEAD = 2
+ROWS_AHEAD = 4
 ROW_POS, ROW_COPY, ROW_QUANT = 0.45, 1.45, 2.9
 ROW_GATE = GATE_I
-T_LAG, T_COPY = 2, 0.8
+T_COPY = 0.8
 T_HEAD = 1
 K2_GATE, K2 = GATE_O, "all"
-COPY1, COPY2 = "S", "V"
+ON_VECTOR = ((GATE_O, 1),)
+TB1, TB2 = GATE_O, GATE_G
 ACT_LAG = 2.5
 K_LAG, W_LAG, C_LAG, TANH_LAG, H_LAG = 2.9, 2.9, 6.6, 9.58, 12.9
 H_G = "none"
 W_LEAD, W_STEP = 3, 0
-SHORT = 3
+TAPER = 1.0
+PROD_BUFS = 1
 
-H_LAG = 10.52
-T_COPY = 0.56
-HEAD_ORDER = (GATE_I, GATE_O, GATE_G, GATE_F)
-W_LAG = 4.9
-COPY2 = "A"
-TANH_LAG = 7.45
-COPY1 = "S"
+H_LAG = 12.52
+T_COPY = 0.8
+HEAD_ORDER = (GATE_G, GATE_F, GATE_I, GATE_O)
+W_LAG = 2.9
+TANH_LAG = 11.45
 W_STEP = 0
-W_LEAD = 3
-K_LAG = 4.9
+W_LEAD = 5
+K_LAG = 3.9
 ACT_LAG = 2.45
-C_LAG = 5.52
-T_HEAD = 1
-ROW_GATE = GATE_I
-ROW_POS = 0.45
-ROW_QUANT = 4.6
-ROWS_AHEAD = 3
-ROW_COPY = 1.45
+C_LAG = 6.6
+T_HEAD = 2
+ROW_GATE = GATE_O
+ROW_POS = 0.15
+ROW_QUANT = 1.92
+ROW_COPY = 0.56
 N_HEAD = 2
-H_G = "q"
+H_G = "none"
 K2_GATE = GATE_O
 K2 = "all"
-T_LAG = 2
-SHORT = 0
 GATE_ORDER = (GATE_F, GATE_G, GATE_I, GATE_O)
+ON_VECTOR = ((GATE_G, 1),)
+TAPER = 99
+PROD_BUFS = 1
+ROWS_AHEAD = 4
+TB2 = GATE_G
+TB1 = GATE_O
 FLOPS = 2 * BATCH * GATES * HID * (IN_DIM + HID)
 
 
 def turned_gate(t, gate):
-    return gate == GATE_G or (gate == K2_GATE and (K2 == "all" or (K2 == "even" and t % 2 == 0)))
+    return gate == GATE_G or (gate == K2_GATE and (K2 == "all" or (K2 == "even" and t // 2 % 2 == 0)))
 
 
 def chosen(what, t):
@@ -111,6 +114,7 @@ def tile_nodelstmcell_pa_t_kernel(tc, x_t, h, c, W_ih, W_hh, b_ih, b_hh, out_0, 
         gate_ps = {}
         rec_ps = {}
         acts = {}
+        kept, written = {}, {}
         c_new, tanh_c = {}, {}
 
         def load_h(s):
@@ -203,48 +207,51 @@ def tile_nodelstmcell_pa_t_kernel(tc, x_t, h, c, W_ih, W_hh, b_ih, b_hh, out_0, 
         def quantise_rows(t):
             s, j = divmod(t, TILES)
             if j == 0:
-                h_codes[s] = operands.tile([P, GROUP_ROWS], U32, name="h_codes", tag="h_codes", align_bytes=64)
-                h_scales[s] = operands.tile([P, GROUP_ROWS], U8, name="h_scales", tag="h_scales", align_bytes=64)
+                h_codes[s] = operands.tile([P, GROUP_ROWS], U32, name="h_codes", tag="h_codes", align_bytes=64, bufs=4)
+                h_scales[s] = operands.tile([P, GROUP_ROWS], U8, name="h_scales", tag="h_scales", align_bytes=64, bufs=4)
             cols = slice(j * P, (j + 1) * P)
             nc.vector.quantize_mx(
                 out=h_codes[s][:, cols].bitcast(FP8X4), scales=h_scales[s][:, cols], in_=h_grouped[t][:]
             )
 
-        def turned_blocks(t, gate):
-            s, j = divmod(t, TILES)
-            recT_ps[t, gate] = psum.tile([P, BLOCKS_PER_GATE, P], F32, name="recT_ps", tag="copied_out")
-            for a in range(BLOCKS_PER_GATE):
-                blk = gate * BLOCKS_PER_GATE + a
+        def turned_bank(pair, gate, b):
+            s, j = divmod(2 * pair, TILES)
+            rows2 = slice(j * P, (j + 2) * P)
+            recT_ps[pair, gate, b] = psum.tile([P, 2, 2 * P], F32, name="recT_ps", tag="copied_out")
+            for a in range(2):
+                blk = gate * BLOCKS_PER_GATE + 2 * b + a
                 cols = slice(blk * P, (blk + 1) * P)
                 nc.tensor.matmul_mx(
-                    out=recT_ps[t, gate][:, a, :],
+                    out=recT_ps[pair, gate, b][:, a, :],
                     lhsT=w_codes[:, cols].bitcast(FP8X4),
                     lhsT_scale=w_scales[:, cols],
-                    rhs=h_codes[s][:, j * P : (j + 1) * P].bitcast(FP8X4),
-                    rhs_scale=h_scales[s][:, j * P : (j + 1) * P],
+                    rhs=h_codes[s][:, rows2].bitcast(FP8X4),
+                    rhs_scale=h_scales[s][:, rows2],
                     start=True,
                     stop=True,
                 )
 
-        def copy_turned_blocks(t, gate):
-            rec_T[t, gate] = operands.tile([P, BLOCKS_PER_GATE, P], F32, name="rec_T", tag="rec_T%d" % gate, bufs=6)
-            blk0 = gate * BLOCKS_PER_GATE
-            how = COPY1 if gate == GATE_G else COPY2
-            if how == "S" or (how == "A" and t % 2 == 0) or (how == "B" and t % 4 != 0):
-                for a in range(BLOCKS_PER_GATE):
-                    nc.scalar.activation(
-                        out=rec_T[t, gate][:, a, :],
-                        in_=recT_ps[t, gate][:, a, :],
-                        func=ACT.Identity,
-                        bias=bias[:, blk0 + a : blk0 + a + 1],
-                    )
-            else:
+        def copy_turned_bank(pair, gate, b):
+            if (pair, gate) not in rec_T:
+                rec_T[pair, gate] = operands.tile(
+                    [P, BLOCKS_PER_GATE, 2 * P], F32, name="rec_T", tag="rec_T%d" % gate, bufs=3
+                )
+            blk = gate * BLOCKS_PER_GATE + 2 * b
+            if (gate, b) in ON_VECTOR:
                 nc.vector.tensor_tensor(
-                    out=rec_T[t, gate][:],
-                    in0=recT_ps[t, gate][:],
-                    in1=bias[:, blk0 : blk0 + BLOCKS_PER_GATE].unsqueeze(2).to_broadcast([P, BLOCKS_PER_GATE, P]),
+                    out=rec_T[pair, gate][:, 2 * b : 2 * b + 2, :],
+                    in0=recT_ps[pair, gate, b][:],
+                    in1=bias[:, blk : blk + 2].unsqueeze(2).to_broadcast([P, 2, 2 * P]),
                     op=ALU.add,
                 )
+            else:
+                for a in range(2):
+                    nc.scalar.activation(
+                        out=rec_T[pair, gate][:, 2 * b + a, :],
+                        in_=recT_ps[pair, gate, b][:, a, :],
+                        func=ACT.Identity,
+                        bias=bias[:, blk + a : blk + a + 1],
+                    )
 
         def input_pass(n, e):
             t, gate = steps[n]
@@ -278,7 +285,7 @@ def tile_nodelstmcell_pa_t_kernel(tc, x_t, h, c, W_ih, W_hh, b_ih, b_hh, out_0, 
             for a in range(2 * half, 2 * half + 2):
                 nc.tensor.matmul(
                     out=gate_ps[n][:, a * P : (a + 1) * P],
-                    lhsT=rec_T[t, gate][:, a, :],
+                    lhsT=rec_T[t // 2, gate][:, a, (t % 2) * P : (t % 2 + 1) * P],
                     rhs=ident_f32[:],
                     is_transpose=True,
                     start=False,
@@ -307,17 +314,17 @@ def tile_nodelstmcell_pa_t_kernel(tc, x_t, h, c, W_ih, W_hh, b_ih, b_hh, out_0, 
 
         def keep_old_cell(t):
             s, j = divmod(t, TILES)
-            keep = acts[t, GATE_F]
-            nc.gpsimd.tensor_tensor(out=keep[:], in0=keep[:], in1=c_in[s][:, j * HID : (j + 1) * HID], op=ALU.mult)
+            kept[t] = work.tile([P, HID], F32, name="kept", tag="kept", bufs=PROD_BUFS)
+            nc.gpsimd.tensor_tensor(out=kept[t][:], in0=acts[t, GATE_F][:], in1=c_in[s][:, j * HID : (j + 1) * HID], op=ALU.mult)
 
         def write_candidate(t):
-            write = acts[t, GATE_I]
-            nc.gpsimd.tensor_tensor(out=write[:], in0=write[:], in1=acts[t, GATE_G][:], op=ALU.mult)
+            written[t] = work.tile([P, HID], F32, name="written", tag="written", bufs=PROD_BUFS)
+            nc.gpsimd.tensor_tensor(out=written[t][:], in0=acts[t, GATE_I][:], in1=acts[t, GATE_G][:], op=ALU.mult)
 
         def new_cell(t):
             s, j = divmod(t, TILES)
             c_new[t] = work.tile([P, HID], F32, name="c_new", tag="c_new")
-            nc.vector.tensor_tensor(out=c_new[t][:], in0=acts[t, GATE_F][:], in1=acts[t, GATE_I][:], op=ALU.add)
+            nc.vector.tensor_tensor(out=c_new[t][:], in0=kept[t][:], in1=written[t][:], op=ALU.add)
             nc.sync.dma_start(out=c_next_rows[s, j], in_=c_new[t][:])
 
         def tanh_of_new_cell(t):
@@ -351,26 +358,28 @@ def tile_nodelstmcell_pa_t_kernel(tc, x_t, h, c, W_ih, W_hh, b_ih, b_hh, out_0, 
                 put(n + 1.55, add_recurrent, n)
             put(n + ACT_LAG, activate, n)
         for t in range(2, N_TILES):
-            if t < N_HEAD:
-                k = t - 2
+            if t < N_HEAD + ROWS_AHEAD:
+                k = min(t - 2, head - 1)
                 put(k + 0.45, transpose_rows, t)
                 put(k + 0.6, copy_rows, t)
                 put(k + 0.7, quantise_rows, t)
-            elif t < N_HEAD + ROWS_AHEAD:
-                k = head - 2 - (N_HEAD + ROWS_AHEAD - t) * 2
-                put(k + 0.45, transpose_rows, t)
-                put(k + 1.45, copy_rows, t)
-                put(k + 1.75, quantise_rows, t)
             else:
                 k = at[t - ROWS_AHEAD, ROW_GATE]
                 put(k + ROW_POS, transpose_rows, t)
                 put(k + ROW_COPY, copy_rows, t)
                 put(k + ROW_QUANT, quantise_rows, t)
-        for n, (t, gate) in enumerate(steps):
-            if turned_gate(t, gate):
-                k = n - (T_HEAD if t < N_HEAD else T_LAG)
-                put(k + 0.42, turned_blocks, t, gate)
-                put(k + T_COPY, copy_turned_blocks, t, gate)
+        for pair in range(N_TILES // 2):
+            for gate in GATE_ORDER:
+                if turned_gate(2 * pair, gate):
+                    for b in range(2):
+                        if pair == 0:
+                            k = at[0, gate] - T_HEAD
+                        elif gate == GATE_G:
+                            k = max(at[2 * pair - 2 + b, TB1], at[0, gate])
+                        else:
+                            k = max(at[2 * pair - 1 + b, TB2], at[0, gate])
+                        put(k + 0.42, turned_bank, pair, gate, b)
+                        put(k + T_COPY, copy_turned_bank, pair, gate, b)
         for q in range(1, GATES):
             gate = HEAD_ORDER[q]
             k = at[0, gate] - W_LEAD
@@ -382,21 +391,25 @@ def tile_nodelstmcell_pa_t_kernel(tc, x_t, h, c, W_ih, W_hh, b_ih, b_hh, out_0, 
             put(k + 2 * dd + 0.43, weights_ih, gate)
             put(k + 2 * dd + 0.65, copy_weights_ih, gate)
             put(k + dd + 0.9, weights_quantise, gate)
+        def lag(t, full, least):
+            return min(full, least + TAPER * (N_TILES - 1 - t))
+
         for t in range(N_TILES):
-            short = t >= N_TILES - SHORT
             b = max(at[t, GATE_I], at[t, GATE_G], at[t, GATE_F])
-            k_key = at[t, GATE_F] + (2.9 if short else K_LAG)
-            w_key = max(at[t, GATE_I], at[t, GATE_G]) + (2.9 if short else W_LAG)
-            c_key = b + (3.6 if short else C_LAG)
-            assert c_key > max(k_key, w_key)
+            k_key = at[t, GATE_F] + lag(t, K_LAG, 2.9)
+            w_key = max(at[t, GATE_I], at[t, GATE_G]) + lag(t, W_LAG, 2.9)
+            c_key = b + lag(t, C_LAG, 3.6)
+            tanh_key = b + lag(t, TANH_LAG, 4.45)
+            h_key = max(b + lag(t, H_LAG, 4.6), at[t, GATE_O] + ACT_LAG + 0.1)
+            assert c_key > max(k_key, w_key) and tanh_key > c_key and h_key > tanh_key
             assert k_key > at[t, GATE_F] + ACT_LAG and w_key > max(at[t, GATE_I], at[t, GATE_G]) + ACT_LAG
             put(k_key, keep_old_cell, t)
             put(w_key, write_candidate, t)
+            put(h_key, new_hidden, t)
             put(c_key, new_cell, t)
-            put(b + (4.58 if short else TANH_LAG), tanh_of_new_cell, t)
-            put(max(b + (4.9 if short else H_LAG), at[t, GATE_O] + ACT_LAG + 0.1), new_hidden, t)
-        put(4, load_h, 3)
-        put(4, load_x, 3)
+            put(tanh_key, tanh_of_new_cell, t)
+        put(2.9, load_h, 3)
+        put(2.9, load_x, 3)
         for s in range(1, N_GROUPS):
             k = at[TILES * s, GATE_F] if TILES * s >= N_HEAD else head
             if s + 3 < N_GROUPS:
@@ -406,9 +419,10 @@ def tile_nodelstmcell_pa_t_kernel(tc, x_t, h, c, W_ih, W_hh, b_ih, b_hh, out_0, 
                 put(k - 0.01, load_cell, s + 1)
 
         bias_rows = const.tile([P, P], BF16)
-        nc.vector.memset(bias_rows[:], 0.0)
-        nc.scalar.dma_start(out=bias_rows[0:BLOCKS, :], in_=b_ih.rearrange("(b n) -> b n", n=P))
-        nc.scalar.dma_start(out=bias_rows[BLOCKS : 2 * BLOCKS, :], in_=b_hh.rearrange("(b n) -> b n", n=P))
+        nc.vector.memset(bias_rows[2 * BLOCKS : 4 * BLOCKS, :], 0.0)
+        nc.vector.memset(bias_rows[4 * BLOCKS :, :], 0.0)
+        nc.sync.dma_start(out=bias_rows[0:BLOCKS, :], in_=b_ih.rearrange("(b n) -> b n", n=P))
+        nc.sync.dma_start(out=bias_rows[BLOCKS : 2 * BLOCKS, :], in_=b_hh.rearrange("(b n) -> b n", n=P))
         load_w_hh(HEAD_ORDER[0])
         load_h(0)
         load_w_ih(HEAD_ORDER[0])

@@ -42,34 +42,41 @@ K_LAG, W_LAG, C_LAG, TANH_LAG, H_LAG = 2.9, 2.9, 6.6, 9.58, 12.9
 H_G = "none"
 W_LEAD, W_STEP = 3, 0
 TAPER = 1.0
-PROD_BUFS = 1
+PROD_BUFS = 2
+LASTV = 1
+LAST_PARTS = 2
+LAST_C = 3.6
+DUM1, DUM2 = 5, 2
+XV = "none"
+LAST_ORDER = GATE_ORDER
 
-H_LAG = 12.52
-T_COPY = 0.8
-HEAD_ORDER = (GATE_G, GATE_F, GATE_I, GATE_O)
-W_LAG = 2.9
-TANH_LAG = 11.45
+T_COPY = 0.56
+HEAD_ORDER = (GATE_G, GATE_O, GATE_F, GATE_I)
+W_LAG = 4.9
+TANH_LAG = 2.08
 W_STEP = 0
 W_LEAD = 5
-K_LAG = 3.9
-ACT_LAG = 2.45
-C_LAG = 6.6
-T_HEAD = 2
-ROW_GATE = GATE_O
-ROW_POS = 0.15
-ROW_QUANT = 1.92
-ROW_COPY = 0.56
+K_LAG = 4.9
+ACT_LAG = 2.55
+C_LAG = 5.4
+T_HEAD = 1
+ROW_GATE = GATE_I
+ROW_POS = 0.45
+ROW_COPY = 1.56
 N_HEAD = 2
-H_G = "none"
-K2_GATE = GATE_O
-K2 = "all"
-GATE_ORDER = (GATE_F, GATE_G, GATE_I, GATE_O)
-ON_VECTOR = ((GATE_G, 1),)
-TAPER = 99
-PROD_BUFS = 1
-ROWS_AHEAD = 4
+GATE_ORDER = (GATE_O, GATE_F, GATE_G, GATE_I)
+ON_VECTOR = ((GATE_G, 0), (GATE_G, 1), (GATE_O, 1))
+PROD_BUFS = 2
+ROWS_AHEAD = 5
 TB2 = GATE_G
-TB1 = GATE_O
+TB1 = GATE_F
+LASTV = 1
+XV = "none"
+LAST_ORDER = (GATE_O, GATE_I, GATE_F, GATE_G)
+LAST_C = 3.6
+LAST_PARTS = 2
+K2 = "all"
+K2_GATE = GATE_I
 FLOPS = 2 * BATCH * GATES * HID * (IN_DIM + HID)
 
 
@@ -91,7 +98,7 @@ def tile_nodelstmcell_pa_t_kernel(tc, x_t, h, c, W_ih, W_hh, b_ih, b_hh, out_0, 
     c_next_rows = out_1.rearrange("(s p j) n -> s j p n", p=P, j=TILES)
 
     steps = [(t, gate) for gate in HEAD_ORDER for t in range(N_HEAD)]
-    steps += [(t, gate) for t in range(N_HEAD, N_TILES) for gate in GATE_ORDER]
+    steps += [(t, gate) for t in range(N_HEAD, N_TILES) for gate in (LAST_ORDER if t == N_TILES - 1 else GATE_ORDER)]
     at = {step: n for n, step in enumerate(steps)}
     n_steps = len(steps)
 
@@ -115,15 +122,19 @@ def tile_nodelstmcell_pa_t_kernel(tc, x_t, h, c, W_ih, W_hh, b_ih, b_hh, out_0, 
         rec_ps = {}
         acts = {}
         kept, written = {}, {}
-        c_new, tanh_c = {}, {}
+        c_new, tanh_c, h_new = {}, {}, {}
 
-        def load_h(s):
-            h_in[s] = rows.tile([P, TILES * HID], BF16, name="h_in", tag="h_in")
-            nc.sync.dma_start(out=h_in[s][:], in_=h_rows[s])
+        def load_h(s, tiles=range(TILES)):
+            if s not in h_in:
+                h_in[s] = rows.tile([P, TILES * HID], BF16, name="h_in", tag="h_in")
+            cols = slice(tiles[0] * HID, (tiles[-1] + 1) * HID)
+            nc.sync.dma_start(out=h_in[s][:, cols], in_=h_rows[s][:, cols])
 
-        def load_x(s):
-            x_in[s] = rows.tile([P, TILES * IN_DIM], BF16, name="x_in", tag="x_in")
-            nc.sync.dma_start(out=x_in[s][:], in_=x_rows[s])
+        def load_x(s, tiles=range(TILES)):
+            if s not in x_in:
+                x_in[s] = rows.tile([P, TILES * IN_DIM], BF16, name="x_in", tag="x_in")
+            cols = slice(tiles[0] * IN_DIM, (tiles[-1] + 1) * IN_DIM)
+            nc.sync.dma_start(out=x_in[s][:, cols], in_=x_rows[s][:, cols])
 
         def load_cell(s):
             c_in[s] = rows.tile([P, TILES * HID], BF16, name="c_in", tag="c_in")
@@ -131,11 +142,13 @@ def tile_nodelstmcell_pa_t_kernel(tc, x_t, h, c, W_ih, W_hh, b_ih, b_hh, out_0, 
 
         w_hh_raw, w_ih_raw = {}, {}
 
-        def load_w_hh(gate):
+        def load_w_hh(gate, halves=1):
             w_hh_raw[gate] = setup.tile([P, BLOCKS_PER_GATE, HID], BF16, name="w_hh_raw", tag="w_hh_raw")
-            nc.sync.dma_start(
-                out=w_hh_raw[gate][:], in_=W_hh[gate * HID : (gate + 1) * HID, :].rearrange("(a p) k -> p a k", p=P)
-            )
+            source = W_hh[gate * HID : (gate + 1) * HID, :].rearrange("(a p) k -> p a k", p=P)
+            n_blocks = BLOCKS_PER_GATE // halves
+            for i in range(halves):
+                blocks = slice(i * n_blocks, (i + 1) * n_blocks)
+                nc.sync.dma_start(out=w_hh_raw[gate][:, blocks, :], in_=source[:, blocks, :])
 
         def load_w_ih(gate):
             w_ih_raw[gate] = setup.tile([P, BLOCKS_PER_GATE, IN_DIM], BF16, name="w_ih_raw", tag="w_ih_raw")
@@ -202,7 +215,7 @@ def tile_nodelstmcell_pa_t_kernel(tc, x_t, h, c, W_ih, W_hh, b_ih, b_hh, out_0, 
                 in_=words_ps[t][:, 0:H_WORDS].rearrange("p (u r) -> p r u", u=H_HALVES),
             )
             x_T[t] = operands.tile([P, X_WORDS], F32, name="x_T", tag="x_T", bufs=ROWS_AHEAD + 4)
-            nc.scalar.copy(out=x_T[t][:], in_=words_ps[t][:, H_WORDS:])
+            (nc.vector.tensor_copy if chosen(XV, t) else nc.scalar.copy)(out=x_T[t][:], in_=words_ps[t][:, H_WORDS:])
 
         def quantise_rows(t):
             s, j = divmod(t, TILES)
@@ -312,32 +325,50 @@ def tile_nodelstmcell_pa_t_kernel(tc, x_t, h, c, W_ih, W_hh, b_ih, b_hh, out_0, 
             else:
                 nc.scalar.activation(out=acts[t, gate][:], in_=acts[t, gate][:], func=func)
 
-        def keep_old_cell(t):
+        def half(i, parts):
+            return slice(i * HID // parts, (i + 1) * HID // parts)
+
+        def keep_old_cell(t, engine):
             s, j = divmod(t, TILES)
             kept[t] = work.tile([P, HID], F32, name="kept", tag="kept", bufs=PROD_BUFS)
-            nc.gpsimd.tensor_tensor(out=kept[t][:], in0=acts[t, GATE_F][:], in1=c_in[s][:, j * HID : (j + 1) * HID], op=ALU.mult)
+            engine.tensor_tensor(
+                out=kept[t][:], in0=acts[t, GATE_F][:], in1=c_in[s][:, j * HID : (j + 1) * HID], op=ALU.mult
+            )
 
-        def write_candidate(t):
-            written[t] = work.tile([P, HID], F32, name="written", tag="written", bufs=PROD_BUFS)
-            nc.gpsimd.tensor_tensor(out=written[t][:], in0=acts[t, GATE_I][:], in1=acts[t, GATE_G][:], op=ALU.mult)
+        def write_candidate(t, engine, i=0, parts=1):
+            if i == 0:
+                written[t] = work.tile([P, HID], F32, name="written", tag="written", bufs=PROD_BUFS)
+            cols = half(i, parts)
+            engine.tensor_tensor(
+                out=written[t][:, cols], in0=acts[t, GATE_I][:, cols], in1=acts[t, GATE_G][:, cols], op=ALU.mult
+            )
 
-        def new_cell(t):
+        def new_cell(t, i=0, parts=1):
             s, j = divmod(t, TILES)
-            c_new[t] = work.tile([P, HID], F32, name="c_new", tag="c_new")
-            nc.vector.tensor_tensor(out=c_new[t][:], in0=kept[t][:], in1=written[t][:], op=ALU.add)
-            nc.sync.dma_start(out=c_next_rows[s, j], in_=c_new[t][:])
+            if i == 0:
+                c_new[t] = work.tile([P, HID], F32, name="c_new", tag="c_new")
+            cols = half(i, parts)
+            nc.vector.tensor_tensor(out=c_new[t][:, cols], in0=kept[t][:, cols], in1=written[t][:, cols], op=ALU.add)
+            nc.sync.dma_start(out=c_next_rows[s, j][:, cols], in_=c_new[t][:, cols])
 
-        def tanh_of_new_cell(t):
-            tanh_c[t] = work.tile([P, HID], F32, name="tanh_c", tag="tanh_c")
-            nc.scalar.activation(out=tanh_c[t][:], in_=c_new[t][:], func=ACT.Tanh)
+        def tanh_of_new_cell(t, i=0, parts=1):
+            if i == 0:
+                tanh_c[t] = work.tile([P, HID], F32, name="tanh_c", tag="tanh_c")
+            cols = half(i, parts)
+            nc.scalar.activation(out=tanh_c[t][:, cols], in_=c_new[t][:, cols], func=ACT.Tanh)
 
-        def new_hidden(t):
+        def new_hidden(t, i=0, parts=1):
             s, j = divmod(t, TILES)
-            h_new = work.tile([P, HID], F32, tag="h_new")
-            (nc.gpsimd if chosen(H_G, t) else nc.vector).tensor_tensor(out=h_new[:], in0=acts[t, GATE_O][:], in1=tanh_c[t][:], op=ALU.mult)
-            nc.sync.dma_start(out=h_next_rows[s, j], in_=h_new[:])
+            if i == 0:
+                h_new[t] = work.tile([P, HID], F32, name="h_new", tag="h_new")
+            cols = half(i, parts)
+            (nc.gpsimd if chosen(H_G, t) else nc.vector).tensor_tensor(
+                out=h_new[t][:, cols], in0=acts[t, GATE_O][:, cols], in1=tanh_c[t][:, cols], op=ALU.mult
+            )
+            nc.sync.dma_start(out=h_next_rows[s, j][:, cols], in_=h_new[t][:, cols])
 
         plan = []
+        waiting = []
 
         def put(key, fn, *args):
             plan.append((key, fn, args))
@@ -351,7 +382,7 @@ def tile_nodelstmcell_pa_t_kernel(tc, x_t, h, c, W_ih, W_hh, b_ih, b_hh, out_0, 
             put(n + 0.3, input_pass, n, 1)
             if turned(n):
                 put(n + 1.1, add_turned, n, 0)
-                put(n + 1.4, add_turned, n, 1)
+                put(n + (1.101 if n == n_steps - 2 else 1.4), add_turned, n, 1)
             else:
                 put(n + 1.05 if turned(n - 1) else n + 0.1, recurrent_rows, n)
                 put(n + 0.5, add_bias, n)
@@ -367,7 +398,7 @@ def tile_nodelstmcell_pa_t_kernel(tc, x_t, h, c, W_ih, W_hh, b_ih, b_hh, out_0, 
                 k = at[t - ROWS_AHEAD, ROW_GATE]
                 put(k + ROW_POS, transpose_rows, t)
                 put(k + ROW_COPY, copy_rows, t)
-                put(k + ROW_QUANT, quantise_rows, t)
+                waiting.append((k + ROW_COPY, t))
         for pair in range(N_TILES // 2):
             for gate in GATE_ORDER:
                 if turned_gate(2 * pair, gate):
@@ -391,23 +422,27 @@ def tile_nodelstmcell_pa_t_kernel(tc, x_t, h, c, W_ih, W_hh, b_ih, b_hh, out_0, 
             put(k + 2 * dd + 0.43, weights_ih, gate)
             put(k + 2 * dd + 0.65, copy_weights_ih, gate)
             put(k + dd + 0.9, weights_quantise, gate)
-        def lag(t, full, least):
-            return min(full, least + TAPER * (N_TILES - 1 - t))
-
         for t in range(N_TILES):
+            last = t == N_TILES - 1
             b = max(at[t, GATE_I], at[t, GATE_G], at[t, GATE_F])
-            k_key = at[t, GATE_F] + lag(t, K_LAG, 2.9)
-            w_key = max(at[t, GATE_I], at[t, GATE_G]) + lag(t, W_LAG, 2.9)
-            c_key = b + lag(t, C_LAG, 3.6)
-            tanh_key = b + lag(t, TANH_LAG, 4.45)
-            h_key = max(b + lag(t, H_LAG, 4.6), at[t, GATE_O] + ACT_LAG + 0.1)
-            assert c_key > max(k_key, w_key) and tanh_key > c_key and h_key > tanh_key
-            assert k_key > at[t, GATE_F] + ACT_LAG and w_key > max(at[t, GATE_I], at[t, GATE_G]) + ACT_LAG
-            put(k_key, keep_old_cell, t)
-            put(w_key, write_candidate, t)
-            put(h_key, new_hidden, t)
-            put(c_key, new_cell, t)
-            put(tanh_key, tanh_of_new_cell, t)
+            c_key = b + (LAST_C if last else C_LAG)
+            k_key = min(at[t, GATE_F] + K_LAG, c_key - 0.1)
+            w_key = min(max(at[t, GATE_I], at[t, GATE_G]) + W_LAG, c_key - 0.05)
+            tanh_key = c_key + (1.0 if last else TANH_LAG)
+            parts = LAST_PARTS if last else 1
+            products = nc.vector if t >= N_TILES - LASTV else nc.gpsimd
+            put(k_key, keep_old_cell, t, products)
+            while waiting and waiting[0][0] < c_key - 0.2:
+                put(c_key - 0.02, quantise_rows, waiting.pop(0)[1])
+            if t > 0:
+                put(max(c_key - 0.01, tanh_before + 0.3, at[t - 1, GATE_O] + ACT_LAG + 0.1), new_hidden, t - 1)
+            tanh_before = tanh_key
+            for i in range(parts):
+                put(w_key + 0.001 * i, write_candidate, t, products, i, parts)
+                put(c_key + 0.001 * i, new_cell, t, i, parts)
+                put(tanh_key + 0.001 * i, tanh_of_new_cell, t, i, parts)
+                if last:
+                    put(max(tanh_key, at[t, GATE_O] + ACT_LAG) + 0.5 + 0.001 * i, new_hidden, t, i, parts)
         put(2.9, load_h, 3)
         put(2.9, load_x, 3)
         for s in range(1, N_GROUPS):
@@ -423,12 +458,14 @@ def tile_nodelstmcell_pa_t_kernel(tc, x_t, h, c, W_ih, W_hh, b_ih, b_hh, out_0, 
         nc.vector.memset(bias_rows[4 * BLOCKS :, :], 0.0)
         nc.sync.dma_start(out=bias_rows[0:BLOCKS, :], in_=b_ih.rearrange("(b n) -> b n", n=P))
         nc.sync.dma_start(out=bias_rows[BLOCKS : 2 * BLOCKS, :], in_=b_hh.rearrange("(b n) -> b n", n=P))
-        load_w_hh(HEAD_ORDER[0])
-        load_h(0)
+        load_w_hh(HEAD_ORDER[0], 2)
         load_w_ih(HEAD_ORDER[0])
-        load_x(0)
+        load_h(0, range(0, 2))
+        load_x(0, range(0, 2))
         load_w_hh(HEAD_ORDER[1])
         load_w_ih(HEAD_ORDER[1])
+        load_h(0, range(2, 4))
+        load_x(0, range(2, 4))
         load_w_hh(HEAD_ORDER[2])
         load_w_ih(HEAD_ORDER[2])
         load_cell(0)
@@ -452,6 +489,17 @@ def tile_nodelstmcell_pa_t_kernel(tc, x_t, h, c, W_ih, W_hh, b_ih, b_hh, out_0, 
         w_scales = const.tile([P, GATES * HID], U8, align_bytes=64)
         w_ih_T = const.tile([P, PAIR, GATES * HID], BF16)
 
+        zeros = const.tile([P, HID], BF16)
+        nc.gpsimd.memset(zeros[:], 0.0)
+
+        def warm_up(n):
+            warm_ps = psum.tile([P, HID], F32, name="warm_ps", tag="gate")
+            for i in range(n):
+                nc.tensor.matmul(out=warm_ps[:], lhsT=zeros[:, 0:P], rhs=zeros[:], start=(i == 0), stop=(i == n - 1))
+
+        if DUM1:
+            warm_up(DUM1)
+
         biasT_ps = psum.tile([P, P], BF16, tag="copied_out")
         nc.tensor.transpose(biasT_ps[:], bias_rows[:], ident_bf16[:])
         bias_pair = const.tile([P, 2 * BLOCKS], F32)
@@ -464,6 +512,8 @@ def tile_nodelstmcell_pa_t_kernel(tc, x_t, h, c, W_ih, W_hh, b_ih, b_hh, out_0, 
         weights_hh_half(HEAD_ORDER[0], 1)
         copy_weights_hh_half(HEAD_ORDER[0], 1, nc.scalar.copy)
         weights_quantise(HEAD_ORDER[0])
+        if DUM2:
+            warm_up(DUM2)
         weights_ih(HEAD_ORDER[0])
         copy_weights_ih(HEAD_ORDER[0])
         for t in range(2):

@@ -30,12 +30,15 @@ PACK = 4
 HEAD_ORDER = (GATE_F, GATE_I, GATE_G, GATE_O)
 N_HEAD = 2
 ROWS_AHEAD = 4
-ROW_POS, ROW_COPY, ROW_QUANT = 0.45, 1.45, 2.9
+ROW_K = (0.05, 0.35, 0.47)
+ROW_COPY = 1.45
+TBK = (0.12, 0.44)
 ROW_GATE = GATE_I
 T_COPY = 0.8
 T_HEAD = 1
 K2_GATE, K2 = GATE_O, "all"
-ON_VECTOR = ((GATE_O, 1),)
+ON_VECTOR = ((GATE_G, 0, 0), (GATE_G, 0, 1))
+HH_V, IH_V, SP_V = False, False, True
 TB1, TB2 = GATE_O, GATE_G
 ACT_LAG = 2.5
 K_LAG, W_LAG, C_LAG, TANH_LAG, H_LAG = 2.9, 2.9, 6.6, 9.58, 12.9
@@ -47,36 +50,45 @@ LASTV = 1
 LAST_PARTS = 2
 LAST_C = 3.6
 DUM1, DUM2 = 5, 2
+MERGE = 1
+TAG_G, TAG_C, BUF_G, BUF_C = "gate", "copied_out", 4, 4
+ADDED = (GATE_F, GATE_O)
 XV = "none"
 LAST_ORDER = GATE_ORDER
 
-T_COPY = 0.56
-HEAD_ORDER = (GATE_G, GATE_O, GATE_F, GATE_I)
+T_COPY = 1.56
+HEAD_ORDER = (GATE_I, GATE_F, GATE_O, GATE_G)
 W_LAG = 4.9
 TANH_LAG = 2.08
 W_STEP = 0
 W_LEAD = 5
-K_LAG = 4.9
-ACT_LAG = 2.55
-C_LAG = 5.4
-T_HEAD = 1
-ROW_GATE = GATE_I
-ROW_POS = 0.45
-ROW_COPY = 1.56
+K_LAG = 2.9
+ACT_LAG = 1.9
+C_LAG = 4.57
+T_HEAD = 2
+ROW_GATE = GATE_F
+ROW_COPY = 1.9
 N_HEAD = 2
-GATE_ORDER = (GATE_O, GATE_F, GATE_G, GATE_I)
-ON_VECTOR = ((GATE_G, 0), (GATE_G, 1), (GATE_O, 1))
+GATE_ORDER = (GATE_F, GATE_O, GATE_I, GATE_G)
+ON_VECTOR = ((GATE_G, 1, 0), (GATE_G, 1, 1))
 PROD_BUFS = 2
-ROWS_AHEAD = 5
-TB2 = GATE_G
-TB1 = GATE_F
+ROWS_AHEAD = 4
+TB2 = GATE_O
+TB1 = GATE_O
 LASTV = 1
-XV = "none"
-LAST_ORDER = (GATE_O, GATE_I, GATE_F, GATE_G)
-LAST_C = 3.6
+XV = "even"
+LAST_ORDER = (GATE_O, GATE_F, GATE_I, GATE_G)
+LAST_C = 4.6
 LAST_PARTS = 2
 K2 = "all"
 K2_GATE = GATE_I
+HH_V = True
+IH_V = True
+SP_V = True
+ROW_K = (0.05, 0.35, 0.36)
+TBK = (0.42, 0.421)
+MERGE = 2
+TAG_G, TAG_C, BUF_G, BUF_C = "bank", "bank", 8, 8
 FLOPS = 2 * BATCH * GATES * HID * (IN_DIM + HID)
 
 
@@ -108,7 +120,7 @@ def tile_nodelstmcell_pa_t_kernel(tc, x_t, h, c, W_ih, W_hh, b_ih, b_hh, out_0, 
         rows = stack.enter_context(tc.tile_pool(name="rows", bufs=3))
         operands = stack.enter_context(tc.tile_pool(name="operands", bufs=3))
         work = stack.enter_context(tc.tile_pool(name="work", bufs=4))
-        psum = stack.enter_context(tc.psum_pool(name="psum", bufs=4))
+        psum = stack.enter_context(tc.psum_pool(name="psum", bufs=1))
         stack.enter_context(tc.manual_schedule())
 
         x_in, h_in, c_in = {}, {}, {}
@@ -120,6 +132,7 @@ def tile_nodelstmcell_pa_t_kernel(tc, x_t, h, c, W_ih, W_hh, b_ih, b_hh, out_0, 
         recT_ps = {}
         gate_ps = {}
         rec_ps = {}
+        sums = {}
         acts = {}
         kept, written = {}, {}
         c_new, tanh_c, h_new = {}, {}, {}
@@ -163,7 +176,7 @@ def tile_nodelstmcell_pa_t_kernel(tc, x_t, h, c, W_ih, W_hh, b_ih, b_hh, out_0, 
                 w_grouped[gate] = setup.tile(
                     [P, HID * PACK], BF16, name="w_grouped", tag="w_grouped", bufs=2, align_bytes=64
                 )
-            wT_ps = psum.tile([P, 2, H_HALVES, P], F32, name="wT_ps", tag="copied_out")
+            wT_ps = psum.tile([P, 2, H_HALVES, P], F32, name="wT_ps", tag=TAG_C, bufs=BUF_C)
             for a in range(2):
                 raw_words = w_hh_raw[gate][:, 2 * half + a, :].bitcast(F32)
                 for u in range(H_HALVES):
@@ -184,7 +197,7 @@ def tile_nodelstmcell_pa_t_kernel(tc, x_t, h, c, W_ih, W_hh, b_ih, b_hh, out_0, 
             nc.vector.quantize_mx(out=w_codes[:, cols].bitcast(FP8X4), scales=w_scales[:, cols], in_=w_grouped[gate][:])
 
         def weights_ih(gate):
-            wT_ps = psum.tile([P, HID], F32, name="wihT_ps", tag="copied_out")
+            wT_ps = psum.tile([P, HID], F32, name="wihT_ps", tag=TAG_C, bufs=BUF_C)
             for a in range(BLOCKS_PER_GATE):
                 nc.tensor.transpose(wT_ps[:, a * P : (a + 1) * P], w_ih_raw[gate][:, a, :].bitcast(F32), ident_f32[:])
             weights_ps[gate, 2] = wT_ps
@@ -193,20 +206,29 @@ def tile_nodelstmcell_pa_t_kernel(tc, x_t, h, c, W_ih, W_hh, b_ih, b_hh, out_0, 
             cols = slice(gate * HID, (gate + 1) * HID)
             halves = weights_ps[gate, 2][:].bitcast(BF16).rearrange("p (n e) -> p e n", e=PAIR)
             nc.scalar.copy(out=w_ih_T[:, 0, cols], in_=halves[:, 0, :])
-            nc.vector.tensor_copy(out=w_ih_T[:, 1, cols], in_=halves[:, 1, :])
+            (nc.vector.tensor_copy if IH_V or gate == HEAD_ORDER[0] else nc.scalar.copy)(
+                out=w_ih_T[:, 1, cols], in_=halves[:, 1, :]
+            )
 
-        def transpose_rows(t):
+        def transpose_h(t, u):
             s, j = divmod(t, TILES)
-            words_ps[t] = psum.tile([P, H_WORDS + X_WORDS], F32, name="words_ps", tag="copied_out")
-            h_words = h_in[s][:].bitcast(F32)
-            for u in range(H_HALVES):
-                nc.tensor.transpose(
-                    words_ps[t][:, u * P : (u + 1) * P],
-                    h_words[:, j * H_WORDS + u : (j + 1) * H_WORDS : H_HALVES],
-                    ident_f32[:],
-                )
+            if u == 0:
+                words_ps[t] = psum.tile([P, H_WORDS + X_WORDS], F32, name="words_ps", tag=TAG_C, bufs=BUF_C)
+            nc.tensor.transpose(
+                words_ps[t][:, u * P : (u + 1) * P],
+                h_in[s][:].bitcast(F32)[:, j * H_WORDS + u : (j + 1) * H_WORDS : H_HALVES],
+                ident_f32[:],
+            )
+
+        def transpose_x(t):
+            s, j = divmod(t, TILES)
             x_words = x_in[s][:].bitcast(F32)
             nc.tensor.transpose(words_ps[t][:, H_WORDS:], x_words[:, j * X_WORDS : (j + 1) * X_WORDS], ident_f32[:])
+
+        def transpose_rows(t):
+            for u in range(H_HALVES):
+                transpose_h(t, u)
+            transpose_x(t)
 
         def copy_rows(t):
             h_grouped[t] = work.tile([P, P * PACK], BF16, name="h_grouped", tag="h_grouped", align_bytes=64)
@@ -227,22 +249,22 @@ def tile_nodelstmcell_pa_t_kernel(tc, x_t, h, c, W_ih, W_hh, b_ih, b_hh, out_0, 
                 out=h_codes[s][:, cols].bitcast(FP8X4), scales=h_scales[s][:, cols], in_=h_grouped[t][:]
             )
 
-        def turned_bank(pair, gate, b):
+        def turned_block(pair, gate, b, a):
             s, j = divmod(2 * pair, TILES)
             rows2 = slice(j * P, (j + 2) * P)
-            recT_ps[pair, gate, b] = psum.tile([P, 2, 2 * P], F32, name="recT_ps", tag="copied_out")
-            for a in range(2):
-                blk = gate * BLOCKS_PER_GATE + 2 * b + a
-                cols = slice(blk * P, (blk + 1) * P)
-                nc.tensor.matmul_mx(
-                    out=recT_ps[pair, gate, b][:, a, :],
-                    lhsT=w_codes[:, cols].bitcast(FP8X4),
-                    lhsT_scale=w_scales[:, cols],
-                    rhs=h_codes[s][:, rows2].bitcast(FP8X4),
-                    rhs_scale=h_scales[s][:, rows2],
-                    start=True,
-                    stop=True,
-                )
+            if a == 0:
+                recT_ps[pair, gate, b] = psum.tile([P, 2, 2 * P], F32, name="recT_ps", tag=TAG_C, bufs=BUF_C)
+            blk = gate * BLOCKS_PER_GATE + 2 * b + a
+            cols = slice(blk * P, (blk + 1) * P)
+            nc.tensor.matmul_mx(
+                out=recT_ps[pair, gate, b][:, a, :],
+                lhsT=w_codes[:, cols].bitcast(FP8X4),
+                lhsT_scale=w_scales[:, cols],
+                rhs=h_codes[s][:, rows2].bitcast(FP8X4),
+                rhs_scale=h_scales[s][:, rows2],
+                start=True,
+                stop=True,
+            )
 
         def copy_turned_bank(pair, gate, b):
             if (pair, gate) not in rec_T:
@@ -250,7 +272,7 @@ def tile_nodelstmcell_pa_t_kernel(tc, x_t, h, c, W_ih, W_hh, b_ih, b_hh, out_0, 
                     [P, BLOCKS_PER_GATE, 2 * P], F32, name="rec_T", tag="rec_T%d" % gate, bufs=3
                 )
             blk = gate * BLOCKS_PER_GATE + 2 * b
-            if (gate, b) in ON_VECTOR:
+            if (gate, b, pair % 2) in ON_VECTOR:
                 nc.vector.tensor_tensor(
                     out=rec_T[pair, gate][:, 2 * b : 2 * b + 2, :],
                     in0=recT_ps[pair, gate, b][:],
@@ -269,7 +291,7 @@ def tile_nodelstmcell_pa_t_kernel(tc, x_t, h, c, W_ih, W_hh, b_ih, b_hh, out_0, 
         def input_pass(n, e):
             t, gate = steps[n]
             if e == 0:
-                gate_ps[n] = psum.tile([P, HID], F32, name="gate_ps", tag="gate")
+                gate_ps[n] = psum.tile([P, HID], F32, name="gate_ps", tag=TAG_G, bufs=BUF_G)
             nc.tensor.matmul(
                 out=gate_ps[n][:],
                 lhsT=x_T[t][:].bitcast(BF16)[:, e:IN_DIM:PAIR],
@@ -281,7 +303,7 @@ def tile_nodelstmcell_pa_t_kernel(tc, x_t, h, c, W_ih, W_hh, b_ih, b_hh, out_0, 
         def recurrent_rows(n):
             t, gate = steps[n]
             s, j = divmod(t, TILES)
-            rec_ps[n] = psum.tile([P, HID], F32, name="rec_ps", tag="copied_out")
+            rec_ps[n] = psum.tile([P, HID], F32, name="rec_ps", tag=TAG_C, bufs=BUF_C)
             nc.tensor.matmul_mx(
                 out=rec_ps[n][:],
                 lhsT=h_codes[s][:, j * P : (j + 1) * P].bitcast(FP8X4),
@@ -307,23 +329,28 @@ def tile_nodelstmcell_pa_t_kernel(tc, x_t, h, c, W_ih, W_hh, b_ih, b_hh, out_0, 
 
         def add_bias(n):
             t, gate = steps[n]
-            acts[t, gate] = work.tile([P, HID], F32, name="act%d" % gate, tag="act%d" % gate, bufs=6)
-            nc.vector.tensor_tensor(
-                out=acts[t, gate][:], in0=gate_ps[n][:], in1=bias_spread[:, gate, :], op=ALU.add
-            )
+            if t not in sums:
+                sums[t] = work.tile([P, 2, HID], F32, name="sums", tag="sums", bufs=6)
+            acts[t, gate] = sums[t][:, ADDED.index(gate), :]
+            nc.vector.tensor_tensor(out=acts[t, gate], in0=gate_ps[n][:], in1=bias_spread[:, gate, :], op=ALU.add)
 
         def add_recurrent(n):
             total = acts[steps[n]]
-            nc.vector.tensor_tensor(out=total[:], in0=rec_ps[n][:], in1=total[:], op=ALU.add)
+            nc.vector.tensor_tensor(out=total, in0=rec_ps[n][:], in1=total, op=ALU.add)
 
         def activate(n):
             t, gate = steps[n]
             func = ACT.Tanh if gate == GATE_G else ACT.Sigmoid
             if turned_gate(t, gate):
-                acts[t, gate] = work.tile([P, HID], F32, name="act%d" % gate, tag="act%d" % gate, bufs=6)
-                nc.scalar.activation(out=acts[t, gate][:], in_=gate_ps[n][:], func=func)
+                act = work.tile([P, HID], F32, name="act%d" % gate, tag="act%d" % gate, bufs=6)
+                nc.scalar.activation(out=act[:], in_=gate_ps[n][:], func=func)
+                acts[t, gate] = act[:]
             else:
-                nc.scalar.activation(out=acts[t, gate][:], in_=acts[t, gate][:], func=func)
+                nc.scalar.activation(out=acts[t, gate], in_=acts[t, gate], func=func)
+
+        def activate_both(t):
+            both = sums[t][:].rearrange("p g n -> p (g n)")
+            nc.scalar.activation(out=both, in_=both, func=ACT.Sigmoid)
 
         def half(i, parts):
             return slice(i * HID // parts, (i + 1) * HID // parts)
@@ -332,7 +359,7 @@ def tile_nodelstmcell_pa_t_kernel(tc, x_t, h, c, W_ih, W_hh, b_ih, b_hh, out_0, 
             s, j = divmod(t, TILES)
             kept[t] = work.tile([P, HID], F32, name="kept", tag="kept", bufs=PROD_BUFS)
             engine.tensor_tensor(
-                out=kept[t][:], in0=acts[t, GATE_F][:], in1=c_in[s][:, j * HID : (j + 1) * HID], op=ALU.mult
+                out=kept[t][:], in0=acts[t, GATE_F], in1=c_in[s][:, j * HID : (j + 1) * HID], op=ALU.mult
             )
 
         def write_candidate(t, engine, i=0, parts=1):
@@ -384,10 +411,14 @@ def tile_nodelstmcell_pa_t_kernel(tc, x_t, h, c, W_ih, W_hh, b_ih, b_hh, out_0, 
                 put(n + 1.1, add_turned, n, 0)
                 put(n + (1.101 if n == n_steps - 2 else 1.4), add_turned, n, 1)
             else:
-                put(n + 1.05 if turned(n - 1) else n + 0.1, recurrent_rows, n)
+                put(n + (1.05 if turned(n - 1) else 0.41 if turned(n - 2) and n > head else 0.1), recurrent_rows, n)
                 put(n + 0.5, add_bias, n)
                 put(n + 1.55, add_recurrent, n)
-            put(n + ACT_LAG, activate, n)
+            if MERGE and not turned(n) and t >= N_HEAD and not (MERGE == 2 and t == N_TILES - 1):
+                if n == max(at[t, gate2] for gate2 in ADDED):
+                    put(n + ACT_LAG, activate_both, t)
+            else:
+                put(n + ACT_LAG, activate, n)
         for t in range(2, N_TILES):
             if t < N_HEAD + ROWS_AHEAD:
                 k = min(t - 2, head - 1)
@@ -396,7 +427,9 @@ def tile_nodelstmcell_pa_t_kernel(tc, x_t, h, c, W_ih, W_hh, b_ih, b_hh, out_0, 
                 put(k + 0.7, quantise_rows, t)
             else:
                 k = at[t - ROWS_AHEAD, ROW_GATE]
-                put(k + ROW_POS, transpose_rows, t)
+                put(k + ROW_K[0], transpose_h, t, 0)
+                put(k + ROW_K[1], transpose_h, t, 1)
+                put(k + ROW_K[2], transpose_x, t)
                 put(k + ROW_COPY, copy_rows, t)
                 waiting.append((k + ROW_COPY, t))
         for pair in range(N_TILES // 2):
@@ -409,14 +442,16 @@ def tile_nodelstmcell_pa_t_kernel(tc, x_t, h, c, W_ih, W_hh, b_ih, b_hh, out_0, 
                             k = max(at[2 * pair - 2 + b, TB1], at[0, gate])
                         else:
                             k = max(at[2 * pair - 1 + b, TB2], at[0, gate])
-                        put(k + 0.42, turned_bank, pair, gate, b)
+                        early = pair == 0 or k < head
+                        put(k + (0.42 if early else TBK[0]), turned_block, pair, gate, b, 0)
+                        put(k + (0.421 if early else TBK[1]), turned_block, pair, gate, b, 1)
                         put(k + T_COPY, copy_turned_bank, pair, gate, b)
         for q in range(1, GATES):
             gate = HEAD_ORDER[q]
             k = at[0, gate] - W_LEAD
             dd = W_STEP
             put(k + 0.43, weights_hh_half, gate, 0)
-            put(k + 0.65, copy_weights_hh_half, gate, 0, nc.vector.tensor_copy)
+            put(k + 0.65, copy_weights_hh_half, gate, 0, nc.vector.tensor_copy if HH_V else nc.scalar.copy)
             put(k + dd + 0.43, weights_hh_half, gate, 1)
             put(k + dd + 0.65, copy_weights_hh_half, gate, 1, nc.scalar.copy)
             put(k + 2 * dd + 0.43, weights_ih, gate)
@@ -426,7 +461,11 @@ def tile_nodelstmcell_pa_t_kernel(tc, x_t, h, c, W_ih, W_hh, b_ih, b_hh, out_0, 
             last = t == N_TILES - 1
             b = max(at[t, GATE_I], at[t, GATE_G], at[t, GATE_F])
             c_key = b + (LAST_C if last else C_LAG)
-            k_key = min(at[t, GATE_F] + K_LAG, c_key - 0.1)
+            f_at = at[t, GATE_F]
+            if MERGE and t >= N_HEAD and not (MERGE == 2 and t == N_TILES - 1) and GATE_F in ADDED:
+                f_at = max(at[t, gate] for gate in ADDED)
+            k_key = min(f_at + K_LAG, c_key - 0.1)
+            assert k_key > f_at + ACT_LAG
             w_key = min(max(at[t, GATE_I], at[t, GATE_G]) + W_LAG, c_key - 0.05)
             tanh_key = c_key + (1.0 if last else TANH_LAG)
             parts = LAST_PARTS if last else 1
@@ -453,6 +492,8 @@ def tile_nodelstmcell_pa_t_kernel(tc, x_t, h, c, W_ih, W_hh, b_ih, b_hh, out_0, 
             if s + 1 < N_GROUPS:
                 put(k - 0.01, load_cell, s + 1)
 
+        zeros = const.tile([P, HID], BF16)
+        nc.vector.memset(zeros[:], 0.0)
         bias_rows = const.tile([P, P], BF16)
         nc.vector.memset(bias_rows[2 * BLOCKS : 4 * BLOCKS, :], 0.0)
         nc.vector.memset(bias_rows[4 * BLOCKS :, :], 0.0)
@@ -489,18 +530,16 @@ def tile_nodelstmcell_pa_t_kernel(tc, x_t, h, c, W_ih, W_hh, b_ih, b_hh, out_0, 
         w_scales = const.tile([P, GATES * HID], U8, align_bytes=64)
         w_ih_T = const.tile([P, PAIR, GATES * HID], BF16)
 
-        zeros = const.tile([P, HID], BF16)
-        nc.gpsimd.memset(zeros[:], 0.0)
 
         def warm_up(n):
-            warm_ps = psum.tile([P, HID], F32, name="warm_ps", tag="gate")
+            warm_ps = psum.tile([P, HID], F32, name="warm_ps", tag=TAG_G, bufs=BUF_G)
             for i in range(n):
                 nc.tensor.matmul(out=warm_ps[:], lhsT=zeros[:, 0:P], rhs=zeros[:], start=(i == 0), stop=(i == n - 1))
 
         if DUM1:
             warm_up(DUM1)
 
-        biasT_ps = psum.tile([P, P], BF16, tag="copied_out")
+        biasT_ps = psum.tile([P, P], BF16, tag=TAG_C, bufs=BUF_C)
         nc.tensor.transpose(biasT_ps[:], bias_rows[:], ident_bf16[:])
         bias_pair = const.tile([P, 2 * BLOCKS], F32)
         nc.vector.tensor_copy(out=bias_pair[:], in_=biasT_ps[:, 0 : 2 * BLOCKS])
@@ -524,16 +563,16 @@ def tile_nodelstmcell_pa_t_kernel(tc, x_t, h, c, W_ih, W_hh, b_ih, b_hh, out_0, 
         bias_spread = const.tile([P, GATES, HID], F32)
 
         def spread_bias(gate):
-            spread_ps = psum.tile([P, HID], F32, name="spread_ps", tag="gate")
+            spread_ps = psum.tile([P, HID], F32, name="spread_ps", tag=TAG_G, bufs=BUF_G)
             for a in range(BLOCKS_PER_GATE):
                 blk = gate * BLOCKS_PER_GATE + a
                 nc.tensor.transpose(
                     spread_ps[:, a * P : (a + 1) * P], bias[:, blk : blk + 1].to_broadcast([P, P]), ident_f32[:]
                 )
-            nc.vector.tensor_copy(out=bias_spread[:, gate, :], in_=spread_ps[:])
+            (nc.vector.tensor_copy if SP_V else nc.scalar.copy)(out=bias_spread[:, gate, :], in_=spread_ps[:])
 
         for gate in HEAD_ORDER:
-            if not (turned_gate(0, gate) and turned_gate(1, gate)):
+            if not all(turned_gate(t, gate) for t in range(TILES)):
                 spread_bias(gate)
 
         for key, fn, args in sorted(plan, key=lambda e: e[0]):

@@ -15,89 +15,32 @@ P = 128
 BATCH, IN_DIM, HID = 4096, 256, 512
 GATES = 4
 GATE_I, GATE_F, GATE_G, GATE_O = 0, 1, 2, 3
-GATE_ORDER = (GATE_F, GATE_G, GATE_I, GATE_O)
+ADDED = (GATE_F, GATE_O)
+TURNED = (GATE_I, GATE_G)
+TILE_ORDER = ADDED + TURNED
+HEAD_ORDER = (GATE_F, GATE_I, GATE_O, GATE_G)
+HEAD_TILES = 2
 TILES = 4
 GROUP_ROWS = TILES * P
 N_GROUPS = BATCH // GROUP_ROWS
 N_TILES = N_GROUPS * TILES
+PAIR_TILES = 2
+PAIR_ROWS = PAIR_TILES * P
+N_PAIRS = N_TILES // PAIR_TILES
 BLOCKS_PER_GATE = HID // P
 BLOCKS = GATES * BLOCKS_PER_GATE
-PAIR = 2
-H_WORDS = HID // PAIR
-X_WORDS = IN_DIM // PAIR
-H_HALVES = H_WORDS // P
+BANK_BLOCKS = 2
+BANKS_PER_GATE = BLOCKS_PER_GATE // BANK_BLOCKS
+HALVES = 2
+H_WORDS = HID // HALVES
+X_WORDS = IN_DIM // HALVES
+WORDS_PER_PACK = H_WORDS // P
 PACK = 4
-HEAD_ORDER = (GATE_F, GATE_I, GATE_G, GATE_O)
-N_HEAD = 2
 ROWS_AHEAD = 4
-ROW_K = (0.05, 0.35, 0.47)
-ROW_COPY = 1.45
-TBK = (0.12, 0.44)
-ROW_GATE = GATE_I
-T_COPY = 0.8
-T_HEAD = 1
-K2_GATE, K2 = GATE_O, "all"
-ON_VECTOR = ((GATE_G, 0, 0), (GATE_G, 0, 1))
-HH_V, IH_V, SP_V = False, False, True
-TB1, TB2 = GATE_O, GATE_G
-ACT_LAG = 2.5
-K_LAG, W_LAG, C_LAG, TANH_LAG, H_LAG = 2.9, 2.9, 6.6, 9.58, 12.9
-H_G = "none"
-W_LEAD, W_STEP = 3, 0
-TAPER = 1.0
-PROD_BUFS = 2
-LASTV = 1
-LAST_PARTS = 2
-LAST_C = 3.6
-DUM1, DUM2 = 5, 2
-MERGE = 1
-TAG_G, TAG_C, BUF_G, BUF_C = "gate", "copied_out", 4, 4
-ADDED = (GATE_F, GATE_O)
-XV = "none"
-LAST_ORDER = GATE_ORDER
+PSUM_BANKS = 8
+WARM_UP = 3
 
-T_COPY = 1.56
-HEAD_ORDER = (GATE_I, GATE_F, GATE_O, GATE_G)
-W_LAG = 4.9
-TANH_LAG = 2.08
-W_STEP = 0
-W_LEAD = 5
-K_LAG = 2.9
-ACT_LAG = 1.9
-C_LAG = 4.57
-T_HEAD = 2
-ROW_GATE = GATE_F
-ROW_COPY = 1.9
-N_HEAD = 2
-GATE_ORDER = (GATE_F, GATE_O, GATE_I, GATE_G)
-ON_VECTOR = ((GATE_G, 1, 0), (GATE_G, 1, 1))
-PROD_BUFS = 2
-ROWS_AHEAD = 4
-TB2 = GATE_O
-TB1 = GATE_O
-LASTV = 1
-XV = "even"
-LAST_ORDER = (GATE_O, GATE_F, GATE_I, GATE_G)
-LAST_C = 4.6
-LAST_PARTS = 2
-K2 = "all"
-K2_GATE = GATE_I
-HH_V = True
-IH_V = True
-SP_V = True
-ROW_K = (0.05, 0.35, 0.36)
-TBK = (0.42, 0.421)
-MERGE = 2
-TAG_G, TAG_C, BUF_G, BUF_C = "bank", "bank", 8, 8
 FLOPS = 2 * BATCH * GATES * HID * (IN_DIM + HID)
-
-
-def turned_gate(t, gate):
-    return gate == GATE_G or (gate == K2_GATE and (K2 == "all" or (K2 == "even" and t // 2 % 2 == 0)))
-
-
-def chosen(what, t):
-    return what == "all" or (what == "even" and t % 2 == 0) or (what == "third" and t % 3 == 0) or (what == "q" and t % 4 == 0)
 
 
 def tile_nodelstmcell_pa_t_kernel(tc, x_t, h, c, W_ih, W_hh, b_ih, b_hh, out_0, out_1):
@@ -109,18 +52,22 @@ def tile_nodelstmcell_pa_t_kernel(tc, x_t, h, c, W_ih, W_hh, b_ih, b_hh, out_0, 
     h_next_rows = out_0.rearrange("(s p j) n -> s j p n", p=P, j=TILES)
     c_next_rows = out_1.rearrange("(s p j) n -> s j p n", p=P, j=TILES)
 
-    steps = [(t, gate) for gate in HEAD_ORDER for t in range(N_HEAD)]
-    steps += [(t, gate) for t in range(N_HEAD, N_TILES) for gate in (LAST_ORDER if t == N_TILES - 1 else GATE_ORDER)]
-    at = {step: n for n, step in enumerate(steps)}
+    steps = [(t, gate) for gate in HEAD_ORDER for t in range(HEAD_TILES)]
+    n_head = len(steps)
+    steps += [(t, gate) for t in range(HEAD_TILES, N_TILES) for gate in TILE_ORDER]
     n_steps = len(steps)
+    at = {step: n for n, step in enumerate(steps)}
+
+    def is_step(n, gates):
+        return 0 <= n < n_steps and steps[n][1] in gates
 
     with ExitStack() as stack:
         const = stack.enter_context(tc.tile_pool(name="const", bufs=1))
-        setup = stack.enter_context(tc.tile_pool(name="setup", bufs=4))
+        setup = stack.enter_context(tc.tile_pool(name="setup", bufs=GATES))
         rows = stack.enter_context(tc.tile_pool(name="rows", bufs=3))
         operands = stack.enter_context(tc.tile_pool(name="operands", bufs=3))
         work = stack.enter_context(tc.tile_pool(name="work", bufs=4))
-        psum = stack.enter_context(tc.psum_pool(name="psum", bufs=1))
+        psum = stack.enter_context(tc.psum_pool(name="psum", bufs=PSUM_BANKS))
         stack.enter_context(tc.manual_schedule())
 
         x_in, h_in, c_in = {}, {}, {}
@@ -133,90 +80,85 @@ def tile_nodelstmcell_pa_t_kernel(tc, x_t, h, c, W_ih, W_hh, b_ih, b_hh, out_0, 
         gate_ps = {}
         rec_ps = {}
         sums = {}
-        acts = {}
+        turned_acts = {}
         kept, written = {}, {}
         c_new, tanh_c, h_new = {}, {}, {}
+        w_hh_raw, w_ih_raw, w_grouped, wT_ps = {}, {}, {}, {}
 
-        def load_h(s, tiles=range(TILES)):
+        def gate_of(t, gate):
+            return sums[t][:, ADDED.index(gate), :] if gate in ADDED else turned_acts[t, gate][:]
+
+        def load_h(s, first=0, last=TILES):
             if s not in h_in:
                 h_in[s] = rows.tile([P, TILES * HID], BF16, name="h_in", tag="h_in")
-            cols = slice(tiles[0] * HID, (tiles[-1] + 1) * HID)
+            cols = slice(first * HID, last * HID)
             nc.sync.dma_start(out=h_in[s][:, cols], in_=h_rows[s][:, cols])
 
-        def load_x(s, tiles=range(TILES)):
+        def load_x(s, first=0, last=TILES):
             if s not in x_in:
                 x_in[s] = rows.tile([P, TILES * IN_DIM], BF16, name="x_in", tag="x_in")
-            cols = slice(tiles[0] * IN_DIM, (tiles[-1] + 1) * IN_DIM)
+            cols = slice(first * IN_DIM, last * IN_DIM)
             nc.sync.dma_start(out=x_in[s][:, cols], in_=x_rows[s][:, cols])
 
         def load_cell(s):
             c_in[s] = rows.tile([P, TILES * HID], BF16, name="c_in", tag="c_in")
             nc.sync.dma_start(out=c_in[s][:], in_=c_rows[s])
 
-        w_hh_raw, w_ih_raw = {}, {}
-
-        def load_w_hh(gate, halves=1):
+        def load_weights(gate, hh_pieces):
+            gate_rows = slice(gate * HID, (gate + 1) * HID)
             w_hh_raw[gate] = setup.tile([P, BLOCKS_PER_GATE, HID], BF16, name="w_hh_raw", tag="w_hh_raw")
-            source = W_hh[gate * HID : (gate + 1) * HID, :].rearrange("(a p) k -> p a k", p=P)
-            n_blocks = BLOCKS_PER_GATE // halves
-            for i in range(halves):
-                blocks = slice(i * n_blocks, (i + 1) * n_blocks)
-                nc.sync.dma_start(out=w_hh_raw[gate][:, blocks, :], in_=source[:, blocks, :])
-
-        def load_w_ih(gate):
+            source = W_hh[gate_rows, :].rearrange("(a p) k -> p a k", p=P)
+            piece = BLOCKS_PER_GATE // hh_pieces
+            for a in range(0, BLOCKS_PER_GATE, piece):
+                nc.sync.dma_start(out=w_hh_raw[gate][:, a : a + piece, :], in_=source[:, a : a + piece, :])
             w_ih_raw[gate] = setup.tile([P, BLOCKS_PER_GATE, IN_DIM], BF16, name="w_ih_raw", tag="w_ih_raw")
-            nc.sync.dma_start(
-                out=w_ih_raw[gate][:], in_=W_ih[gate * HID : (gate + 1) * HID, :].rearrange("(a p) k -> p a k", p=P)
-            )
+            nc.sync.dma_start(out=w_ih_raw[gate][:], in_=W_ih[gate_rows, :].rearrange("(a p) k -> p a k", p=P))
 
-        w_grouped, weights_ps = {}, {}
+        def transpose_weights_hh(gate):
+            for half in range(2):
+                wT_ps[gate, half] = psum.tile([P, 2, WORDS_PER_PACK, P], F32, name="w_hh_ps", tag="bank")
+                for a in range(2):
+                    raw_words = w_hh_raw[gate][:, 2 * half + a, :].bitcast(F32)
+                    for u in range(WORDS_PER_PACK):
+                        nc.tensor.transpose(
+                            wT_ps[gate, half][:, a, u, :], raw_words[:, u:H_WORDS:WORDS_PER_PACK], ident_f32[:]
+                        )
 
-        def weights_hh_half(gate, half):
+        def transpose_weights_ih(gate):
+            wT_ps[gate, "ih"] = psum.tile([P, HID], F32, name="w_ih_ps", tag="bank")
+            for a in range(BLOCKS_PER_GATE):
+                nc.tensor.transpose(
+                    wT_ps[gate, "ih"][:, a * P : (a + 1) * P], w_ih_raw[gate][:, a, :].bitcast(F32), ident_f32[:]
+                )
+
+        def copy_weights_hh_half(gate, half, copy_out):
             if half == 0:
                 w_grouped[gate] = setup.tile(
                     [P, HID * PACK], BF16, name="w_grouped", tag="w_grouped", bufs=2, align_bytes=64
                 )
-            wT_ps = psum.tile([P, 2, H_HALVES, P], F32, name="wT_ps", tag=TAG_C, bufs=BUF_C)
-            for a in range(2):
-                raw_words = w_hh_raw[gate][:, 2 * half + a, :].bitcast(F32)
-                for u in range(H_HALVES):
-                    nc.tensor.transpose(wT_ps[:, a, u, :], raw_words[:, u:H_WORDS:H_HALVES], ident_f32[:])
-            weights_ps[gate, half] = wT_ps
-
-        def copy_weights_hh_half(gate, half, copy_out):
             grouped_words = w_grouped[gate][:].bitcast(F32).rearrange(
-                "p (a n u) -> p a n u", a=BLOCKS_PER_GATE, u=H_HALVES
+                "p (a n u) -> p a n u", a=BLOCKS_PER_GATE, u=WORDS_PER_PACK
             )
             copy_out(
                 out=grouped_words[:, 2 * half : 2 * half + 2, :, :],
-                in_=weights_ps[gate, half][:].rearrange("p a u n -> p a n u"),
+                in_=wT_ps[gate, half][:].rearrange("p a u n -> p a n u"),
             )
 
-        def weights_quantise(gate):
+        def copy_weights_ih_half(gate, e, copy_out):
+            both = wT_ps[gate, "ih"][:].bitcast(BF16).rearrange("p (n e) -> p e n", e=HALVES)
+            copy_out(out=w_ih_T[:, e, gate * HID : (gate + 1) * HID], in_=both[:, e, :])
+
+        def quantise_weights(gate):
             cols = slice(gate * HID, (gate + 1) * HID)
             nc.vector.quantize_mx(out=w_codes[:, cols].bitcast(FP8X4), scales=w_scales[:, cols], in_=w_grouped[gate][:])
-
-        def weights_ih(gate):
-            wT_ps = psum.tile([P, HID], F32, name="wihT_ps", tag=TAG_C, bufs=BUF_C)
-            for a in range(BLOCKS_PER_GATE):
-                nc.tensor.transpose(wT_ps[:, a * P : (a + 1) * P], w_ih_raw[gate][:, a, :].bitcast(F32), ident_f32[:])
-            weights_ps[gate, 2] = wT_ps
-
-        def copy_weights_ih(gate):
-            cols = slice(gate * HID, (gate + 1) * HID)
-            halves = weights_ps[gate, 2][:].bitcast(BF16).rearrange("p (n e) -> p e n", e=PAIR)
-            nc.scalar.copy(out=w_ih_T[:, 0, cols], in_=halves[:, 0, :])
-            (nc.vector.tensor_copy if IH_V or gate == HEAD_ORDER[0] else nc.scalar.copy)(
-                out=w_ih_T[:, 1, cols], in_=halves[:, 1, :]
-            )
 
         def transpose_h(t, u):
             s, j = divmod(t, TILES)
             if u == 0:
-                words_ps[t] = psum.tile([P, H_WORDS + X_WORDS], F32, name="words_ps", tag=TAG_C, bufs=BUF_C)
+                words_ps[t] = psum.tile([P, H_WORDS + X_WORDS], F32, name="words_ps", tag="bank")
             nc.tensor.transpose(
                 words_ps[t][:, u * P : (u + 1) * P],
-                h_in[s][:].bitcast(F32)[:, j * H_WORDS + u : (j + 1) * H_WORDS : H_HALVES],
+                h_in[s][:].bitcast(F32)[:, j * H_WORDS + u : (j + 1) * H_WORDS : WORDS_PER_PACK],
                 ident_f32[:],
             )
 
@@ -225,65 +167,65 @@ def tile_nodelstmcell_pa_t_kernel(tc, x_t, h, c, W_ih, W_hh, b_ih, b_hh, out_0, 
             x_words = x_in[s][:].bitcast(F32)
             nc.tensor.transpose(words_ps[t][:, H_WORDS:], x_words[:, j * X_WORDS : (j + 1) * X_WORDS], ident_f32[:])
 
-        def transpose_rows(t):
-            for u in range(H_HALVES):
-                transpose_h(t, u)
-            transpose_x(t)
-
         def copy_rows(t):
             h_grouped[t] = work.tile([P, P * PACK], BF16, name="h_grouped", tag="h_grouped", align_bytes=64)
             nc.scalar.copy(
-                out=h_grouped[t][:].bitcast(F32).rearrange("p (r u) -> p r u", u=H_HALVES),
-                in_=words_ps[t][:, 0:H_WORDS].rearrange("p (u r) -> p r u", u=H_HALVES),
+                out=h_grouped[t][:].bitcast(F32).rearrange("p (r u) -> p r u", u=WORDS_PER_PACK),
+                in_=words_ps[t][:, 0:H_WORDS].rearrange("p (u r) -> p r u", u=WORDS_PER_PACK),
             )
-            x_T[t] = operands.tile([P, X_WORDS], F32, name="x_T", tag="x_T", bufs=ROWS_AHEAD + 4)
-            (nc.vector.tensor_copy if chosen(XV, t) else nc.scalar.copy)(out=x_T[t][:], in_=words_ps[t][:, H_WORDS:])
+            x_T[t] = operands.tile([P, X_WORDS], F32, name="x_T", tag="x_T", bufs=2 * ROWS_AHEAD)
+            copy_out = nc.vector.tensor_copy if t % 2 == 0 else nc.scalar.copy
+            copy_out(out=x_T[t][:], in_=words_ps[t][:, H_WORDS:])
 
         def quantise_rows(t):
             s, j = divmod(t, TILES)
             if j == 0:
-                h_codes[s] = operands.tile([P, GROUP_ROWS], U32, name="h_codes", tag="h_codes", align_bytes=64, bufs=4)
-                h_scales[s] = operands.tile([P, GROUP_ROWS], U8, name="h_scales", tag="h_scales", align_bytes=64, bufs=4)
+                h_codes[s] = operands.tile([P, GROUP_ROWS], U32, name="h_codes", tag="h_codes", align_bytes=64)
+                h_scales[s] = operands.tile([P, GROUP_ROWS], U8, name="h_scales", tag="h_scales", align_bytes=64)
             cols = slice(j * P, (j + 1) * P)
             nc.vector.quantize_mx(
                 out=h_codes[s][:, cols].bitcast(FP8X4), scales=h_scales[s][:, cols], in_=h_grouped[t][:]
             )
 
-        def turned_block(pair, gate, b, a):
-            s, j = divmod(2 * pair, TILES)
-            rows2 = slice(j * P, (j + 2) * P)
-            if a == 0:
-                recT_ps[pair, gate, b] = psum.tile([P, 2, 2 * P], F32, name="recT_ps", tag=TAG_C, bufs=BUF_C)
-            blk = gate * BLOCKS_PER_GATE + 2 * b + a
-            cols = slice(blk * P, (blk + 1) * P)
-            nc.tensor.matmul_mx(
-                out=recT_ps[pair, gate, b][:, a, :],
-                lhsT=w_codes[:, cols].bitcast(FP8X4),
-                lhsT_scale=w_scales[:, cols],
-                rhs=h_codes[s][:, rows2].bitcast(FP8X4),
-                rhs_scale=h_scales[s][:, rows2],
-                start=True,
-                stop=True,
-            )
+        def turned_bank(pair, gate, bank):
+            s, q = divmod(pair, TILES // PAIR_TILES)
+            pair_rows = slice(q * PAIR_ROWS, (q + 1) * PAIR_ROWS)
+            recT_ps[pair, gate, bank] = psum.tile([P, BANK_BLOCKS, PAIR_ROWS], F32, name="recT_ps", tag="bank")
+            for a in range(BANK_BLOCKS):
+                blk = gate * BLOCKS_PER_GATE + bank * BANK_BLOCKS + a
+                cols = slice(blk * P, (blk + 1) * P)
+                nc.tensor.matmul_mx(
+                    out=recT_ps[pair, gate, bank][:, a, :],
+                    lhsT=w_codes[:, cols].bitcast(FP8X4),
+                    lhsT_scale=w_scales[:, cols],
+                    rhs=h_codes[s][:, pair_rows].bitcast(FP8X4),
+                    rhs_scale=h_scales[s][:, pair_rows],
+                    start=True,
+                    stop=True,
+                )
 
-        def copy_turned_bank(pair, gate, b):
+        def on_vector(gate, bank):
+            return gate == GATE_G and bank == 0
+
+        def copy_turned_bank(pair, gate, bank):
             if (pair, gate) not in rec_T:
                 rec_T[pair, gate] = operands.tile(
-                    [P, BLOCKS_PER_GATE, 2 * P], F32, name="rec_T", tag="rec_T%d" % gate, bufs=3
+                    [P, BLOCKS_PER_GATE, PAIR_ROWS], F32, name="rec_T", tag="rec_T%d" % gate
                 )
-            blk = gate * BLOCKS_PER_GATE + 2 * b
-            if (gate, b, pair % 2) in ON_VECTOR:
+            first = bank * BANK_BLOCKS
+            blk = gate * BLOCKS_PER_GATE + first
+            if on_vector(gate, bank):
                 nc.vector.tensor_tensor(
-                    out=rec_T[pair, gate][:, 2 * b : 2 * b + 2, :],
-                    in0=recT_ps[pair, gate, b][:],
-                    in1=bias[:, blk : blk + 2].unsqueeze(2).to_broadcast([P, 2, 2 * P]),
+                    out=rec_T[pair, gate][:, first : first + BANK_BLOCKS, :],
+                    in0=recT_ps[pair, gate, bank][:],
+                    in1=bias[:, blk : blk + BANK_BLOCKS].unsqueeze(2).to_broadcast([P, BANK_BLOCKS, PAIR_ROWS]),
                     op=ALU.add,
                 )
             else:
-                for a in range(2):
+                for a in range(BANK_BLOCKS):
                     nc.scalar.activation(
-                        out=rec_T[pair, gate][:, 2 * b + a, :],
-                        in_=recT_ps[pair, gate, b][:, a, :],
+                        out=rec_T[pair, gate][:, first + a, :],
+                        in_=recT_ps[pair, gate, bank][:, a, :],
                         func=ACT.Identity,
                         bias=bias[:, blk + a : blk + a + 1],
                     )
@@ -291,206 +233,106 @@ def tile_nodelstmcell_pa_t_kernel(tc, x_t, h, c, W_ih, W_hh, b_ih, b_hh, out_0, 
         def input_pass(n, e):
             t, gate = steps[n]
             if e == 0:
-                gate_ps[n] = psum.tile([P, HID], F32, name="gate_ps", tag=TAG_G, bufs=BUF_G)
+                gate_ps[n] = psum.tile([P, HID], F32, name="gate_ps", tag="bank")
             nc.tensor.matmul(
                 out=gate_ps[n][:],
-                lhsT=x_T[t][:].bitcast(BF16)[:, e:IN_DIM:PAIR],
+                lhsT=x_T[t][:].bitcast(BF16)[:, e:IN_DIM:HALVES],
                 rhs=w_ih_T[:, e, gate * HID : (gate + 1) * HID],
                 start=(e == 0),
-                stop=(e == PAIR - 1 and not turned_gate(t, gate)),
-            )
-
-        def recurrent_rows(n):
-            t, gate = steps[n]
-            s, j = divmod(t, TILES)
-            rec_ps[n] = psum.tile([P, HID], F32, name="rec_ps", tag=TAG_C, bufs=BUF_C)
-            nc.tensor.matmul_mx(
-                out=rec_ps[n][:],
-                lhsT=h_codes[s][:, j * P : (j + 1) * P].bitcast(FP8X4),
-                lhsT_scale=h_scales[s][:, j * P : (j + 1) * P],
-                rhs=w_codes[:, gate * HID : (gate + 1) * HID].bitcast(FP8X4),
-                rhs_scale=w_scales[:, gate * HID : (gate + 1) * HID],
-                start=True,
-                stop=True,
+                stop=(e == HALVES - 1 and gate in ADDED),
             )
 
         def add_turned(n, half):
             t, gate = steps[n]
-            s, j = divmod(t, TILES)
+            pair, j = divmod(t, PAIR_TILES)
             for a in range(2 * half, 2 * half + 2):
                 nc.tensor.matmul(
                     out=gate_ps[n][:, a * P : (a + 1) * P],
-                    lhsT=rec_T[t // 2, gate][:, a, (t % 2) * P : (t % 2 + 1) * P],
+                    lhsT=rec_T[pair, gate][:, a, j * P : (j + 1) * P],
                     rhs=ident_f32[:],
                     is_transpose=True,
                     start=False,
                     stop=(a == BLOCKS_PER_GATE - 1),
                 )
 
+        def recurrent_rows(n):
+            t, gate = steps[n]
+            s, j = divmod(t, TILES)
+            tile_rows = slice(j * P, (j + 1) * P)
+            cols = slice(gate * HID, (gate + 1) * HID)
+            rec_ps[n] = psum.tile([P, HID], F32, name="rec_ps", tag="bank")
+            nc.tensor.matmul_mx(
+                out=rec_ps[n][:],
+                lhsT=h_codes[s][:, tile_rows].bitcast(FP8X4),
+                lhsT_scale=h_scales[s][:, tile_rows],
+                rhs=w_codes[:, cols].bitcast(FP8X4),
+                rhs_scale=w_scales[:, cols],
+                start=True,
+                stop=True,
+            )
+
         def add_bias(n):
             t, gate = steps[n]
             if t not in sums:
-                sums[t] = work.tile([P, 2, HID], F32, name="sums", tag="sums", bufs=6)
-            acts[t, gate] = sums[t][:, ADDED.index(gate), :]
-            nc.vector.tensor_tensor(out=acts[t, gate], in0=gate_ps[n][:], in1=bias_spread[:, gate, :], op=ALU.add)
+                sums[t] = work.tile([P, len(ADDED), HID], F32, name="sums", tag="sums", bufs=6)
+            nc.vector.tensor_tensor(
+                out=gate_of(t, gate), in0=gate_ps[n][:], in1=bias_spread[:, ADDED.index(gate), :], op=ALU.add
+            )
 
         def add_recurrent(n):
-            total = acts[steps[n]]
+            total = gate_of(*steps[n])
             nc.vector.tensor_tensor(out=total, in0=rec_ps[n][:], in1=total, op=ALU.add)
 
-        def activate(n):
-            t, gate = steps[n]
-            func = ACT.Tanh if gate == GATE_G else ACT.Sigmoid
-            if turned_gate(t, gate):
-                act = work.tile([P, HID], F32, name="act%d" % gate, tag="act%d" % gate, bufs=6)
-                nc.scalar.activation(out=act[:], in_=gate_ps[n][:], func=func)
-                acts[t, gate] = act[:]
-            else:
-                nc.scalar.activation(out=acts[t, gate], in_=acts[t, gate], func=func)
+        def activated_at(t, gate):
+            if gate in ADDED and t >= HEAD_TILES:
+                return at[t, ADDED[-1]] + 1
+            return at[t, gate] + 1
 
-        def activate_both(t):
-            both = sums[t][:].rearrange("p g n -> p (g n)")
-            nc.scalar.activation(out=both, in_=both, func=ACT.Sigmoid)
-
-        def half(i, parts):
-            return slice(i * HID // parts, (i + 1) * HID // parts)
+        def activate(t, gate):
+            if gate in TURNED:
+                turned_acts[t, gate] = work.tile([P, HID], F32, name="act%d" % gate, tag="act%d" % gate, bufs=6)
+                func = ACT.Tanh if gate == GATE_G else ACT.Sigmoid
+                nc.scalar.activation(out=turned_acts[t, gate][:], in_=gate_ps[at[t, gate]][:], func=func)
+            elif t < HEAD_TILES:
+                nc.scalar.activation(out=gate_of(t, gate), in_=gate_of(t, gate), func=ACT.Sigmoid)
+            elif gate == ADDED[-1]:
+                both = sums[t][:].rearrange("p g n -> p (g n)")
+                nc.scalar.activation(out=both, in_=both, func=ACT.Sigmoid)
 
         def keep_old_cell(t, engine):
             s, j = divmod(t, TILES)
-            kept[t] = work.tile([P, HID], F32, name="kept", tag="kept", bufs=PROD_BUFS)
+            kept[t] = work.tile([P, HID], F32, name="kept", tag="kept", bufs=2)
             engine.tensor_tensor(
-                out=kept[t][:], in0=acts[t, GATE_F], in1=c_in[s][:, j * HID : (j + 1) * HID], op=ALU.mult
+                out=kept[t][:], in0=gate_of(t, GATE_F), in1=c_in[s][:, j * HID : (j + 1) * HID], op=ALU.mult
             )
 
-        def write_candidate(t, engine, i=0, parts=1):
-            if i == 0:
-                written[t] = work.tile([P, HID], F32, name="written", tag="written", bufs=PROD_BUFS)
-            cols = half(i, parts)
+        def write_candidate(t, engine, cols):
+            if t not in written:
+                written[t] = work.tile([P, HID], F32, name="written", tag="written", bufs=2)
             engine.tensor_tensor(
-                out=written[t][:, cols], in0=acts[t, GATE_I][:, cols], in1=acts[t, GATE_G][:, cols], op=ALU.mult
+                out=written[t][:, cols], in0=gate_of(t, GATE_I)[:, cols], in1=gate_of(t, GATE_G)[:, cols], op=ALU.mult
             )
 
-        def new_cell(t, i=0, parts=1):
+        def new_cell(t, cols):
             s, j = divmod(t, TILES)
-            if i == 0:
+            if t not in c_new:
                 c_new[t] = work.tile([P, HID], F32, name="c_new", tag="c_new")
-            cols = half(i, parts)
             nc.vector.tensor_tensor(out=c_new[t][:, cols], in0=kept[t][:, cols], in1=written[t][:, cols], op=ALU.add)
             nc.sync.dma_start(out=c_next_rows[s, j][:, cols], in_=c_new[t][:, cols])
 
-        def tanh_of_new_cell(t, i=0, parts=1):
-            if i == 0:
+        def tanh_of_new_cell(t, cols):
+            if t not in tanh_c:
                 tanh_c[t] = work.tile([P, HID], F32, name="tanh_c", tag="tanh_c")
-            cols = half(i, parts)
             nc.scalar.activation(out=tanh_c[t][:, cols], in_=c_new[t][:, cols], func=ACT.Tanh)
 
-        def new_hidden(t, i=0, parts=1):
+        def new_hidden(t, cols):
             s, j = divmod(t, TILES)
-            if i == 0:
+            if t not in h_new:
                 h_new[t] = work.tile([P, HID], F32, name="h_new", tag="h_new")
-            cols = half(i, parts)
-            (nc.gpsimd if chosen(H_G, t) else nc.vector).tensor_tensor(
-                out=h_new[t][:, cols], in0=acts[t, GATE_O][:, cols], in1=tanh_c[t][:, cols], op=ALU.mult
+            nc.vector.tensor_tensor(
+                out=h_new[t][:, cols], in0=gate_of(t, GATE_O)[:, cols], in1=tanh_c[t][:, cols], op=ALU.mult
             )
             nc.sync.dma_start(out=h_next_rows[s, j][:, cols], in_=h_new[t][:, cols])
-
-        plan = []
-        waiting = []
-
-        def put(key, fn, *args):
-            plan.append((key, fn, args))
-
-        def turned(n):
-            return 0 <= n < n_steps and turned_gate(*steps[n])
-
-        head = N_HEAD * GATES
-        for n, (t, gate) in enumerate(steps):
-            put(n, input_pass, n, 0)
-            put(n + 0.3, input_pass, n, 1)
-            if turned(n):
-                put(n + 1.1, add_turned, n, 0)
-                put(n + (1.101 if n == n_steps - 2 else 1.4), add_turned, n, 1)
-            else:
-                put(n + (1.05 if turned(n - 1) else 0.41 if turned(n - 2) and n > head else 0.1), recurrent_rows, n)
-                put(n + 0.5, add_bias, n)
-                put(n + 1.55, add_recurrent, n)
-            if MERGE and not turned(n) and t >= N_HEAD and not (MERGE == 2 and t == N_TILES - 1):
-                if n == max(at[t, gate2] for gate2 in ADDED):
-                    put(n + ACT_LAG, activate_both, t)
-            else:
-                put(n + ACT_LAG, activate, n)
-        for t in range(2, N_TILES):
-            if t < N_HEAD + ROWS_AHEAD:
-                k = min(t - 2, head - 1)
-                put(k + 0.45, transpose_rows, t)
-                put(k + 0.6, copy_rows, t)
-                put(k + 0.7, quantise_rows, t)
-            else:
-                k = at[t - ROWS_AHEAD, ROW_GATE]
-                put(k + ROW_K[0], transpose_h, t, 0)
-                put(k + ROW_K[1], transpose_h, t, 1)
-                put(k + ROW_K[2], transpose_x, t)
-                put(k + ROW_COPY, copy_rows, t)
-                waiting.append((k + ROW_COPY, t))
-        for pair in range(N_TILES // 2):
-            for gate in GATE_ORDER:
-                if turned_gate(2 * pair, gate):
-                    for b in range(2):
-                        if pair == 0:
-                            k = at[0, gate] - T_HEAD
-                        elif gate == GATE_G:
-                            k = max(at[2 * pair - 2 + b, TB1], at[0, gate])
-                        else:
-                            k = max(at[2 * pair - 1 + b, TB2], at[0, gate])
-                        early = pair == 0 or k < head
-                        put(k + (0.42 if early else TBK[0]), turned_block, pair, gate, b, 0)
-                        put(k + (0.421 if early else TBK[1]), turned_block, pair, gate, b, 1)
-                        put(k + T_COPY, copy_turned_bank, pair, gate, b)
-        for q in range(1, GATES):
-            gate = HEAD_ORDER[q]
-            k = at[0, gate] - W_LEAD
-            dd = W_STEP
-            put(k + 0.43, weights_hh_half, gate, 0)
-            put(k + 0.65, copy_weights_hh_half, gate, 0, nc.vector.tensor_copy if HH_V else nc.scalar.copy)
-            put(k + dd + 0.43, weights_hh_half, gate, 1)
-            put(k + dd + 0.65, copy_weights_hh_half, gate, 1, nc.scalar.copy)
-            put(k + 2 * dd + 0.43, weights_ih, gate)
-            put(k + 2 * dd + 0.65, copy_weights_ih, gate)
-            put(k + dd + 0.9, weights_quantise, gate)
-        for t in range(N_TILES):
-            last = t == N_TILES - 1
-            b = max(at[t, GATE_I], at[t, GATE_G], at[t, GATE_F])
-            c_key = b + (LAST_C if last else C_LAG)
-            f_at = at[t, GATE_F]
-            if MERGE and t >= N_HEAD and not (MERGE == 2 and t == N_TILES - 1) and GATE_F in ADDED:
-                f_at = max(at[t, gate] for gate in ADDED)
-            k_key = min(f_at + K_LAG, c_key - 0.1)
-            assert k_key > f_at + ACT_LAG
-            w_key = min(max(at[t, GATE_I], at[t, GATE_G]) + W_LAG, c_key - 0.05)
-            tanh_key = c_key + (1.0 if last else TANH_LAG)
-            parts = LAST_PARTS if last else 1
-            products = nc.vector if t >= N_TILES - LASTV else nc.gpsimd
-            put(k_key, keep_old_cell, t, products)
-            while waiting and waiting[0][0] < c_key - 0.2:
-                put(c_key - 0.02, quantise_rows, waiting.pop(0)[1])
-            if t > 0:
-                put(max(c_key - 0.01, tanh_before + 0.3, at[t - 1, GATE_O] + ACT_LAG + 0.1), new_hidden, t - 1)
-            tanh_before = tanh_key
-            for i in range(parts):
-                put(w_key + 0.001 * i, write_candidate, t, products, i, parts)
-                put(c_key + 0.001 * i, new_cell, t, i, parts)
-                put(tanh_key + 0.001 * i, tanh_of_new_cell, t, i, parts)
-                if last:
-                    put(max(tanh_key, at[t, GATE_O] + ACT_LAG) + 0.5 + 0.001 * i, new_hidden, t, i, parts)
-        put(2.9, load_h, 3)
-        put(2.9, load_x, 3)
-        for s in range(1, N_GROUPS):
-            k = at[TILES * s, GATE_F] if TILES * s >= N_HEAD else head
-            if s + 3 < N_GROUPS:
-                put(k - 0.01, load_h, s + 3)
-                put(k - 0.01, load_x, s + 3)
-            if s + 1 < N_GROUPS:
-                put(k - 0.01, load_cell, s + 1)
 
         zeros = const.tile([P, HID], BF16)
         nc.vector.memset(zeros[:], 0.0)
@@ -499,28 +341,24 @@ def tile_nodelstmcell_pa_t_kernel(tc, x_t, h, c, W_ih, W_hh, b_ih, b_hh, out_0, 
         nc.vector.memset(bias_rows[4 * BLOCKS :, :], 0.0)
         nc.sync.dma_start(out=bias_rows[0:BLOCKS, :], in_=b_ih.rearrange("(b n) -> b n", n=P))
         nc.sync.dma_start(out=bias_rows[BLOCKS : 2 * BLOCKS, :], in_=b_hh.rearrange("(b n) -> b n", n=P))
-        load_w_hh(HEAD_ORDER[0], 2)
-        load_w_ih(HEAD_ORDER[0])
-        load_h(0, range(0, 2))
-        load_x(0, range(0, 2))
-        load_w_hh(HEAD_ORDER[1])
-        load_w_ih(HEAD_ORDER[1])
-        load_h(0, range(2, 4))
-        load_x(0, range(2, 4))
-        load_w_hh(HEAD_ORDER[2])
-        load_w_ih(HEAD_ORDER[2])
+        load_weights(HEAD_ORDER[0], 2)
+        load_h(0, 0, HEAD_TILES)
+        load_x(0, 0, HEAD_TILES)
+        load_weights(HEAD_ORDER[1], 1)
+        load_weights(HEAD_ORDER[2], 1)
+        load_h(0, HEAD_TILES)
+        load_x(0, HEAD_TILES)
         load_cell(0)
-        load_w_hh(HEAD_ORDER[3])
-        load_w_ih(HEAD_ORDER[3])
+        load_weights(HEAD_ORDER[3], 1)
         load_h(1)
         load_x(1)
         load_cell(1)
         load_h(2)
         load_x(2)
 
-        warm = const.tile([P, 1], F32)
-        nc.vector.memset(warm[:], 0.0)
-        nc.scalar.activation(out=warm[:], in_=warm[:], func=ACT.Sigmoid)
+        table_input = const.tile([P, 1], F32)
+        nc.vector.memset(table_input[:], 0.0)
+        nc.scalar.activation(out=table_input[:], in_=table_input[:], func=ACT.Sigmoid)
 
         ident_f32 = const.tile([P, P], F32)
         make_identity(nc, ident_f32[:])
@@ -528,52 +366,175 @@ def tile_nodelstmcell_pa_t_kernel(tc, x_t, h, c, W_ih, W_hh, b_ih, b_hh, out_0, 
         make_identity(nc, ident_bf16[:])
         w_codes = const.tile([P, GATES * HID], U32, align_bytes=64)
         w_scales = const.tile([P, GATES * HID], U8, align_bytes=64)
-        w_ih_T = const.tile([P, PAIR, GATES * HID], BF16)
+        w_ih_T = const.tile([P, HALVES, GATES * HID], BF16)
 
+        warm_ps = psum.tile([P, HID], F32, name="warm_ps", tag="bank")
+        for i in range(WARM_UP):
+            nc.tensor.matmul(
+                out=warm_ps[:], lhsT=zeros[:, 0:P], rhs=zeros[:], start=(i == 0), stop=(i == WARM_UP - 1)
+            )
 
-        def warm_up(n):
-            warm_ps = psum.tile([P, HID], F32, name="warm_ps", tag=TAG_G, bufs=BUF_G)
-            for i in range(n):
-                nc.tensor.matmul(out=warm_ps[:], lhsT=zeros[:, 0:P], rhs=zeros[:], start=(i == 0), stop=(i == n - 1))
-
-        if DUM1:
-            warm_up(DUM1)
-
-        biasT_ps = psum.tile([P, P], BF16, tag=TAG_C, bufs=BUF_C)
+        biasT_ps = psum.tile([P, P], BF16, name="biasT_ps", tag="bank")
         nc.tensor.transpose(biasT_ps[:], bias_rows[:], ident_bf16[:])
         bias_pair = const.tile([P, 2 * BLOCKS], F32)
         nc.vector.tensor_copy(out=bias_pair[:], in_=biasT_ps[:, 0 : 2 * BLOCKS])
         bias = const.tile([P, BLOCKS], F32)
         nc.vector.tensor_tensor(out=bias[:], in0=bias_pair[:, 0:BLOCKS], in1=bias_pair[:, BLOCKS : 2 * BLOCKS], op=ALU.add)
 
-        weights_hh_half(HEAD_ORDER[0], 0)
-        copy_weights_hh_half(HEAD_ORDER[0], 0, nc.vector.tensor_copy)
-        weights_hh_half(HEAD_ORDER[0], 1)
-        copy_weights_hh_half(HEAD_ORDER[0], 1, nc.scalar.copy)
-        weights_quantise(HEAD_ORDER[0])
-        if DUM2:
-            warm_up(DUM2)
-        weights_ih(HEAD_ORDER[0])
+        def copy_weights_hh(gate):
+            copy_weights_hh_half(gate, 0, nc.vector.tensor_copy)
+            copy_weights_hh_half(gate, 1, nc.scalar.copy)
+
+        def copy_weights_ih(gate):
+            copy_weights_ih_half(gate, 0, nc.scalar.copy)
+            copy_weights_ih_half(gate, 1, nc.vector.tensor_copy)
+
+        transpose_weights_hh(HEAD_ORDER[0])
+        copy_weights_hh(HEAD_ORDER[0])
+        quantise_weights(HEAD_ORDER[0])
+        transpose_weights_ih(HEAD_ORDER[0])
         copy_weights_ih(HEAD_ORDER[0])
-        for t in range(2):
-            transpose_rows(t)
+        for t in range(HEAD_TILES):
+            for u in range(WORDS_PER_PACK):
+                transpose_h(t, u)
+            transpose_x(t)
             copy_rows(t)
             quantise_rows(t)
 
-        bias_spread = const.tile([P, GATES, HID], F32)
-
-        def spread_bias(gate):
-            spread_ps = psum.tile([P, HID], F32, name="spread_ps", tag=TAG_G, bufs=BUF_G)
+        bias_spread = const.tile([P, len(ADDED), HID], F32)
+        for g, gate in enumerate(ADDED):
+            spread_ps = psum.tile([P, HID], F32, name="spread_ps", tag="bank")
             for a in range(BLOCKS_PER_GATE):
                 blk = gate * BLOCKS_PER_GATE + a
                 nc.tensor.transpose(
                     spread_ps[:, a * P : (a + 1) * P], bias[:, blk : blk + 1].to_broadcast([P, P]), ident_f32[:]
                 )
-            (nc.vector.tensor_copy if SP_V else nc.scalar.copy)(out=bias_spread[:, gate, :], in_=spread_ps[:])
+            nc.scalar.copy(out=bias_spread[:, g, :], in_=spread_ps[:])
 
-        for gate in HEAD_ORDER:
-            if not all(turned_gate(t, gate) for t in range(TILES)):
-                spread_bias(gate)
+        due = {}
 
-        for key, fn, args in sorted(plan, key=lambda e: e[0]):
-            fn(*args)
+        def put(step, what, *which):
+            due.setdefault((step, what), []).append(which)
+
+        for gate in HEAD_ORDER[1:]:
+            put(at[0, gate] - (3 if gate in TURNED else 2), "weights", gate)
+        for t in range(HEAD_TILES, HEAD_TILES + ROWS_AHEAD):
+            put(t + 1, "first rows", t)
+        for t in range(HEAD_TILES + ROWS_AHEAD, N_TILES):
+            put(at[t - ROWS_AHEAD, TILE_ORDER[0]], "rows", t)
+            put(at[t - ROWS_AHEAD, TILE_ORDER[0]] + 1, "copy of rows", t)
+        for pair in range(N_PAIRS):
+            for gate in TURNED:
+                for bank in range(BANKS_PER_GATE):
+                    beside = at[PAIR_TILES * pair - 1 + bank, ADDED[-1]] if pair > 0 else 0
+                    step = max(beside, at[0, gate] - (1 if pair == 0 else 0))
+                    put(step, "turned bank", pair, gate, bank)
+                    put(step + 1, "copy of turned bank", pair, gate, bank)
+        for n in range(n_steps):
+            if is_step(n, ADDED):
+                if is_step(n - 1, TURNED):
+                    put(n + 1, "product behind pass 0", n)
+                elif is_step(n - 2, TURNED) and n > n_head:
+                    put(n, "product behind pass 1", n)
+                else:
+                    put(n, "product behind pass 0", n)
+        last_tile = N_TILES - 1
+        for t in range(N_TILES):
+            put(activated_at(t, GATE_F) + 1, "keep", t)
+        for t in range(last_tile):
+            cell_step = at[t, GATE_G] + GATES
+            put(cell_step, "cell", t)
+            put(cell_step + 2, "tanh", t)
+            if t + 1 < last_tile:
+                put(max(at[t + 1, GATE_G] + GATES, cell_step + 2), "hidden", t)
+        put(HEAD_TILES + 1, "load rows", 3)
+        for s in range(1, N_GROUPS):
+            first_step = at[TILES * s, TILE_ORDER[0]]
+            if s + 3 < N_GROUPS:
+                put(first_step, "load rows", s + 3)
+            if s + 1 < N_GROUPS:
+                put(first_step, "load cell", s + 1)
+
+        everything = slice(0, HID)
+        copied_rows = []
+        first = min(step for step, what in due)
+        for n in range(first, max(step for step, what in due) + 1):
+            running = 0 <= n < n_steps
+            for (s,) in due.get((n, "load rows"), []):
+                load_h(s)
+                load_x(s)
+            for (s,) in due.get((n, "load cell"), []):
+                load_cell(s)
+
+            if running:
+                input_pass(n, 0)
+            for (t,) in due.get((n, "rows"), []):
+                transpose_h(t, 0)
+            if is_step(n - 1, TURNED):
+                add_turned(n - 1, 0)
+            for (m,) in due.get((n, "product behind pass 0"), []):
+                recurrent_rows(m)
+            for (t,) in due.get((n, "first rows"), []):
+                for u in range(WORDS_PER_PACK):
+                    transpose_h(t, u)
+                transpose_x(t)
+            if running:
+                input_pass(n, 1)
+            for (t,) in due.get((n, "rows"), []):
+                transpose_h(t, 1)
+                transpose_x(t)
+            if is_step(n - 1, TURNED):
+                add_turned(n - 1, 1)
+            for (m,) in due.get((n, "product behind pass 1"), []):
+                recurrent_rows(m)
+            for bank in due.get((n, "turned bank"), []):
+                turned_bank(*bank)
+            for (gate,) in due.get((n, "weights"), []):
+                transpose_weights_hh(gate)
+                transpose_weights_ih(gate)
+
+            for (t,) in due.get((n, "cell"), []):
+                write_candidate(t, nc.gpsimd, everything)
+            if is_step(n, ADDED):
+                add_bias(n)
+            if is_step(n - 1, ADDED):
+                add_recurrent(n - 1)
+            for bank in due.get((n, "copy of turned bank"), []):
+                copy_turned_bank(*bank)
+
+            for (t,) in due.get((n, "first rows"), []):
+                copy_rows(t)
+            for (gate,) in due.get((n, "weights"), []):
+                copy_weights_hh(gate)
+                copy_weights_ih(gate)
+            for (t,) in due.get((n, "tanh"), []):
+                tanh_of_new_cell(t, everything)
+            for (t,) in due.get((n, "first rows"), []):
+                quantise_rows(t)
+            if is_step(n - 1, TILE_ORDER):
+                activate(*steps[n - 1])
+            for (t,) in due.get((n, "copy of rows"), []):
+                copy_rows(t)
+                copied_rows.append(t)
+            for (gate,) in due.get((n, "weights"), []):
+                quantise_weights(gate)
+            if (n, "cell") in due or (n, "hidden") in due:
+                while copied_rows:
+                    quantise_rows(copied_rows.pop(0))
+            for (t,) in due.get((n, "hidden"), []):
+                new_hidden(t, everything)
+            for (t,) in due.get((n, "cell"), []):
+                new_cell(t, everything)
+            for (t,) in due.get((n, "keep"), []):
+                keep_old_cell(t, nc.gpsimd if t < last_tile else nc.vector)
+
+        halves = [slice(i * HID // 2, (i + 1) * HID // 2) for i in range(2)]
+        for cols in halves:
+            write_candidate(last_tile, nc.vector, cols)
+        new_hidden(last_tile - 1, everything)
+        for cols in halves:
+            new_cell(last_tile, cols)
+        for cols in halves:
+            tanh_of_new_cell(last_tile, cols)
+        for cols in halves:
+            new_hidden(last_tile, cols)

@@ -16,6 +16,10 @@ BATCH, IN_DIM, HID = 4096, 256, 512
 GATES = 4
 GATE_I, GATE_F, GATE_G, GATE_O = 0, 1, 2, 3
 ADDED = (GATE_F, GATE_O)
+ADDED3 = (GATE_F, GATE_O, GATE_I)
+THREE = lambda pair: False
+ONV = lambda pair, gate, bank: gate == GATE_I and bank == 1
+XV = lambda t: t % 2 == 0
 TURNED = (GATE_I, GATE_G)
 TILE_ORDER = ADDED + TURNED
 HEAD_ORDER = (GATE_F, GATE_I, GATE_O, GATE_G)
@@ -58,8 +62,14 @@ def tile_nodelstmcell_pa_t_kernel(tc, x_t, h, c, W_ih, W_hh, b_ih, b_hh, out_0, 
     n_steps = len(steps)
     at = {step: n for n, step in enumerate(steps)}
 
-    def is_step(n, gates):
-        return 0 <= n < n_steps and steps[n][1] in gates
+    def added(t):
+        return ADDED3 if THREE(t // PAIR_TILES) else ADDED
+
+    def is_added(n):
+        return n_head <= n < n_steps and steps[n][1] in added(steps[n][0])
+
+    def is_turned(n):
+        return n_head <= n < n_steps and steps[n][1] not in added(steps[n][0])
 
     with ExitStack() as stack:
         const = stack.enter_context(tc.tile_pool(name="const", bufs=1))
@@ -86,7 +96,7 @@ def tile_nodelstmcell_pa_t_kernel(tc, x_t, h, c, W_ih, W_hh, b_ih, b_hh, out_0, 
         w_hh_raw, w_ih_raw, w_grouped, wT_ps = {}, {}, {}, {}
 
         def gate_of(t, gate):
-            return sums[t][:, ADDED.index(gate), :] if gate in ADDED else turned_acts[t, gate][:]
+            return sums[t][:, ADDED3.index(gate), :] if gate in added(t) else turned_acts[t, gate][:]
 
         def load_h(s, first=0, last=TILES):
             if s not in h_in:
@@ -104,35 +114,37 @@ def tile_nodelstmcell_pa_t_kernel(tc, x_t, h, c, W_ih, W_hh, b_ih, b_hh, out_0, 
             c_in[s] = rows.tile([P, TILES * HID], BF16, name="c_in", tag="c_in")
             nc.sync.dma_start(out=c_in[s][:], in_=c_rows[s])
 
-        def load_weights(gate, hh_pieces):
+        def load_w_ih(gate):
             gate_rows = slice(gate * HID, (gate + 1) * HID)
-            w_hh_raw[gate] = setup.tile([P, BLOCKS_PER_GATE, HID], BF16, name="w_hh_raw", tag="w_hh_raw")
-            source = W_hh[gate_rows, :].rearrange("(a p) k -> p a k", p=P)
-            piece = BLOCKS_PER_GATE // hh_pieces
-            for a in range(0, BLOCKS_PER_GATE, piece):
-                nc.sync.dma_start(out=w_hh_raw[gate][:, a : a + piece, :], in_=source[:, a : a + piece, :])
             w_ih_raw[gate] = setup.tile([P, BLOCKS_PER_GATE, IN_DIM], BF16, name="w_ih_raw", tag="w_ih_raw")
             nc.sync.dma_start(out=w_ih_raw[gate][:], in_=W_ih[gate_rows, :].rearrange("(a p) k -> p a k", p=P))
 
-        def transpose_weights_hh(gate):
-            for half in range(2):
-                wT_ps[gate, half] = psum.tile([P, 2, WORDS_PER_PACK, P], F32, name="w_hh_ps", tag="bank")
-                for a in range(2):
-                    raw_words = w_hh_raw[gate][:, 2 * half + a, :].bitcast(F32)
-                    for u in range(WORDS_PER_PACK):
-                        nc.tensor.transpose(
-                            wT_ps[gate, half][:, a, u, :], raw_words[:, u:H_WORDS:WORDS_PER_PACK], ident_f32[:]
-                        )
+        def load_w_hh(gate, pieces):
+            gate_rows = slice(gate * HID, (gate + 1) * HID)
+            w_hh_raw[gate] = setup.tile([P, BLOCKS_PER_GATE, HID], BF16, name="w_hh_raw", tag="w_hh_raw")
+            source = W_hh[gate_rows, :].rearrange("(a p) k -> p a k", p=P)
+            piece = BLOCKS_PER_GATE // pieces
+            for a in range(0, BLOCKS_PER_GATE, piece):
+                nc.sync.dma_start(out=w_hh_raw[gate][:, a : a + piece, :], in_=source[:, a : a + piece, :])
 
-        def transpose_weights_ih(gate):
+        def transpose_w_hh(gate, half):
+            wT_ps[gate, half] = psum.tile([P, 2, WORDS_PER_PACK, P], F32, name="w_hh_ps", tag="bank")
+            for a in range(2):
+                raw_words = w_hh_raw[gate][:, 2 * half + a, :].bitcast(F32)
+                for u in range(WORDS_PER_PACK):
+                    nc.tensor.transpose(
+                        wT_ps[gate, half][:, a, u, :], raw_words[:, u:H_WORDS:WORDS_PER_PACK], ident_f32[:]
+                    )
+
+        def transpose_w_ih(gate):
             wT_ps[gate, "ih"] = psum.tile([P, HID], F32, name="w_ih_ps", tag="bank")
             for a in range(BLOCKS_PER_GATE):
                 nc.tensor.transpose(
                     wT_ps[gate, "ih"][:, a * P : (a + 1) * P], w_ih_raw[gate][:, a, :].bitcast(F32), ident_f32[:]
                 )
 
-        def copy_weights_hh_half(gate, half, copy_out):
-            if half == 0:
+        def copy_w_hh(gate, half, copy_out):
+            if gate not in w_grouped:
                 w_grouped[gate] = setup.tile(
                     [P, HID * PACK], BF16, name="w_grouped", tag="w_grouped", bufs=2, align_bytes=64
                 )
@@ -144,9 +156,10 @@ def tile_nodelstmcell_pa_t_kernel(tc, x_t, h, c, W_ih, W_hh, b_ih, b_hh, out_0, 
                 in_=wT_ps[gate, half][:].rearrange("p a u n -> p a n u"),
             )
 
-        def copy_weights_ih_half(gate, e, copy_out):
+        def copy_w_ih(gate, copy_out):
             both = wT_ps[gate, "ih"][:].bitcast(BF16).rearrange("p (n e) -> p e n", e=HALVES)
-            copy_out(out=w_ih_T[:, e, gate * HID : (gate + 1) * HID], in_=both[:, e, :])
+            for e in range(HALVES):
+                copy_out(out=w_ih_T[:, e, gate * HID : (gate + 1) * HID], in_=both[:, e, :])
 
         def quantise_weights(gate):
             cols = slice(gate * HID, (gate + 1) * HID)
@@ -154,7 +167,7 @@ def tile_nodelstmcell_pa_t_kernel(tc, x_t, h, c, W_ih, W_hh, b_ih, b_hh, out_0, 
 
         def transpose_h(t, u):
             s, j = divmod(t, TILES)
-            if u == 0:
+            if t not in words_ps:
                 words_ps[t] = psum.tile([P, H_WORDS + X_WORDS], F32, name="words_ps", tag="bank")
             nc.tensor.transpose(
                 words_ps[t][:, u * P : (u + 1) * P],
@@ -164,17 +177,20 @@ def tile_nodelstmcell_pa_t_kernel(tc, x_t, h, c, W_ih, W_hh, b_ih, b_hh, out_0, 
 
         def transpose_x(t):
             s, j = divmod(t, TILES)
+            if t not in words_ps:
+                words_ps[t] = psum.tile([P, H_WORDS + X_WORDS], F32, name="words_ps", tag="bank")
             x_words = x_in[s][:].bitcast(F32)
             nc.tensor.transpose(words_ps[t][:, H_WORDS:], x_words[:, j * X_WORDS : (j + 1) * X_WORDS], ident_f32[:])
 
-        def copy_rows(t):
+        def copy_h(t):
             h_grouped[t] = work.tile([P, P * PACK], BF16, name="h_grouped", tag="h_grouped", align_bytes=64)
             nc.scalar.copy(
                 out=h_grouped[t][:].bitcast(F32).rearrange("p (r u) -> p r u", u=WORDS_PER_PACK),
                 in_=words_ps[t][:, 0:H_WORDS].rearrange("p (u r) -> p r u", u=WORDS_PER_PACK),
             )
+
+        def copy_x(t, copy_out):
             x_T[t] = operands.tile([P, X_WORDS], F32, name="x_T", tag="x_T", bufs=2 * ROWS_AHEAD)
-            copy_out = nc.vector.tensor_copy if t % 2 == 0 else nc.scalar.copy
             copy_out(out=x_T[t][:], in_=words_ps[t][:, H_WORDS:])
 
         def quantise_rows(t):
@@ -204,8 +220,8 @@ def tile_nodelstmcell_pa_t_kernel(tc, x_t, h, c, W_ih, W_hh, b_ih, b_hh, out_0, 
                     stop=True,
                 )
 
-        def on_vector(gate, bank):
-            return gate == GATE_G and bank == 0
+        def on_vector(pair, gate, bank):
+            return ONV(pair, gate, bank)
 
         def copy_turned_bank(pair, gate, bank):
             if (pair, gate) not in rec_T:
@@ -214,7 +230,7 @@ def tile_nodelstmcell_pa_t_kernel(tc, x_t, h, c, W_ih, W_hh, b_ih, b_hh, out_0, 
                 )
             first = bank * BANK_BLOCKS
             blk = gate * BLOCKS_PER_GATE + first
-            if on_vector(gate, bank):
+            if on_vector(pair, gate, bank):
                 nc.vector.tensor_tensor(
                     out=rec_T[pair, gate][:, first : first + BANK_BLOCKS, :],
                     in0=recT_ps[pair, gate, bank][:],
@@ -239,7 +255,7 @@ def tile_nodelstmcell_pa_t_kernel(tc, x_t, h, c, W_ih, W_hh, b_ih, b_hh, out_0, 
                 lhsT=x_T[t][:].bitcast(BF16)[:, e:IN_DIM:HALVES],
                 rhs=w_ih_T[:, e, gate * HID : (gate + 1) * HID],
                 start=(e == 0),
-                stop=(e == HALVES - 1 and gate in ADDED),
+                stop=(e == HALVES - 1 and gate in added(t)),
             )
 
         def add_turned(n, half):
@@ -274,9 +290,9 @@ def tile_nodelstmcell_pa_t_kernel(tc, x_t, h, c, W_ih, W_hh, b_ih, b_hh, out_0, 
         def add_bias(n):
             t, gate = steps[n]
             if t not in sums:
-                sums[t] = work.tile([P, len(ADDED), HID], F32, name="sums", tag="sums", bufs=6)
+                sums[t] = work.tile([P, len(added(t)), HID], F32, name="sums", tag="sums", bufs=6)
             nc.vector.tensor_tensor(
-                out=gate_of(t, gate), in0=gate_ps[n][:], in1=bias_spread[:, ADDED.index(gate), :], op=ALU.add
+                out=gate_of(t, gate), in0=gate_ps[n][:], in1=bias_spread[:, ADDED3.index(gate), :], op=ALU.add
             )
 
         def add_recurrent(n):
@@ -284,18 +300,18 @@ def tile_nodelstmcell_pa_t_kernel(tc, x_t, h, c, W_ih, W_hh, b_ih, b_hh, out_0, 
             nc.vector.tensor_tensor(out=total, in0=rec_ps[n][:], in1=total, op=ALU.add)
 
         def activated_at(t, gate):
-            if gate in ADDED and t >= HEAD_TILES:
-                return at[t, ADDED[-1]] + 1
+            if gate in added(t) and t >= HEAD_TILES:
+                return at[t, added(t)[-1]] + 1
             return at[t, gate] + 1
 
         def activate(t, gate):
-            if gate in TURNED:
+            if gate not in added(t):
                 turned_acts[t, gate] = work.tile([P, HID], F32, name="act%d" % gate, tag="act%d" % gate, bufs=6)
                 func = ACT.Tanh if gate == GATE_G else ACT.Sigmoid
                 nc.scalar.activation(out=turned_acts[t, gate][:], in_=gate_ps[at[t, gate]][:], func=func)
             elif t < HEAD_TILES:
                 nc.scalar.activation(out=gate_of(t, gate), in_=gate_of(t, gate), func=ACT.Sigmoid)
-            elif gate == ADDED[-1]:
+            elif gate == added(t)[-1]:
                 both = sums[t][:].rearrange("p g n -> p (g n)")
                 nc.scalar.activation(out=both, in_=both, func=ACT.Sigmoid)
 
@@ -341,15 +357,19 @@ def tile_nodelstmcell_pa_t_kernel(tc, x_t, h, c, W_ih, W_hh, b_ih, b_hh, out_0, 
         nc.vector.memset(bias_rows[4 * BLOCKS :, :], 0.0)
         nc.sync.dma_start(out=bias_rows[0:BLOCKS, :], in_=b_ih.rearrange("(b n) -> b n", n=P))
         nc.sync.dma_start(out=bias_rows[BLOCKS : 2 * BLOCKS, :], in_=b_hh.rearrange("(b n) -> b n", n=P))
-        load_weights(HEAD_ORDER[0], 2)
-        load_h(0, 0, HEAD_TILES)
+        load_w_ih(HEAD_ORDER[0])
         load_x(0, 0, HEAD_TILES)
-        load_weights(HEAD_ORDER[1], 1)
-        load_weights(HEAD_ORDER[2], 1)
+        load_w_hh(HEAD_ORDER[0], 2)
+        load_h(0, 0, HEAD_TILES)
+        load_w_ih(HEAD_ORDER[1])
+        load_w_hh(HEAD_ORDER[1], 1)
+        load_w_ih(HEAD_ORDER[2])
+        load_w_hh(HEAD_ORDER[2], 1)
         load_h(0, HEAD_TILES)
         load_x(0, HEAD_TILES)
+        load_w_ih(HEAD_ORDER[3])
+        load_w_hh(HEAD_ORDER[3], 1)
         load_cell(0)
-        load_weights(HEAD_ORDER[3], 1)
         load_h(1)
         load_x(1)
         load_cell(1)
@@ -374,80 +394,151 @@ def tile_nodelstmcell_pa_t_kernel(tc, x_t, h, c, W_ih, W_hh, b_ih, b_hh, out_0, 
                 out=warm_ps[:], lhsT=zeros[:, 0:P], rhs=zeros[:], start=(i == 0), stop=(i == WARM_UP - 1)
             )
 
-        biasT_ps = psum.tile([P, P], BF16, name="biasT_ps", tag="bank")
-        nc.tensor.transpose(biasT_ps[:], bias_rows[:], ident_bf16[:])
-        bias_pair = const.tile([P, 2 * BLOCKS], F32)
-        nc.vector.tensor_copy(out=bias_pair[:], in_=biasT_ps[:, 0 : 2 * BLOCKS])
+        both_rows = const.tile([P, BLOCKS], BF16)
+        nc.vector.tensor_tensor(
+            out=both_rows[:], in0=ident_bf16[:, 0:BLOCKS], in1=ident_bf16[:, BLOCKS : 2 * BLOCKS], op=ALU.add
+        )
+        bias_ps = psum.tile([P, BLOCKS], F32, name="bias_ps", tag="bank")
+        nc.tensor.matmul(out=bias_ps[:], lhsT=bias_rows[:], rhs=both_rows[:], start=True, stop=True)
         bias = const.tile([P, BLOCKS], F32)
-        nc.vector.tensor_tensor(out=bias[:], in0=bias_pair[:, 0:BLOCKS], in1=bias_pair[:, BLOCKS : 2 * BLOCKS], op=ALU.add)
-
-        def copy_weights_hh(gate):
-            copy_weights_hh_half(gate, 0, nc.vector.tensor_copy)
-            copy_weights_hh_half(gate, 1, nc.scalar.copy)
-
-        def copy_weights_ih(gate):
-            copy_weights_ih_half(gate, 0, nc.scalar.copy)
-            copy_weights_ih_half(gate, 1, nc.vector.tensor_copy)
-
-        transpose_weights_hh(HEAD_ORDER[0])
-        copy_weights_hh(HEAD_ORDER[0])
-        quantise_weights(HEAD_ORDER[0])
-        transpose_weights_ih(HEAD_ORDER[0])
-        copy_weights_ih(HEAD_ORDER[0])
-        for t in range(HEAD_TILES):
-            for u in range(WORDS_PER_PACK):
-                transpose_h(t, u)
-            transpose_x(t)
-            copy_rows(t)
-            quantise_rows(t)
-
-        bias_spread = const.tile([P, len(ADDED), HID], F32)
-        for g, gate in enumerate(ADDED):
+        nc.vector.tensor_copy(out=bias[:], in_=bias_ps[:])
+        bias_spread = const.tile([P, len(ADDED3), HID], F32)
+        for g, gate in enumerate(ADDED3):
             spread_ps = psum.tile([P, HID], F32, name="spread_ps", tag="bank")
             for a in range(BLOCKS_PER_GATE):
                 blk = gate * BLOCKS_PER_GATE + a
-                nc.tensor.transpose(
-                    spread_ps[:, a * P : (a + 1) * P], bias[:, blk : blk + 1].to_broadcast([P, P]), ident_f32[:]
+                nc.tensor.matmul(
+                    out=spread_ps[:, a * P : (a + 1) * P],
+                    lhsT=both_rows[:, blk : blk + 1].to_broadcast([P, P]),
+                    rhs=bias_rows[:],
+                    start=True,
+                    stop=True,
                 )
             nc.scalar.copy(out=bias_spread[:, g, :], in_=spread_ps[:])
+
+        head_tiles = range(HEAD_TILES)
+
+        def passes_of(gate):
+            for t in head_tiles:
+                for e in range(HALVES):
+                    input_pass(at[t, gate], e)
+
+        def weights_ih(gate):
+            transpose_w_ih(gate)
+            copy_w_ih(gate, nc.scalar.copy)
+
+        def weights_hh(gate):
+            transpose_w_hh(gate, 0)
+            copy_w_hh(gate, 0, nc.vector.tensor_copy)
+            transpose_w_hh(gate, 1)
+            copy_w_hh(gate, 1, nc.scalar.copy)
+
+        def first_rows(t):
+            transpose_x(t)
+            for u in range(WORDS_PER_PACK):
+                transpose_h(t, u)
+            copy_x(t, nc.scalar.copy)
+            copy_h(t)
+
+        first, second, third, fourth = HEAD_ORDER
+        weights_ih(first)
+        weights_hh(first)
+        for t in head_tiles:
+            first_rows(t)
+        quantise_weights(first)
+        for t in head_tiles:
+            quantise_rows(t)
+        weights_ih(second)
+        passes_of(first)
+        for t in head_tiles:
+            add_bias(at[t, first])
+        weights_hh(second)
+        for t in head_tiles:
+            recurrent_rows(at[t, first])
+        quantise_weights(second)
+        for t in head_tiles:
+            add_recurrent(at[t, first])
+        weights_ih(third)
+        passes_of(second)
+        weights_hh(third)
+        for bank in range(BANKS_PER_GATE):
+            turned_bank(0, second, bank)
+            copy_turned_bank(0, second, bank)
+        quantise_weights(third)
+        for t in head_tiles:
+            activate(t, first)
+        first_rows(2)
+        passes_of(third)
+        for t in head_tiles:
+            add_bias(at[t, third])
+        for t in head_tiles:
+            keep_old_cell(t, nc.gpsimd)
+        quantise_rows(2)
+        weights_ih(fourth)
+        for t in head_tiles:
+            for half in range(2):
+                add_turned(at[t, second], half)
+        weights_hh(fourth)
+        for t in head_tiles:
+            recurrent_rows(at[t, third])
+        for t in head_tiles:
+            activate(t, second)
+        quantise_weights(fourth)
+        for t in head_tiles:
+            add_recurrent(at[t, third])
+        first_rows(3)
+        passes_of(fourth)
+        for bank in range(BANKS_PER_GATE):
+            turned_bank(0, fourth, bank)
+            copy_turned_bank(0, fourth, bank)
+        quantise_rows(3)
+        for t in head_tiles:
+            activate(t, third)
+        first_rows(4)
+        for bank in range(BANKS_PER_GATE):
+            turned_bank(1, GATE_I, bank)
+            copy_turned_bank(1, GATE_I, bank)
+        for t in head_tiles:
+            for half in range(2):
+                add_turned(at[t, fourth], half)
+        for t in head_tiles:
+            activate(t, fourth)
+        first_rows(5)
+        quantise_rows(4)
 
         due = {}
 
         def put(step, what, *which):
-            due.setdefault((step, what), []).append(which)
+            due.setdefault((max(step, n_head), what), []).append(which)
 
-        for gate in HEAD_ORDER[1:]:
-            put(at[0, gate] - (3 if gate in TURNED else 2), "weights", gate)
-        for t in range(HEAD_TILES, HEAD_TILES + ROWS_AHEAD):
-            put(t + 1, "first rows", t)
         for t in range(HEAD_TILES + ROWS_AHEAD, N_TILES):
             put(at[t - ROWS_AHEAD, TILE_ORDER[0]], "rows", t)
             put(at[t - ROWS_AHEAD, TILE_ORDER[0]] + 1, "copy of rows", t)
-        for pair in range(N_PAIRS):
-            for gate in TURNED:
+        for pair in range(1, N_PAIRS):
+            for gate in (TURNED[1:] if pair == 1 or THREE(pair) else TURNED):
                 for bank in range(BANKS_PER_GATE):
-                    beside = at[PAIR_TILES * pair - 1 + bank, ADDED[-1]] if pair > 0 else 0
-                    step = max(beside, at[0, gate] - (1 if pair == 0 else 0))
+                    beside = PAIR_TILES * pair - (1 if gate == GATE_G else 2) + bank
+                    step = at[beside, ADDED[-1]] if beside >= HEAD_TILES else n_head
                     put(step, "turned bank", pair, gate, bank)
                     put(step + 1, "copy of turned bank", pair, gate, bank)
-        for n in range(n_steps):
-            if is_step(n, ADDED):
-                if is_step(n - 1, TURNED):
+        for n in range(n_head, n_steps):
+            if is_added(n):
+                if is_turned(n - 1) and n + 1 < n_steps:
                     put(n + 1, "product behind pass 0", n)
-                elif is_step(n - 2, TURNED) and n > n_head:
+                elif is_turned(n - 2):
                     put(n, "product behind pass 1", n)
                 else:
                     put(n, "product behind pass 0", n)
         last_tile = N_TILES - 1
-        for t in range(N_TILES):
+        for t in range(HEAD_TILES, N_TILES):
             put(activated_at(t, GATE_F) + 1, "keep", t)
         for t in range(last_tile):
-            cell_step = at[t, GATE_G] + GATES
+            cell_step = at[t, GATE_G] + 4
             put(cell_step, "cell", t)
             put(cell_step + 2, "tanh", t)
             if t + 1 < last_tile:
-                put(max(at[t + 1, GATE_G] + GATES, cell_step + 2), "hidden", t)
-        put(HEAD_TILES + 1, "load rows", 3)
+                put(cell_step + 4, "hidden", t)
+        put(n_head, "load rows", 3)
         for s in range(1, N_GROUPS):
             first_step = at[TILES * s, TILE_ORDER[0]]
             if s + 3 < N_GROUPS:
@@ -456,10 +547,9 @@ def tile_nodelstmcell_pa_t_kernel(tc, x_t, h, c, W_ih, W_hh, b_ih, b_hh, out_0, 
                 put(first_step, "load cell", s + 1)
 
         everything = slice(0, HID)
-        copied_rows = []
-        first = min(step for step, what in due)
-        for n in range(first, max(step for step, what in due) + 1):
-            running = 0 <= n < n_steps
+        copied_rows = [5]
+        for n in range(n_head, max(step for step, what in due) + 1):
+            running = n < n_steps
             for (s,) in due.get((n, "load rows"), []):
                 load_h(s)
                 load_x(s)
@@ -470,55 +560,40 @@ def tile_nodelstmcell_pa_t_kernel(tc, x_t, h, c, W_ih, W_hh, b_ih, b_hh, out_0, 
                 input_pass(n, 0)
             for (t,) in due.get((n, "rows"), []):
                 transpose_h(t, 0)
-            if is_step(n - 1, TURNED):
+            if is_turned(n - 1):
                 add_turned(n - 1, 0)
             for (m,) in due.get((n, "product behind pass 0"), []):
                 recurrent_rows(m)
-            for (t,) in due.get((n, "first rows"), []):
-                for u in range(WORDS_PER_PACK):
-                    transpose_h(t, u)
-                transpose_x(t)
             if running:
                 input_pass(n, 1)
             for (t,) in due.get((n, "rows"), []):
                 transpose_h(t, 1)
                 transpose_x(t)
-            if is_step(n - 1, TURNED):
+            if is_turned(n - 1):
                 add_turned(n - 1, 1)
             for (m,) in due.get((n, "product behind pass 1"), []):
                 recurrent_rows(m)
             for bank in due.get((n, "turned bank"), []):
                 turned_bank(*bank)
-            for (gate,) in due.get((n, "weights"), []):
-                transpose_weights_hh(gate)
-                transpose_weights_ih(gate)
 
             for (t,) in due.get((n, "cell"), []):
                 write_candidate(t, nc.gpsimd, everything)
-            if is_step(n, ADDED):
+            if is_added(n):
                 add_bias(n)
-            if is_step(n - 1, ADDED):
+            if is_added(n - 1):
                 add_recurrent(n - 1)
             for bank in due.get((n, "copy of turned bank"), []):
                 copy_turned_bank(*bank)
 
-            for (t,) in due.get((n, "first rows"), []):
-                copy_rows(t)
-            for (gate,) in due.get((n, "weights"), []):
-                copy_weights_hh(gate)
-                copy_weights_ih(gate)
             for (t,) in due.get((n, "tanh"), []):
                 tanh_of_new_cell(t, everything)
-            for (t,) in due.get((n, "first rows"), []):
-                quantise_rows(t)
-            if is_step(n - 1, TILE_ORDER):
+            if n_head < n <= n_steps:
                 activate(*steps[n - 1])
             for (t,) in due.get((n, "copy of rows"), []):
-                copy_rows(t)
+                copy_h(t)
+                copy_x(t, nc.vector.tensor_copy if XV(t) else nc.scalar.copy)
                 copied_rows.append(t)
-            for (gate,) in due.get((n, "weights"), []):
-                quantise_weights(gate)
-            if (n, "cell") in due or (n, "hidden") in due:
+            if n == n_head or (n, "cell") in due or (n, "hidden") in due:
                 while copied_rows:
                     quantise_rows(copied_rows.pop(0))
             for (t,) in due.get((n, "hidden"), []):

@@ -20,8 +20,11 @@ ADDED3 = (GATE_F, GATE_O, GATE_I)
 THREE = lambda pair: False
 ONV = lambda pair, gate, bank: gate == GATE_I and bank == 1
 XV = lambda t: t % 2 == 0
+HV = lambda t: False
+GH = lambda t: t in ()
 TURNED = (GATE_I, GATE_G)
 TILE_ORDER = ADDED + TURNED
+LAST_ORDER = (GATE_F, GATE_O, GATE_I, GATE_G)
 HEAD_ORDER = (GATE_F, GATE_I, GATE_O, GATE_G)
 HEAD_TILES = 2
 TILES = 4
@@ -58,7 +61,9 @@ def tile_nodelstmcell_pa_t_kernel(tc, x_t, h, c, W_ih, W_hh, b_ih, b_hh, out_0, 
 
     steps = [(t, gate) for gate in HEAD_ORDER for t in range(HEAD_TILES)]
     n_head = len(steps)
-    steps += [(t, gate) for t in range(HEAD_TILES, N_TILES) for gate in TILE_ORDER]
+    last_tile = N_TILES - 1
+    for t in range(HEAD_TILES, N_TILES):
+        steps += [(t, gate) for gate in (LAST_ORDER if t == last_tile else TILE_ORDER)]
     n_steps = len(steps)
     at = {step: n for n, step in enumerate(steps)}
 
@@ -127,14 +132,17 @@ def tile_nodelstmcell_pa_t_kernel(tc, x_t, h, c, W_ih, W_hh, b_ih, b_hh, out_0, 
             for a in range(0, BLOCKS_PER_GATE, piece):
                 nc.sync.dma_start(out=w_hh_raw[gate][:, a : a + piece, :], in_=source[:, a : a + piece, :])
 
+        def transpose_w_hh_block(gate, blk, u):
+            half, a = divmod(blk, 2)
+            if (gate, half) not in wT_ps:
+                wT_ps[gate, half] = psum.tile([P, 2, WORDS_PER_PACK, P], F32, name="w_hh_ps", tag="bank")
+            raw_words = w_hh_raw[gate][:, blk, :].bitcast(F32)
+            nc.tensor.transpose(wT_ps[gate, half][:, a, u, :], raw_words[:, u:H_WORDS:WORDS_PER_PACK], ident_f32[:])
+
         def transpose_w_hh(gate, half):
-            wT_ps[gate, half] = psum.tile([P, 2, WORDS_PER_PACK, P], F32, name="w_hh_ps", tag="bank")
             for a in range(2):
-                raw_words = w_hh_raw[gate][:, 2 * half + a, :].bitcast(F32)
                 for u in range(WORDS_PER_PACK):
-                    nc.tensor.transpose(
-                        wT_ps[gate, half][:, a, u, :], raw_words[:, u:H_WORDS:WORDS_PER_PACK], ident_f32[:]
-                    )
+                    transpose_w_hh_block(gate, 2 * half + a, u)
 
         def transpose_w_ih(gate):
             wT_ps[gate, "ih"] = psum.tile([P, HID], F32, name="w_ih_ps", tag="bank")
@@ -182,9 +190,9 @@ def tile_nodelstmcell_pa_t_kernel(tc, x_t, h, c, W_ih, W_hh, b_ih, b_hh, out_0, 
             x_words = x_in[s][:].bitcast(F32)
             nc.tensor.transpose(words_ps[t][:, H_WORDS:], x_words[:, j * X_WORDS : (j + 1) * X_WORDS], ident_f32[:])
 
-        def copy_h(t):
+        def copy_h(t, copy_out=nc.scalar.copy):
             h_grouped[t] = work.tile([P, P * PACK], BF16, name="h_grouped", tag="h_grouped", align_bytes=64)
-            nc.scalar.copy(
+            copy_out(
                 out=h_grouped[t][:].bitcast(F32).rearrange("p (r u) -> p r u", u=WORDS_PER_PACK),
                 in_=words_ps[t][:, 0:H_WORDS].rearrange("p (u r) -> p r u", u=WORDS_PER_PACK),
             )
@@ -300,7 +308,7 @@ def tile_nodelstmcell_pa_t_kernel(tc, x_t, h, c, W_ih, W_hh, b_ih, b_hh, out_0, 
             nc.vector.tensor_tensor(out=total, in0=rec_ps[n][:], in1=total, op=ALU.add)
 
         def activated_at(t, gate):
-            if gate in added(t) and t >= HEAD_TILES:
+            if gate in added(t) and HEAD_TILES <= t < last_tile:
                 return at[t, added(t)[-1]] + 1
             return at[t, gate] + 1
 
@@ -309,7 +317,7 @@ def tile_nodelstmcell_pa_t_kernel(tc, x_t, h, c, W_ih, W_hh, b_ih, b_hh, out_0, 
                 turned_acts[t, gate] = work.tile([P, HID], F32, name="act%d" % gate, tag="act%d" % gate, bufs=6)
                 func = ACT.Tanh if gate == GATE_G else ACT.Sigmoid
                 nc.scalar.activation(out=turned_acts[t, gate][:], in_=gate_ps[at[t, gate]][:], func=func)
-            elif t < HEAD_TILES:
+            elif t < HEAD_TILES or t == last_tile:
                 nc.scalar.activation(out=gate_of(t, gate), in_=gate_of(t, gate), func=ACT.Sigmoid)
             elif gate == added(t)[-1]:
                 both = sums[t][:].rearrange("p g n -> p (g n)")
@@ -341,11 +349,11 @@ def tile_nodelstmcell_pa_t_kernel(tc, x_t, h, c, W_ih, W_hh, b_ih, b_hh, out_0, 
                 tanh_c[t] = work.tile([P, HID], F32, name="tanh_c", tag="tanh_c")
             nc.scalar.activation(out=tanh_c[t][:, cols], in_=c_new[t][:, cols], func=ACT.Tanh)
 
-        def new_hidden(t, cols):
+        def new_hidden(t, cols, engine=nc.vector):
             s, j = divmod(t, TILES)
             if t not in h_new:
                 h_new[t] = work.tile([P, HID], F32, name="h_new", tag="h_new")
-            nc.vector.tensor_tensor(
+            engine.tensor_tensor(
                 out=h_new[t][:, cols], in0=gate_of(t, GATE_O)[:, cols], in1=tanh_c[t][:, cols], op=ALU.mult
             )
             nc.sync.dma_start(out=h_next_rows[s, j][:, cols], in_=h_new[t][:, cols])
@@ -418,18 +426,23 @@ def tile_nodelstmcell_pa_t_kernel(tc, x_t, h, c, W_ih, W_hh, b_ih, b_hh, out_0, 
 
         head_tiles = range(HEAD_TILES)
 
-        def passes_of(gate):
+        def passes_of(gate, after=None):
             for t in head_tiles:
                 for e in range(HALVES):
                     input_pass(at[t, gate], e)
+                    if after is not None:
+                        transpose_w_hh_block(after, t, e)
+            if after is not None:
+                copy_w_hh(after, 0, nc.vector.tensor_copy)
 
         def weights_ih(gate):
             transpose_w_ih(gate)
             copy_w_ih(gate, nc.scalar.copy)
 
         def weights_hh(gate):
-            transpose_w_hh(gate, 0)
-            copy_w_hh(gate, 0, nc.vector.tensor_copy)
+            if (gate, 0) not in wT_ps:
+                transpose_w_hh(gate, 0)
+                copy_w_hh(gate, 0, nc.vector.tensor_copy)
             transpose_w_hh(gate, 1)
             copy_w_hh(gate, 1, nc.scalar.copy)
 
@@ -449,7 +462,7 @@ def tile_nodelstmcell_pa_t_kernel(tc, x_t, h, c, W_ih, W_hh, b_ih, b_hh, out_0, 
         for t in head_tiles:
             quantise_rows(t)
         weights_ih(second)
-        passes_of(first)
+        passes_of(first, second)
         for t in head_tiles:
             add_bias(at[t, first])
         weights_hh(second)
@@ -459,7 +472,7 @@ def tile_nodelstmcell_pa_t_kernel(tc, x_t, h, c, W_ih, W_hh, b_ih, b_hh, out_0, 
         for t in head_tiles:
             add_recurrent(at[t, first])
         weights_ih(third)
-        passes_of(second)
+        passes_of(second, third)
         weights_hh(third)
         for bank in range(BANKS_PER_GATE):
             turned_bank(0, second, bank)
@@ -468,7 +481,7 @@ def tile_nodelstmcell_pa_t_kernel(tc, x_t, h, c, W_ih, W_hh, b_ih, b_hh, out_0, 
         for t in head_tiles:
             activate(t, first)
         first_rows(2)
-        passes_of(third)
+        passes_of(third, fourth)
         for t in head_tiles:
             add_bias(at[t, third])
         for t in head_tiles:
@@ -529,15 +542,14 @@ def tile_nodelstmcell_pa_t_kernel(tc, x_t, h, c, W_ih, W_hh, b_ih, b_hh, out_0, 
                     put(n, "product behind pass 1", n)
                 else:
                     put(n, "product behind pass 0", n)
-        last_tile = N_TILES - 1
         for t in range(HEAD_TILES, N_TILES):
             put(activated_at(t, GATE_F) + 1, "keep", t)
         for t in range(last_tile):
-            cell_step = at[t, GATE_G] + 4
+            cell_step = at[t, GATE_G] + (4 if t < last_tile - 1 else 4)
             put(cell_step, "cell", t)
-            put(cell_step + 2, "tanh", t)
+            put(cell_step + (2 if t < last_tile - 1 else 2), "tanh", t)
             if t + 1 < last_tile:
-                put(cell_step + 4, "hidden", t)
+                put(cell_step + (4 if t < last_tile - 2 else 3), "hidden", t)
         put(n_head, "load rows", 3)
         for s in range(1, N_GROUPS):
             first_step = at[TILES * s, TILE_ORDER[0]]
@@ -587,17 +599,19 @@ def tile_nodelstmcell_pa_t_kernel(tc, x_t, h, c, W_ih, W_hh, b_ih, b_hh, out_0, 
 
             for (t,) in due.get((n, "tanh"), []):
                 tanh_of_new_cell(t, everything)
-            if n_head < n <= n_steps:
+            if n_head < n <= n_steps and steps[n - 1] != (last_tile, GATE_O):
                 activate(*steps[n - 1])
+            if n == n_steps:
+                activate(last_tile, GATE_O)
             for (t,) in due.get((n, "copy of rows"), []):
-                copy_h(t)
+                copy_h(t, nc.vector.tensor_copy if HV(t) else nc.scalar.copy)
                 copy_x(t, nc.vector.tensor_copy if XV(t) else nc.scalar.copy)
                 copied_rows.append(t)
             if n == n_head or (n, "cell") in due or (n, "hidden") in due:
                 while copied_rows:
                     quantise_rows(copied_rows.pop(0))
             for (t,) in due.get((n, "hidden"), []):
-                new_hidden(t, everything)
+                new_hidden(t, everything, nc.gpsimd if GH(t) else nc.vector)
             for (t,) in due.get((n, "cell"), []):
                 new_cell(t, everything)
             for (t,) in due.get((n, "keep"), []):
@@ -606,10 +620,10 @@ def tile_nodelstmcell_pa_t_kernel(tc, x_t, h, c, W_ih, W_hh, b_ih, b_hh, out_0, 
         halves = [slice(i * HID // 2, (i + 1) * HID // 2) for i in range(2)]
         for cols in halves:
             write_candidate(last_tile, nc.vector, cols)
-        new_hidden(last_tile - 1, everything)
         for cols in halves:
             new_cell(last_tile, cols)
         for cols in halves:
             tanh_of_new_cell(last_tile, cols)
+        new_hidden(last_tile - 1, everything, nc.vector)
         for cols in halves:
             new_hidden(last_tile, cols)

@@ -18,7 +18,7 @@ GATE_I, GATE_F, GATE_G, GATE_O = 0, 1, 2, 3
 ADDED = (GATE_F, GATE_O)
 ADDED3 = (GATE_F, GATE_O, GATE_I)
 THREE = lambda pair: False
-ONV = lambda pair, gate, bank: gate == GATE_I and bank == 1
+ONV = lambda pair, gate, bank: gate == GATE_I and bank == 1 or pair == 0 and bank == 0
 XV = lambda t: t % 2 == 0
 HV = lambda t: False
 GH = lambda t: t in ()
@@ -537,7 +537,7 @@ def tile_nodelstmcell_pa_t_kernel(tc, x_t, h, c, W_ih, W_hh, b_ih, b_hh, out_0, 
         for n in range(n_head, n_steps):
             if is_added(n):
                 if is_turned(n - 1) and n + 1 < n_steps:
-                    put(n + 1, "product behind pass 0", n)
+                    put(n + 1, "product behind pass 1", n)
                 elif is_turned(n - 2):
                     put(n, "product behind pass 1", n)
                 else:

@@ -18,7 +18,7 @@ GATE_I, GATE_F, GATE_G, GATE_O = 0, 1, 2, 3
 ADDED = (GATE_F, GATE_O)
 ADDED3 = (GATE_F, GATE_O, GATE_I)
 THREE = lambda pair: False
-ONV = lambda pair, gate, bank: gate == GATE_I and bank == 1 or pair == 0 and bank == 0
+ONV = lambda pair, gate, bank: gate == GATE_I and bank == 1
 XV = lambda t: t % 2 == 0
 HV = lambda t: False
 GH = lambda t: t in ()
@@ -264,6 +264,31 @@ def tile_nodelstmcell_pa_t_kernel(tc, x_t, h, c, W_ih, W_hh, b_ih, b_hh, out_0, 
                 rhs=w_ih_T[:, e, gate * HID : (gate + 1) * HID],
                 start=(e == 0),
                 stop=(e == HALVES - 1 and gate in added(t)),
+            )
+
+        def input_half(n, part, e):
+            t, gate = steps[n]
+            if part == 0 and e == 0:
+                gate_ps[n] = psum.tile([P, HID], F32, name="gate_ps", tag="bank")
+            cols = slice(part * HID // 2, (part + 1) * HID // 2)
+            nc.tensor.matmul(
+                out=gate_ps[n][:, cols],
+                lhsT=x_T[t][:].bitcast(BF16)[:, e:IN_DIM:HALVES],
+                rhs=w_ih_T[:, e, gate * HID + cols.start : gate * HID + cols.stop],
+                start=(e == 0),
+                stop=(e == HALVES - 1),
+            )
+
+        def add_turned_block(n, a):
+            t, gate = steps[n]
+            pair, j = divmod(t, PAIR_TILES)
+            nc.tensor.matmul(
+                out=gate_ps[n][:, a * P : (a + 1) * P],
+                lhsT=rec_T[pair, gate][:, a, j * P : (j + 1) * P],
+                rhs=ident_f32[:],
+                is_transpose=True,
+                start=False,
+                stop=(a == BLOCKS_PER_GATE - 1),
             )
 
         def add_turned(n, half):
@@ -568,20 +593,35 @@ def tile_nodelstmcell_pa_t_kernel(tc, x_t, h, c, W_ih, W_hh, b_ih, b_hh, out_0, 
             for (s,) in due.get((n, "load cell"), []):
                 load_cell(s)
 
-            if running:
+            split = running and steps[n][1] == GATE_F and n > n_head
+            if split:
+                rows_now = due.get((n, "rows"), [])
+                k = 0
+                for part in range(2):
+                    for e in range(HALVES):
+                        input_half(n, part, e)
+                        for (t,) in rows_now:
+                            if k < 2:
+                                transpose_h(t, k)
+                            elif k == 2:
+                                transpose_x(t)
+                        if is_turned(n - 1):
+                            add_turned_block(n - 1, k)
+                        k += 1
+            if running and not split:
                 input_pass(n, 0)
-            for (t,) in due.get((n, "rows"), []):
+            for (t,) in due.get((n, "rows"), []) if not split else []:
                 transpose_h(t, 0)
-            if is_turned(n - 1):
+            if is_turned(n - 1) and not split:
                 add_turned(n - 1, 0)
             for (m,) in due.get((n, "product behind pass 0"), []):
                 recurrent_rows(m)
-            if running:
+            if running and not split:
                 input_pass(n, 1)
-            for (t,) in due.get((n, "rows"), []):
+            for (t,) in due.get((n, "rows"), []) if not split else []:
                 transpose_h(t, 1)
                 transpose_x(t)
-            if is_turned(n - 1):
+            if is_turned(n - 1) and not split:
                 add_turned(n - 1, 1)
             for (m,) in due.get((n, "product behind pass 1"), []):
                 recurrent_rows(m)

@@ -20,7 +20,7 @@ ADDED3 = (GATE_F, GATE_O, GATE_I)
 THREE = lambda pair: False
 ONV = lambda pair, gate, bank: gate == GATE_I and bank == 1
 XV = lambda t: t % 2 == 0
-HV = lambda t: False
+HV = lambda t: t % 4 == 0
 GH = lambda t: t in ()
 TURNED = (GATE_I, GATE_G)
 TILE_ORDER = ADDED + TURNED

@@ -395,7 +395,7 @@ def tile_nodelstmcell_pa_t_kernel(tc, x_t, h, c, W_ih, W_hh, b_ih, b_hh, out_0, 
         load_w_hh(HEAD_ORDER[0], 2)
         load_h(0, 0, HEAD_TILES)
         load_w_ih(HEAD_ORDER[1])
-        load_w_hh(HEAD_ORDER[1], 1)
+        load_w_hh(HEAD_ORDER[1], 2)
         load_w_ih(HEAD_ORDER[2])
         load_w_hh(HEAD_ORDER[2], 1)
         load_h(0, HEAD_TILES)
@@ -451,12 +451,16 @@ def tile_nodelstmcell_pa_t_kernel(tc, x_t, h, c, W_ih, W_hh, b_ih, b_hh, out_0, 
 
         head_tiles = range(HEAD_TILES)
 
-        def passes_of(gate, after=None):
+        def passes_of(gate, after=None, rows=()):
+            rows = list(rows)
             for t in head_tiles:
                 for e in range(HALVES):
                     input_pass(at[t, gate], e)
                     if after is not None:
                         transpose_w_hh_block(after, t, e)
+                    if rows:
+                        for f, *args in rows.pop(0):
+                            f(*args)
             if after is not None:
                 copy_w_hh(after, 0, nc.vector.tensor_copy)
 
@@ -525,23 +529,27 @@ def tile_nodelstmcell_pa_t_kernel(tc, x_t, h, c, W_ih, W_hh, b_ih, b_hh, out_0, 
         for t in head_tiles:
             add_recurrent(at[t, third])
         first_rows(3)
-        passes_of(fourth)
+        passes_of(fourth, None, [[(transpose_h, 4, 0)], [(transpose_h, 4, 1), (transpose_x, 4)], [(transpose_h, 5, 0)]])
+        copy_x(4, nc.scalar.copy)
+        copy_h(4)
         for bank in range(BANKS_PER_GATE):
             turned_bank(0, fourth, bank)
             copy_turned_bank(0, fourth, bank)
         quantise_rows(3)
         for t in head_tiles:
             activate(t, third)
-        first_rows(4)
         for bank in range(BANKS_PER_GATE):
             turned_bank(1, GATE_I, bank)
             copy_turned_bank(1, GATE_I, bank)
+        transpose_h(5, 1)
+        transpose_x(5)
+        copy_x(5, nc.scalar.copy)
+        copy_h(5)
         for t in head_tiles:
             for half in range(2):
                 add_turned(at[t, fourth], half)
         for t in head_tiles:
             activate(t, fourth)
-        first_rows(5)
         quantise_rows(4)
 
         due = {}

@@ -18,7 +18,7 @@ GATE_I, GATE_F, GATE_G, GATE_O = 0, 1, 2, 3
 ADDED = (GATE_F, GATE_O)
 ADDED3 = (GATE_F, GATE_O, GATE_I)
 THREE = lambda pair: False
-ONV = lambda pair, gate, bank: gate == GATE_I and bank == 1
+ONV = lambda pair, gate, bank: gate == GATE_I and bank == 1 or pair == 0 and gate == GATE_G and bank == 0
 XV = lambda t: t % 2 == 0
 HV = lambda t: t % 4 == 0
 GH = lambda t: t in ()
@@ -484,9 +484,14 @@ def tile_nodelstmcell_pa_t_kernel(tc, x_t, h, c, W_ih, W_hh, b_ih, b_hh, out_0, 
 
         first, second, third, fourth = HEAD_ORDER
         weights_ih(first)
+        for t in head_tiles:
+            transpose_x(t)
+            copy_x(t, nc.vector.tensor_copy)
         weights_hh(first)
         for t in head_tiles:
-            first_rows(t)
+            for u in range(WORDS_PER_PACK):
+                transpose_h(t, u)
+            copy_h(t)
         quantise_weights(first)
         for t in head_tiles:
             quantise_rows(t)
@@ -526,16 +531,16 @@ def tile_nodelstmcell_pa_t_kernel(tc, x_t, h, c, W_ih, W_hh, b_ih, b_hh, out_0, 
         for t in head_tiles:
             activate(t, second)
         quantise_weights(fourth)
-        for t in head_tiles:
-            add_recurrent(at[t, third])
         first_rows(3)
+        add_recurrent(at[0, third])
+        quantise_rows(3)
+        add_recurrent(at[1, third])
         passes_of(fourth, None, [[(transpose_h, 4, 0)], [(transpose_h, 4, 1), (transpose_x, 4)], [(transpose_h, 5, 0)]])
         copy_x(4, nc.scalar.copy)
         copy_h(4)
         for bank in range(BANKS_PER_GATE):
             turned_bank(0, fourth, bank)
             copy_turned_bank(0, fourth, bank)
-        quantise_rows(3)
         for t in head_tiles:
             activate(t, third)
         for bank in range(BANKS_PER_GATE):

@@ -204,8 +204,8 @@ def tile_nodelstmcell_pa_t_kernel(tc, x_t, h, c, W_ih, W_hh, b_ih, b_hh, out_0, 
         def quantise_rows(t):
             s, j = divmod(t, TILES)
             if j == 0:
-                h_codes[s] = operands.tile([P, GROUP_ROWS], U32, name="h_codes", tag="h_codes", align_bytes=64)
-                h_scales[s] = operands.tile([P, GROUP_ROWS], U8, name="h_scales", tag="h_scales", align_bytes=64)
+                h_codes[s] = operands.tile([P, GROUP_ROWS], U32, name="h_codes", tag="h_codes", align_bytes=256)
+                h_scales[s] = operands.tile([P, GROUP_ROWS], U8, name="h_scales", tag="h_scales", align_bytes=256)
             cols = slice(j * P, (j + 1) * P)
             nc.vector.quantize_mx(
                 out=h_codes[s][:, cols].bitcast(FP8X4), scales=h_scales[s][:, cols], in_=h_grouped[t][:]
@@ -417,8 +417,8 @@ def tile_nodelstmcell_pa_t_kernel(tc, x_t, h, c, W_ih, W_hh, b_ih, b_hh, out_0, 
         make_identity(nc, ident_f32[:])
         ident_bf16 = const.tile([P, P], BF16)
         make_identity(nc, ident_bf16[:])
-        w_codes = const.tile([P, GATES * HID], U32, align_bytes=64)
-        w_scales = const.tile([P, GATES * HID], U8, align_bytes=64)
+        w_codes = const.tile([P, GATES * HID], U32, align_bytes=256)
+        w_scales = const.tile([P, GATES * HID], U8, align_bytes=256)
         w_ih_T = const.tile([P, HALVES, GATES * HID], BF16)
 
         warm_ps = psum.tile([P, HID], F32, name="warm_ps", tag="bank")

from contextlib import ExitStack

import concourse.mybir as mybir
from concourse.masks import make_identity

F32 = mybir.dt.float32
BF16 = mybir.dt.bfloat16
U32 = mybir.dt.uint32
U8 = mybir.dt.uint8
FP8X4 = mybir.dt.float8_e4m3fn_x4
ACT = mybir.ActivationFunctionType
ALU = mybir.AluOpType

P = 128
BATCH, IN_DIM, HID = 4096, 256, 512
GATES = 4
GATE_I, GATE_F, GATE_G, GATE_O = 0, 1, 2, 3
ADDED = (GATE_F, GATE_O)
ADDED3 = (GATE_F, GATE_O, GATE_I)
THREE = lambda pair: False
ONV = lambda pair, gate, bank: gate == GATE_I and bank == 1 or pair == 0 and gate == GATE_G and bank == 0
XV = lambda t: t % 2 == 0
HV = lambda t: t % 4 == 0
GH = lambda t: t in ()
TURNED = (GATE_I, GATE_G)
TILE_ORDER = ADDED + TURNED
LAST_ORDER = (GATE_F, GATE_O, GATE_I, GATE_G)
HEAD_ORDER = (GATE_F, GATE_I, GATE_O, GATE_G)
HEAD_TILES = 2
TILES = 4
GROUP_ROWS = TILES * P
N_GROUPS = BATCH // GROUP_ROWS
N_TILES = N_GROUPS * TILES
PAIR_TILES = 2
PAIR_ROWS = PAIR_TILES * P
N_PAIRS = N_TILES // PAIR_TILES
BLOCKS_PER_GATE = HID // P
BLOCKS = GATES * BLOCKS_PER_GATE
BANK_BLOCKS = 2
BANKS_PER_GATE = BLOCKS_PER_GATE // BANK_BLOCKS
HALVES = 2
H_WORDS = HID // HALVES
X_WORDS = IN_DIM // HALVES
WORDS_PER_PACK = H_WORDS // P
PACK = 4
ROWS_AHEAD = 4
PSUM_BANKS = 8
WARM_UP = 3

FLOPS = 2 * BATCH * GATES * HID * (IN_DIM + HID)


def tile_nodelstmcell_pa_t_kernel(tc, x_t, h, c, W_ih, W_hh, b_ih, b_hh, out_0, out_1):
    nc = tc.nc

    x_rows = x_t.rearrange("(s p j) k -> s p (j k)", p=P, j=TILES)
    h_rows = h.rearrange("(s p j) k -> s p (j k)", p=P, j=TILES)
    c_rows = c.rearrange("(s p j) n -> s p (j n)", p=P, j=TILES)
    h_next_rows = out_0.rearrange("(s p j) n -> s j p n", p=P, j=TILES)
    c_next_rows = out_1.rearrange("(s p j) n -> s j p n", p=P, j=TILES)

    steps = [(t, gate) for gate in HEAD_ORDER for t in range(HEAD_TILES)]
    n_head = len(steps)
    last_tile = N_TILES - 1
    for t in range(HEAD_TILES, N_TILES):
        steps += [(t, gate) for gate in (LAST_ORDER if t == last_tile else TILE_ORDER)]
    n_steps = len(steps)
    at = {step: n for n, step in enumerate(steps)}

    def added(t):
        return ADDED3 if THREE(t // PAIR_TILES) else ADDED

    def is_added(n):
        return n_head <= n < n_steps and steps[n][1] in added(steps[n][0])

    def is_turned(n):
        return n_head <= n < n_steps and steps[n][1] not in added(steps[n][0])

    with ExitStack() as stack:
        const = stack.enter_context(tc.tile_pool(name="const", bufs=1))
        setup = stack.enter_context(tc.tile_pool(name="setup", bufs=GATES))
        rows = stack.enter_context(tc.tile_pool(name="rows", bufs=3))
        operands = stack.enter_context(tc.tile_pool(name="operands", bufs=3))
        work = stack.enter_context(tc.tile_pool(name="work", bufs=4))
        psum = stack.enter_context(tc.psum_pool(name="psum", bufs=PSUM_BANKS))
        stack.enter_context(tc.manual_schedule())

        x_in, h_in, c_in = {}, {}, {}
        h_codes, h_scales = {}, {}
        x_T = {}
        words_ps = {}
        h_grouped = {}
        rec_T = {}
        recT_ps = {}
        gate_ps = {}
        rec_ps = {}
        sums = {}
        turned_acts = {}
        kept, written = {}, {}
        c_new, tanh_c, h_new = {}, {}, {}
        w_hh_raw, w_ih_raw, w_grouped, wT_ps = {}, {}, {}, {}

        def gate_of(t, gate):
            return sums[t][:, ADDED3.index(gate), :] if gate in added(t) else turned_acts[t, gate][:]

        def load_h(s, first=0, last=TILES):
            if s not in h_in:
                h_in[s] = rows.tile([P, TILES * HID], BF16, name="h_in", tag="h_in")
            cols = slice(first * HID, last * HID)
            nc.sync.dma_start(out=h_in[s][:, cols], in_=h_rows[s][:, cols])

        def load_x(s, first=0, last=TILES):
            if s not in x_in:
                x_in[s] = rows.tile([P, TILES * IN_DIM], BF16, name="x_in", tag="x_in")
            cols = slice(first * IN_DIM, last * IN_DIM)
            nc.sync.dma_start(out=x_in[s][:, cols], in_=x_rows[s][:, cols])

        def load_cell(s):
            c_in[s] = rows.tile([P, TILES * HID], BF16, name="c_in", tag="c_in")
            nc.sync.dma_start(out=c_in[s][:], in_=c_rows[s])

        def load_w_ih(gate):
            gate_rows = slice(gate * HID, (gate + 1) * HID)
            w_ih_raw[gate] = setup.tile([P, BLOCKS_PER_GATE, IN_DIM], BF16, name="w_ih_raw", tag="w_ih_raw")
            nc.sync.dma_start(out=w_ih_raw[gate][:], in_=W_ih[gate_rows, :].rearrange("(a p) k -> p a k", p=P))

        def load_w_hh(gate, pieces):
            gate_rows = slice(gate * HID, (gate + 1) * HID)
            w_hh_raw[gate] = setup.tile([P, BLOCKS_PER_GATE, HID], BF16, name="w_hh_raw", tag="w_hh_raw")
            source = W_hh[gate_rows, :].rearrange("(a p) k -> p a k", p=P)
            piece = BLOCKS_PER_GATE // pieces
            for a in range(0, BLOCKS_PER_GATE, piece):
                nc.sync.dma_start(out=w_hh_raw[gate][:, a : a + piece, :], in_=source[:, a : a + piece, :])

        def transpose_w_hh_block(gate, blk, u):
            half, a = divmod(blk, 2)
            if (gate, half) not in wT_ps:
                wT_ps[gate, half] = psum.tile([P, 2, WORDS_PER_PACK, P], F32, name="w_hh_ps", tag="bank")
            raw_words = w_hh_raw[gate][:, blk, :].bitcast(F32)
            nc.tensor.transpose(wT_ps[gate, half][:, a, u, :], raw_words[:, u:H_WORDS:WORDS_PER_PACK], ident_f32[:])

        def transpose_w_hh(gate, half):
            for a in range(2):
                for u in range(WORDS_PER_PACK):
                    transpose_w_hh_block(gate, 2 * half + a, u)

        def transpose_w_ih(gate):
            wT_ps[gate, "ih"] = psum.tile([P, HID], F32, name="w_ih_ps", tag="bank")
            for a in range(BLOCKS_PER_GATE):
                nc.tensor.transpose(
                    wT_ps[gate, "ih"][:, a * P : (a + 1) * P], w_ih_raw[gate][:, a, :].bitcast(F32), ident_f32[:]
                )

        def copy_w_hh(gate, half, copy_out):
            if gate not in w_grouped:
                w_grouped[gate] = setup.tile(
                    [P, HID * PACK], BF16, name="w_grouped", tag="w_grouped", bufs=2, align_bytes=64
                )
            grouped_words = w_grouped[gate][:].bitcast(F32).rearrange(
                "p (a n u) -> p a n u", a=BLOCKS_PER_GATE, u=WORDS_PER_PACK
            )
            copy_out(
                out=grouped_words[:, 2 * half : 2 * half + 2, :, :],
                in_=wT_ps[gate, half][:].rearrange("p a u n -> p a n u"),
            )

        def copy_w_ih(gate, copy_out):
            both = wT_ps[gate, "ih"][:].bitcast(BF16).rearrange("p (n e) -> p e n", e=HALVES)
            for e in range(HALVES):
                copy_out(out=w_ih_T[:, e, gate * HID : (gate + 1) * HID], in_=both[:, e, :])

        def quantise_weights(gate):
            cols = slice(gate * HID, (gate + 1) * HID)
            nc.vector.quantize_mx(out=w_codes[:, cols].bitcast(FP8X4), scales=w_scales[:, cols], in_=w_grouped[gate][:])

        def transpose_h(t, u):
            s, j = divmod(t, TILES)
            if t not in words_ps:
                words_ps[t] = psum.tile([P, H_WORDS + X_WORDS], F32, name="words_ps", tag="bank")
            nc.tensor.transpose(
                words_ps[t][:, u * P : (u + 1) * P],
                h_in[s][:].bitcast(F32)[:, j * H_WORDS + u : (j + 1) * H_WORDS : WORDS_PER_PACK],
                ident_f32[:],
            )

        def transpose_x(t):
            s, j = divmod(t, TILES)
            if t not in words_ps:
                words_ps[t] = psum.tile([P, H_WORDS + X_WORDS], F32, name="words_ps", tag="bank")
            x_words = x_in[s][:].bitcast(F32)
            nc.tensor.transpose(words_ps[t][:, H_WORDS:], x_words[:, j * X_WORDS : (j + 1) * X_WORDS], ident_f32[:])

        def copy_h(t, copy_out=nc.scalar.copy):
            h_grouped[t] = work.tile([P, P * PACK], BF16, name="h_grouped", tag="h_grouped", align_bytes=64)
            copy_out(
                out=h_grouped[t][:].bitcast(F32).rearrange("p (r u) -> p r u", u=WORDS_PER_PACK),
                in_=words_ps[t][:, 0:H_WORDS].rearrange("p (u r) -> p r u", u=WORDS_PER_PACK),
            )

        def copy_x(t, copy_out):
            x_T[t] = operands.tile([P, X_WORDS], F32, name="x_T", tag="x_T", bufs=2 * ROWS_AHEAD)
            copy_out(out=x_T[t][:], in_=words_ps[t][:, H_WORDS:])

        def quantise_rows(t):
            s, j = divmod(t, TILES)
            if j == 0:
                h_codes[s] = operands.tile([P, GROUP_ROWS], U32, name="h_codes", tag="h_codes", align_bytes=256)
                h_scales[s] = operands.tile([P, GROUP_ROWS], U8, name="h_scales", tag="h_scales", align_bytes=256)
            cols = slice(j * P, (j + 1) * P)
            nc.vector.quantize_mx(
                out=h_codes[s][:, cols].bitcast(FP8X4), scales=h_scales[s][:, cols], in_=h_grouped[t][:]
            )

        def turned_bank(pair, gate, bank):
            s, q = divmod(pair, TILES // PAIR_TILES)
            pair_rows = slice(q * PAIR_ROWS, (q + 1) * PAIR_ROWS)
            recT_ps[pair, gate, bank] = psum.tile([P, BANK_BLOCKS, PAIR_ROWS], F32, name="recT_ps", tag="bank")
            for a in range(BANK_BLOCKS):
                blk = gate * BLOCKS_PER_GATE + bank * BANK_BLOCKS + a
                cols = slice(blk * P, (blk + 1) * P)
                nc.tensor.matmul_mx(
                    out=recT_ps[pair, gate, bank][:, a, :],
                    lhsT=w_codes[:, cols].bitcast(FP8X4),
                    lhsT_scale=w_scales[:, cols],
                    rhs=h_codes[s][:, pair_rows].bitcast(FP8X4),
                    rhs_scale=h_scales[s][:, pair_rows],
                    start=True,
                    stop=True,
                )

        def on_vector(pair, gate, bank):
            return ONV(pair, gate, bank)

        def copy_turned_bank(pair, gate, bank):
            if (pair, gate) not in rec_T:
                rec_T[pair, gate] = operands.tile(
                    [P, BLOCKS_PER_GATE, PAIR_ROWS], F32, name="rec_T", tag="rec_T%d" % gate
                )
            first = bank * BANK_BLOCKS
            blk = gate * BLOCKS_PER_GATE + first
            if on_vector(pair, gate, bank):
                nc.vector.tensor_tensor(
                    out=rec_T[pair, gate][:, first : first + BANK_BLOCKS, :],
                    in0=recT_ps[pair, gate, bank][:],
                    in1=bias[:, blk : blk + BANK_BLOCKS].unsqueeze(2).to_broadcast([P, BANK_BLOCKS, PAIR_ROWS]),
                    op=ALU.add,
                )
            else:
                for a in range(BANK_BLOCKS):
                    nc.scalar.activation(
                        out=rec_T[pair, gate][:, first + a, :],
                        in_=recT_ps[pair, gate, bank][:, a, :],
                        func=ACT.Identity,
                        bias=bias[:, blk + a : blk + a + 1],
                    )

        def input_pass(n, e):
            t, gate = steps[n]
            if e == 0:
                gate_ps[n] = psum.tile([P, HID], F32, name="gate_ps", tag="bank")
            nc.tensor.matmul(
                out=gate_ps[n][:],
                lhsT=x_T[t][:].bitcast(BF16)[:, e:IN_DIM:HALVES],
                rhs=w_ih_T[:, e, gate * HID : (gate + 1) * HID],
                start=(e == 0),
                stop=(e == HALVES - 1 and gate in added(t)),
            )

        def input_half(n, part, e):
            t, gate = steps[n]
            if part == 0 and e == 0:
                gate_ps[n] = psum.tile([P, HID], F32, name="gate_ps", tag="bank")
            cols = slice(part * HID // 2, (part + 1) * HID // 2)
            nc.tensor.matmul(
                out=gate_ps[n][:, cols],
                lhsT=x_T[t][:].bitcast(BF16)[:, e:IN_DIM:HALVES],
                rhs=w_ih_T[:, e, gate * HID + cols.start : gate * HID + cols.stop],
                start=(e == 0),
                stop=(e == HALVES - 1),
            )

        def add_turned_block(n, a):
            t, gate = steps[n]
            pair, j = divmod(t, PAIR_TILES)
            nc.tensor.matmul(
                out=gate_ps[n][:, a * P : (a + 1) * P],
                lhsT=rec_T[pair, gate][:, a, j * P : (j + 1) * P],
                rhs=ident_f32[:],
                is_transpose=True,
                start=False,
                stop=(a == BLOCKS_PER_GATE - 1),
            )

        def add_turned(n, half):
            t, gate = steps[n]
            pair, j = divmod(t, PAIR_TILES)
            for a in range(2 * half, 2 * half + 2):
                nc.tensor.matmul(
                    out=gate_ps[n][:, a * P : (a + 1) * P],
                    lhsT=rec_T[pair, gate][:, a, j * P : (j + 1) * P],
                    rhs=ident_f32[:],
                    is_transpose=True,
                    start=False,
                    stop=(a == BLOCKS_PER_GATE - 1),
                )

        def recurrent_rows(n):
            t, gate = steps[n]
            s, j = divmod(t, TILES)
            tile_rows = slice(j * P, (j + 1) * P)
            cols = slice(gate * HID, (gate + 1) * HID)
            rec_ps[n] = psum.tile([P, HID], F32, name="rec_ps", tag="bank")
            nc.tensor.matmul_mx(
                out=rec_ps[n][:],
                lhsT=h_codes[s][:, tile_rows].bitcast(FP8X4),
                lhsT_scale=h_scales[s][:, tile_rows],
                rhs=w_codes[:, cols].bitcast(FP8X4),
                rhs_scale=w_scales[:, cols],
                start=True,
                stop=True,
            )

        def add_bias(n):
            t, gate = steps[n]
            if t not in sums:
                sums[t] = work.tile([P, len(added(t)), HID], F32, name="sums", tag="sums", bufs=6)
            nc.vector.tensor_tensor(
                out=gate_of(t, gate), in0=gate_ps[n][:], in1=bias_spread[:, ADDED3.index(gate), :], op=ALU.add
            )

        def add_recurrent(n):
            total = gate_of(*steps[n])
            nc.vector.tensor_tensor(out=total, in0=rec_ps[n][:], in1=total, op=ALU.add)

        def activated_at(t, gate):
            if gate in added(t) and HEAD_TILES <= t < last_tile:
                return at[t, added(t)[-1]] + 1
            return at[t, gate] + 1

        def activate(t, gate):
            if gate not in added(t):
                turned_acts[t, gate] = work.tile([P, HID], F32, name="act%d" % gate, tag="act%d" % gate, bufs=6)
                func = ACT.Tanh if gate == GATE_G else ACT.Sigmoid
                nc.scalar.activation(out=turned_acts[t, gate][:], in_=gate_ps[at[t, gate]][:], func=func)
            elif t < HEAD_TILES or t == last_tile:
                nc.scalar.activation(out=gate_of(t, gate), in_=gate_of(t, gate), func=ACT.Sigmoid)
            elif gate == added(t)[-1]:
                both = sums[t][:].rearrange("p g n -> p (g n)")
                nc.scalar.activation(out=both, in_=both, func=ACT.Sigmoid)

        def keep_old_cell(t, engine):
            s, j = divmod(t, TILES)
            kept[t] = work.tile([P, HID], F32, name="kept", tag="kept", bufs=2)
            engine.tensor_tensor(
                out=kept[t][:], in0=gate_of(t, GATE_F), in1=c_in[s][:, j * HID : (j + 1) * HID], op=ALU.mult
            )

        def write_candidate(t, engine, cols):
            if t not in written:
                written[t] = work.tile([P, HID], F32, name="written", tag="written", bufs=2)
            engine.tensor_tensor(
                out=written[t][:, cols], in0=gate_of(t, GATE_I)[:, cols], in1=gate_of(t, GATE_G)[:, cols], op=ALU.mult
            )

        def new_cell(t, cols):
            s, j = divmod(t, TILES)
            if t not in c_new:
                c_new[t] = work.tile([P, HID], F32, name="c_new", tag="c_new")
            nc.vector.tensor_tensor(out=c_new[t][:, cols], in0=kept[t][:, cols], in1=written[t][:, cols], op=ALU.add)
            nc.sync.dma_start(out=c_next_rows[s, j][:, cols], in_=c_new[t][:, cols])

        def tanh_of_new_cell(t, cols):
            if t not in tanh_c:
                tanh_c[t] = work.tile([P, HID], F32, name="tanh_c", tag="tanh_c")
            nc.scalar.activation(out=tanh_c[t][:, cols], in_=c_new[t][:, cols], func=ACT.Tanh)

        def new_hidden(t, cols, engine=nc.vector):
            s, j = divmod(t, TILES)
            if t not in h_new:
                h_new[t] = work.tile([P, HID], F32, name="h_new", tag="h_new")
            engine.tensor_tensor(
                out=h_new[t][:, cols], in0=gate_of(t, GATE_O)[:, cols], in1=tanh_c[t][:, cols], op=ALU.mult
            )
            nc.sync.dma_start(out=h_next_rows[s, j][:, cols], in_=h_new[t][:, cols])

        zeros = const.tile([P, HID], BF16)
        nc.vector.memset(zeros[:], 0.0)
        bias_rows = const.tile([P, P], BF16)
        nc.vector.memset(bias_rows[2 * BLOCKS : 4 * BLOCKS, :], 0.0)
        nc.vector.memset(bias_rows[4 * BLOCKS :, :], 0.0)
        nc.sync.dma_start(out=bias_rows[0:BLOCKS, :], in_=b_ih.rearrange("(b n) -> b n", n=P))
        nc.sync.dma_start(out=bias_rows[BLOCKS : 2 * BLOCKS, :], in_=b_hh.rearrange("(b n) -> b n", n=P))
        load_w_ih(HEAD_ORDER[0])
        load_x(0, 0, HEAD_TILES)
        load_w_hh(HEAD_ORDER[0], 2)
        load_h(0, 0, HEAD_TILES)
        load_w_ih(HEAD_ORDER[1])
        load_w_hh(HEAD_ORDER[1], 2)
        load_w_ih(HEAD_ORDER[2])
        load_w_hh(HEAD_ORDER[2], 1)
        load_h(0, HEAD_TILES)
        load_x(0, HEAD_TILES)
        load_w_ih(HEAD_ORDER[3])
        load_w_hh(HEAD_ORDER[3], 1)
        load_cell(0)
        load_h(1)
        load_x(1)
        load_cell(1)
        load_h(2)
        load_x(2)

        table_input = const.tile([P, 1], F32)
        nc.vector.memset(table_input[:], 0.0)
        nc.scalar.activation(out=table_input[:], in_=table_input[:], func=ACT.Sigmoid)

        ident_f32 = const.tile([P, P], F32)
        make_identity(nc, ident_f32[:])
        ident_bf16 = const.tile([P, P], BF16)
        make_identity(nc, ident_bf16[:])
        w_codes = const.tile([P, GATES * HID], U32, align_bytes=256)
        w_scales = const.tile([P, GATES * HID], U8, align_bytes=256)
        w_ih_T = const.tile([P, HALVES, GATES * HID], BF16)

        warm_ps = psum.tile([P, HID], F32, name="warm_ps", tag="bank")
        for i in range(WARM_UP):
            nc.tensor.matmul(
                out=warm_ps[:], lhsT=zeros[:, 0:P], rhs=zeros[:], start=(i == 0), stop=(i == WARM_UP - 1)
            )

        both_rows = const.tile([P, BLOCKS], BF16)
        nc.vector.tensor_tensor(
            out=both_rows[:], in0=ident_bf16[:, 0:BLOCKS], in1=ident_bf16[:, BLOCKS : 2 * BLOCKS], op=ALU.add
        )
        bias_ps = psum.tile([P, BLOCKS], F32, name="bias_ps", tag="bank")
        nc.tensor.matmul(out=bias_ps[:], lhsT=bias_rows[:], rhs=both_rows[:], start=True, stop=True)
        bias = const.tile([P, BLOCKS], F32)
        nc.vector.tensor_copy(out=bias[:], in_=bias_ps[:])
        bias_spread = const.tile([P, len(ADDED3), HID], F32)
        for g, gate in enumerate(ADDED3):
            spread_ps = psum.tile([P, HID], F32, name="spread_ps", tag="bank")
            for a in range(BLOCKS_PER_GATE):
                blk = gate * BLOCKS_PER_GATE + a
                nc.tensor.matmul(
                    out=spread_ps[:, a * P : (a + 1) * P],
                    lhsT=both_rows[:, blk : blk + 1].to_broadcast([P, P]),
                    rhs=bias_rows[:],
                    start=True,
                    stop=True,
                )
            nc.scalar.copy(out=bias_spread[:, g, :], in_=spread_ps[:])

        head_tiles = range(HEAD_TILES)

        def passes_of(gate, after=None, rows=()):
            rows = list(rows)
            for t in head_tiles:
                for e in range(HALVES):
                    input_pass(at[t, gate], e)
                    if after is not None:
                        transpose_w_hh_block(after, t, e)
                    if rows:
                        for f, *args in rows.pop(0):
                            f(*args)
            if after is not None:
                copy_w_hh(after, 0, nc.vector.tensor_copy)

        def weights_ih(gate):
            transpose_w_ih(gate)
            copy_w_ih(gate, nc.scalar.copy)

        def weights_hh(gate):
            if (gate, 0) not in wT_ps:
                transpose_w_hh(gate, 0)
                copy_w_hh(gate, 0, nc.vector.tensor_copy)
            transpose_w_hh(gate, 1)
            copy_w_hh(gate, 1, nc.scalar.copy)

        def first_rows(t):
            transpose_x(t)
            for u in range(WORDS_PER_PACK):
                transpose_h(t, u)
            copy_x(t, nc.scalar.copy)
            copy_h(t)

        first, second, third, fourth = HEAD_ORDER
        weights_ih(first)
        for t in head_tiles:
            transpose_x(t)
            copy_x(t, nc.vector.tensor_copy)
        weights_hh(first)
        for t in head_tiles:
            for u in range(WORDS_PER_PACK):
                transpose_h(t, u)
            copy_h(t)
        quantise_weights(first)
        for t in head_tiles:
            quantise_rows(t)
        weights_ih(second)
        passes_of(first, second)
        for t in head_tiles:
            add_bias(at[t, first])
        weights_hh(second)
        for t in head_tiles:
            recurrent_rows(at[t, first])
        quantise_weights(second)
        for t in head_tiles:
            add_recurrent(at[t, first])
        weights_ih(third)
        passes_of(second, third)
        weights_hh(third)
        for bank in range(BANKS_PER_GATE):
            turned_bank(0, second, bank)
            copy_turned_bank(0, second, bank)
        quantise_weights(third)
        for t in head_tiles:
            activate(t, first)
        first_rows(2)
        passes_of(third, fourth)
        for t in head_tiles:
            add_bias(at[t, third])
        for t in head_tiles:
            keep_old_cell(t, nc.gpsimd)
        quantise_rows(2)
        weights_ih(fourth)
        for t in head_tiles:
            for half in range(2):
                add_turned(at[t, second], half)
        weights_hh(fourth)
        for t in head_tiles:
            recurrent_rows(at[t, third])
        for t in head_tiles:
            activate(t, second)
        quantise_weights(fourth)
        first_rows(3)
        add_recurrent(at[0, third])
        quantise_rows(3)
        add_recurrent(at[1, third])
        passes_of(fourth, None, [[(transpose_h, 4, 0)], [(transpose_h, 4, 1), (transpose_x, 4)], [(transpose_h, 5, 0)]])
        copy_x(4, nc.scalar.copy)
        copy_h(4)
        for bank in range(BANKS_PER_GATE):
            turned_bank(0, fourth, bank)
            copy_turned_bank(0, fourth, bank)
        for t in head_tiles:
            activate(t, third)
        for bank in range(BANKS_PER_GATE):
            turned_bank(1, GATE_I, bank)
            copy_turned_bank(1, GATE_I, bank)
        transpose_h(5, 1)
        transpose_x(5)
        copy_x(5, nc.scalar.copy)
        copy_h(5)
        for t in head_tiles:
            for half in range(2):
                add_turned(at[t, fourth], half)
        for t in head_tiles:
            activate(t, fourth)
        quantise_rows(4)

        due = {}

        def put(step, what, *which):
            due.setdefault((max(step, n_head), what), []).append(which)

        for t in range(HEAD_TILES + ROWS_AHEAD, N_TILES):
            put(at[t - ROWS_AHEAD, TILE_ORDER[0]], "rows", t)
            put(at[t - ROWS_AHEAD, TILE_ORDER[0]] + 1, "copy of rows", t)
        for pair in range(1, N_PAIRS):
            for gate in (TURNED[1:] if pair == 1 or THREE(pair) else TURNED):
                for bank in range(BANKS_PER_GATE):
                    beside = PAIR_TILES * pair - (1 if gate == GATE_G else 2) + bank
                    step = at[beside, ADDED[-1]] if beside >= HEAD_TILES else n_head
                    put(step, "turned bank", pair, gate, bank)
                    put(step + 1, "copy of turned bank", pair, gate, bank)
        for n in range(n_head, n_steps):
            if is_added(n):
                if is_turned(n - 1) and n + 1 < n_steps:
                    put(n + 1, "product behind pass 1", n)
                elif is_turned(n - 2):
                    put(n, "product behind pass 1", n)
                else:
                    put(n, "product behind pass 0", n)
        for t in range(HEAD_TILES, N_TILES):
            put(activated_at(t, GATE_F) + 1, "keep", t)
        for t in range(last_tile):
            cell_step = at[t, GATE_G] + (4 if t < last_tile - 1 else 4)
            put(cell_step, "cell", t)
            put(cell_step + (2 if t < last_tile - 1 else 2), "tanh", t)
            if t + 1 < last_tile:
                put(cell_step + (4 if t < last_tile - 2 else 3), "hidden", t)
        put(n_head, "load rows", 3)
        for s in range(1, N_GROUPS):
            first_step = at[TILES * s, TILE_ORDER[0]]
            if s + 3 < N_GROUPS:
                put(first_step, "load rows", s + 3)
            if s + 1 < N_GROUPS:
                put(first_step, "load cell", s + 1)

        everything = slice(0, HID)
        copied_rows = [5]
        for n in range(n_head, max(step for step, what in due) + 1):
            running = n < n_steps
            for (s,) in due.get((n, "load rows"), []):
                load_h(s)
                load_x(s)
            for (s,) in due.get((n, "load cell"), []):
                load_cell(s)

            split = running and steps[n][1] == GATE_F and n > n_head
            if split:
                rows_now = due.get((n, "rows"), [])
                k = 0
                for part in range(2):
                    for e in range(HALVES):
                        input_half(n, part, e)
                        for (t,) in rows_now:
                            if k < 2:
                                transpose_h(t, k)
                            elif k == 2:
                                transpose_x(t)
                        if is_turned(n - 1):
                            add_turned_block(n - 1, k)
                        k += 1
            if running and not split:
                input_pass(n, 0)
            for (t,) in due.get((n, "rows"), []) if not split else []:
                transpose_h(t, 0)
            if is_turned(n - 1) and not split:
                add_turned(n - 1, 0)
            for (m,) in due.get((n, "product behind pass 0"), []):
                recurrent_rows(m)
            if running and not split:
                input_pass(n, 1)
            for (t,) in due.get((n, "rows"), []) if not split else []:
                transpose_h(t, 1)
                transpose_x(t)
            if is_turned(n - 1) and not split:
                add_turned(n - 1, 1)
            for (m,) in due.get((n, "product behind pass 1"), []):
                recurrent_rows(m)
            for bank in due.get((n, "turned bank"), []):
                turned_bank(*bank)

            for (t,) in due.get((n, "cell"), []):
                write_candidate(t, nc.gpsimd, everything)
            if is_added(n):
                add_bias(n)
            if is_added(n - 1):
                add_recurrent(n - 1)
            for bank in due.get((n, "copy of turned bank"), []):
                copy_turned_bank(*bank)

            for (t,) in due.get((n, "tanh"), []):
                tanh_of_new_cell(t, everything)
            if n_head < n <= n_steps and steps[n - 1] != (last_tile, GATE_O):
                activate(*steps[n - 1])
            if n == n_steps:
                activate(last_tile, GATE_O)
            for (t,) in due.get((n, "copy of rows"), []):
                copy_h(t, nc.vector.tensor_copy if HV(t) else nc.scalar.copy)
                copy_x(t, nc.vector.tensor_copy if XV(t) else nc.scalar.copy)
                copied_rows.append(t)
            if n == n_head or (n, "cell") in due or (n, "hidden") in due:
                while copied_rows:
                    quantise_rows(copied_rows.pop(0))
            for (t,) in due.get((n, "hidden"), []):
                new_hidden(t, everything, nc.gpsimd if GH(t) else nc.vector)
            for (t,) in due.get((n, "cell"), []):
                new_cell(t, everything)
            for (t,) in due.get((n, "keep"), []):
                keep_old_cell(t, nc.gpsimd if t < last_tile else nc.vector)

        halves = [slice(i * HID // 2, (i + 1) * HID // 2) for i in range(2)]
        for cols in halves:
            write_candidate(last_tile, nc.vector, cols)
        for cols in halves:
            new_cell(last_tile, cols)
        for cols in halves:
            tanh_of_new_cell(last_tile, cols)
        new_hidden(last_tile - 1, everything, nc.vector)
        for cols in halves:
            new_hidden(last_tile, cols)
